import numpy as np
import ml_dtypes


def mxq(x, axis, fmt="e4m3"):
    dtype, down = {"e4m3": (ml_dtypes.float8_e4m3fn, 7), "e5m2": (ml_dtypes.float8_e5m2, 14)}[fmt]
    v = np.moveaxis(np.asarray(x, np.float32).astype(ml_dtypes.bfloat16).astype(np.float64), axis, -1)
    blocks = v.reshape(v.shape[:-1] + (-1, 32))
    amax = np.abs(blocks).max(-1, keepdims=True)
    byte = np.maximum(np.where(amax > 0, np.frexp(amax)[1] - 1 + 127, 0) - down, 1)
    scale = np.exp2(byte - 127.0)
    codes = (blocks / scale).astype(np.float32).astype(dtype).astype(np.float64)
    return np.moveaxis((codes * scale).reshape(v.shape), -1, axis)


WIDE = False


def mx_kscale(k):
    if not WIDE:
        return np.ones(k)
    levels = np.array([10, -10, 5, -5, 0])
    a = np.random.permutation(np.resize(levels, k // 512 * 4)).reshape(k // 512, 4)
    idx = np.arange(k)
    return np.exp2(a[idx // 512, idx % 128 // 32])


BF16 = ml_dtypes.bfloat16


def bf(x):
    return np.asarray(x, np.float32).astype(BF16)


def f64(x):
    return np.asarray(x).astype(np.float64)


N, D, B = 16384, 128, 1024


def setup_inputs():
    s = mx_kscale(B)
    centre = np.random.standard_normal((1, D))
    spread = 0.15 + 0.3 * np.random.random((N, 1))
    x = centre + spread * np.random.standard_normal((N, D))
    if float(s.max()) > float(s.min()):
        x[::B, :] = 0.0
        x[::B, 0] = 2.0 ** 20
    return {"features": bf(x)}


def reference(features):
    f = f64(features)
    n, d = f.shape
    nb = n // B
    x = f[: nb * B].reshape(nb, B, d)
    sq = np.sum(x * x, axis=-1)
    d2 = sq[:, :, None] + sq[:, None, :] - 2.0 * (x @ x.transpose(0, 2, 1))
    d2 = np.maximum(d2, 0.0)
    w = np.exp(-d2 / (2.0 * (d / 10.0)))
    out = (mxq(w, 2, "e4m3") @ mxq(x, 1, "e4m3")) / B
    out = out.reshape(nb * B, d)
    if nb * B < n:
        out = np.concatenate([out, np.zeros((n - nb * B, d))], axis=0)
    return out

@@ -1,0 +1,161 @@
+from contextlib import ExitStack
+
+import concourse.mybir as mybir
+from concourse.masks import make_identity
+
+F32 = mybir.dt.float32
+BF16 = mybir.dt.bfloat16
+U32 = mybir.dt.uint32
+U8 = mybir.dt.uint8
+FP8X4 = mybir.dt.float8_e4m3fn_x4
+ALU = mybir.AluOpType
+ACT = mybir.ActivationFunctionType
+AX = mybir.AxisListType
+
+P = 128
+NB = 16
+D = 128
+FLOPS = 2 * 2 * 16 * 1024 * 1024 * 128
+
+
+def tile_blockselfattention_kernel(tc, features, out):
+    nc = tc.nc
+    with ExitStack() as ctx:
+        const = ctx.enter_context(tc.tile_pool(name="const", bufs=1))
+        work = ctx.enter_context(tc.tile_pool(name="work", bufs=2))
+        xtp = ctx.enter_context(tc.tile_pool(name="xtp", bufs=3))
+        hbp = ctx.enter_context(tc.tile_pool(name="hbp", bufs=3))
+        up = ctx.enter_context(tc.tile_pool(name="up", bufs=3))
+        gp = ctx.enter_context(tc.tile_pool(name="gp", bufs=3))
+        wp = ctx.enter_context(tc.tile_pool(name="wp", bufs=2))
+        op = ctx.enter_context(tc.tile_pool(name="op", bufs=3))
+        ps_s = ctx.enter_context(tc.psum_pool(name="ps_s", bufs=4))
+        ps_t = ctx.enter_context(tc.psum_pool(name="ps_t", bufs=1))
+        ps_o = ctx.enter_context(tc.psum_pool(name="ps_o", bufs=2))
+
+        x_sb = const.tile([P, 2 * NB, 4, D], BF16, name="x_sb")
+        xv = features.rearrange("(q p t) d -> p q (t d)", p=P, t=4)
+        for q0, q1 in ((0, 2), (2, 4), (4, 8), (8, 16), (16, 32)):
+            nc.sync.dma_start(
+                out=x_sb[:, q0:q1].rearrange("p q t d -> p q (t d)"), in_=xv[:, q0:q1, :]
+            )
+
+        ident_b = const.tile([P, P], BF16, name="ident_b")
+        make_identity(nc, ident_b[:])
+        ident_f = const.tile([P, P], F32, name="ident_f")
+        make_identity(nc, ident_f[:])
+        h_col = const.tile([P, P], F32, name="h_col")
+        nc.vector.memset(h_col[:], 0.0)
+        xq = const.tile([P, NB, 256], U32, name="xq", align_bytes=64)
+        xs = const.tile([P, NB, 256], U8, name="xs", align_bytes=64)
+
+        x_t = {}
+        h_b = {}
+        w_q = {}
+        w_s = {}
+        g_of = {}
+
+        def prologue(b):
+            xb = x_sb[:, 2 * b : 2 * b + 2]
+            sqf = work.tile([P, 8, D], F32, name="sqf")
+            nc.scalar.activation(
+                out=sqf[:].rearrange("p a d -> p (a d)"),
+                in_=xb.rearrange("p g t d -> p (g t d)"),
+                func=ACT.Square,
+            )
+            sq8 = work.tile([P, 8], F32, name="sq8")
+            nc.vector.tensor_reduce(out=sq8[:], in_=sqf[:], axis=AX.X, op=ALU.add)
+            nc.vector.tensor_scalar_mul(out=h_col[:, 8 * b : 8 * b + 8], in0=sq8[:], scalar1=0.5)
+
+            xt_ps = ps_t.tile([P, 8, P], BF16, name="xt_ps")
+            for a in range(8):
+                nc.tensor.transpose(xt_ps[:, a, :], x_sb[:, 2 * b + a // 4, a % 4, :], ident_b[:])
+            xt = xtp.tile([P, 8 * P], BF16, name="xt")
+            nc.scalar.copy(out=xt[:], in_=xt_ps[:].rearrange("p a c -> p (a c)"))
+            x_t[b] = xt
+
+            ht_ps = ps_t.tile([P, P], F32, name="ht_ps")
+            nc.tensor.transpose(ht_ps[:], h_col[:], ident_f[:])
+            ht = work.tile([P, P], F32, name="ht")
+            nc.vector.tensor_copy(out=ht[:], in_=ht_ps[:])
+            scratch = out[1024 * b : 1024 * b + 8, :]
+            nc.sync.dma_start(out=scratch, in_=ht[8 * b : 8 * b + 8, :])
+            hb = hbp.tile([P, 1024], F32, name="hb")
+            nc.sync.dma_start(
+                out=hb[:], in_=scratch.rearrange("a p -> (a p)").partition_broadcast(P)
+            )
+            h_b[b] = hb
+
+            xg = work.tile([P, 2, D, 4], BF16, name="xg", align_bytes=64)
+            nc.vector.tensor_copy(out=xg[:], in_=xb.rearrange("p g t d -> p g d t"))
+            nc.vector.quantize_mx(
+                out=xq[:, b, :].bitcast(FP8X4),
+                scales=xs[:, b, :],
+                in_=xg[:].rearrange("p g d t -> p (g d t)"),
+            )
+            w_q[b] = wp.tile([P, 2, 1024], U32, name="wq", align_bytes=64)
+            w_s[b] = wp.tile([P, 2, 1024], U8, name="ws", align_bytes=64)
+
+        def front(b, hh, g):
+            xt = x_t[b]
+            cols = slice(512 * hh, 512 * hh + 512)
+            u = up.tile([P, 4, 512], F32, name="u")
+            for t in range(4):
+                a = 4 * g + t
+                s_ps = ps_s.tile([P, 512], F32, name="s_ps")
+                nc.tensor.matmul(
+                    s_ps[:], lhsT=xt[:, P * a : P * a + P], rhs=xt[:, cols], start=True, stop=True
+                )
+                nc.vector.scalar_tensor_tensor(
+                    out=u[:, t, :],
+                    in0=s_ps[:],
+                    scalar=h_col[:, 8 * b + a : 8 * b + a + 1],
+                    in1=h_b[b][:, cols],
+                    op0=ALU.subtract,
+                    op1=ALU.subtract,
+                )
+            grp = gp.tile([P, 512, 4], BF16, name="grp", align_bytes=64)
+            nc.scalar.activation(
+                out=grp[:], in_=u[:].rearrange("p t c -> p c t"), func=ACT.Exp, scale=0.078125
+            )
+            g_of[(b, hh, g)] = grp
+
+        def back(b, hh, g):
+            cols = slice(512 * hh, 512 * hh + 512)
+            flat = g_of.pop((b, hh, g))[:].rearrange("p c t -> p (c t)")
+            nc.vector.tensor_scalar_min(out=flat, in0=flat, scalar1=1.0)
+            nc.vector.quantize_mx(
+                out=w_q[b][:, g, cols].bitcast(FP8X4), scales=w_s[b][:, g, cols], in_=flat
+            )
+            if g == 0:
+                return
+            acc = ps_o.tile([P, 4, D], F32, name="acc")
+            for mm in range(4):
+                mc = slice(512 * hh + P * mm, 512 * hh + P * mm + P)
+                for gg in range(2):
+                    nc.tensor.matmul_mx(
+                        out=acc[:, mm, :],
+                        lhsT=w_q[b][:, gg, mc].bitcast(FP8X4),
+                        lhsT_scale=w_s[b][:, gg, mc],
+                        rhs=xq[:, b, P * gg : P * gg + P].bitcast(FP8X4),
+                        rhs_scale=xs[:, b, P * gg : P * gg + P],
+                        start=(gg == 0),
+                        stop=(gg == 1),
+                    )
+            osb = op.tile([P, 4, D], F32, name="osb")
+            nc.scalar.activation(out=osb[:], in_=acc[:], func=ACT.Copy, scale=1.0 / 1024.0)
+            rows = out[1024 * b + 512 * hh : 1024 * b + 512 * hh + 512, :]
+            nc.sync.dma_start(
+                out=rows.rearrange("(p t) d -> p (t d)", t=4),
+                in_=osb[:].rearrange("p t d -> p (t d)"),
+            )
+
+        units = [(b, hh, g) for b in range(NB) for hh in range(2) for g in range(2)]
+        prologue(0)
+        for k, unit in enumerate(units):
+            front(*unit)
+            if unit[1] == 0 and unit[2] == 0 and unit[0] + 1 < NB:
+                prologue(unit[0] + 1)
+            if k >= 1:
+                back(*units[k - 1])
+        back(*units[-1])

@@ -26,12 +26,13 @@ def tile_blockselfattention_kernel(tc, features, out):
         xtp = ctx.enter_context(tc.tile_pool(name="xtp", bufs=3))
         hbp = ctx.enter_context(tc.tile_pool(name="hbp", bufs=3))
         up = ctx.enter_context(tc.tile_pool(name="up", bufs=3))
-        gp = ctx.enter_context(tc.tile_pool(name="gp", bufs=3))
+        gp = ctx.enter_context(tc.tile_pool(name="gp", bufs=4))
         wp = ctx.enter_context(tc.tile_pool(name="wp", bufs=2))
         op = ctx.enter_context(tc.tile_pool(name="op", bufs=3))
         ps_s = ctx.enter_context(tc.psum_pool(name="ps_s", bufs=4))
-        ps_t = ctx.enter_context(tc.psum_pool(name="ps_t", bufs=1))
-        ps_o = ctx.enter_context(tc.psum_pool(name="ps_o", bufs=2))
+        ps_m = ctx.enter_context(tc.psum_pool(name="ps_m", bufs=1))
+        ps_t = ctx.enter_context(tc.psum_pool(name="ps_t", bufs=2))
+        ps_o = ctx.enter_context(tc.psum_pool(name="ps_o", bufs=1))
 
         x_sb = const.tile([P, 2 * NB, 4, D], BF16, name="x_sb")
         xv = features.rearrange("(q p t) d -> p q (t d)", p=P, t=4)
@@ -57,24 +58,25 @@ def tile_blockselfattention_kernel(tc, features, out):
 
         def prologue(b):
             xb = x_sb[:, 2 * b : 2 * b + 2]
+            xa = xb.rearrange("p g t d -> p (g t) d")
             sqf = work.tile([P, 8, D], F32, name="sqf")
-            nc.scalar.activation(
-                out=sqf[:].rearrange("p a d -> p (a d)"),
-                in_=xb.rearrange("p g t d -> p (g t d)"),
-                func=ACT.Square,
-            )
+            nc.gpsimd.tensor_tensor(out=sqf[:], in0=xa, in1=xa, op=ALU.mult)
+            for w in (64, 32, 16):
+                nc.gpsimd.tensor_tensor(
+                    out=sqf[:, :, 0:w], in0=sqf[:, :, 0:w], in1=sqf[:, :, w : 2 * w], op=ALU.add
+                )
             sq8 = work.tile([P, 8], F32, name="sq8")
-            nc.vector.tensor_reduce(out=sq8[:], in_=sqf[:], axis=AX.X, op=ALU.add)
+            nc.vector.tensor_reduce(out=sq8[:], in_=sqf[:, :, 0:16], axis=AX.X, op=ALU.add)
             nc.vector.tensor_scalar_mul(out=h_col[:, 8 * b : 8 * b + 8], in0=sq8[:], scalar1=0.5)
 
-            xt_ps = ps_t.tile([P, 8, P], BF16, name="xt_ps")
+            xt_ps = ps_m.tile([P, 8, P], BF16, name="xt_ps", tag="misc")
             for a in range(8):
                 nc.tensor.transpose(xt_ps[:, a, :], x_sb[:, 2 * b + a // 4, a % 4, :], ident_b[:])
             xt = xtp.tile([P, 8 * P], BF16, name="xt")
             nc.scalar.copy(out=xt[:], in_=xt_ps[:].rearrange("p a c -> p (a c)"))
             x_t[b] = xt
 
-            ht_ps = ps_t.tile([P, P], F32, name="ht_ps")
+            ht_ps = ps_m.tile([P, P], F32, name="ht_ps", tag="misc")
             nc.tensor.transpose(ht_ps[:], h_col[:], ident_f[:])
             ht = work.tile([P, P], F32, name="ht")
             nc.vector.tensor_copy(out=ht[:], in_=ht_ps[:])
@@ -87,7 +89,14 @@ def tile_blockselfattention_kernel(tc, features, out):
             h_b[b] = hb
 
             xg = work.tile([P, 2, D, 4], BF16, name="xg", align_bytes=64)
-            nc.vector.tensor_copy(out=xg[:], in_=xb.rearrange("p g t d -> p g d t"))
+            nc.gpsimd.tensor_scalar(
+                out=xg[:],
+                in0=xb.rearrange("p g t d -> p g d t"),
+                scalar1=1.0,
+                scalar2=0.0,
+                op0=ALU.mult,
+                op1=ALU.add,
+            )
             nc.vector.quantize_mx(
                 out=xq[:, b, :].bitcast(FP8X4),
                 scales=xs[:, b, :],
@@ -120,15 +129,15 @@ def tile_blockselfattention_kernel(tc, features, out):
             )
             g_of[(b, hh, g)] = grp
 
-        def back(b, hh, g):
+        def quantise(b, hh, g, grp):
             cols = slice(512 * hh, 512 * hh + 512)
-            flat = g_of.pop((b, hh, g))[:].rearrange("p c t -> p (c t)")
-            nc.vector.tensor_scalar_min(out=flat, in0=flat, scalar1=1.0)
             nc.vector.quantize_mx(
-                out=w_q[b][:, g, cols].bitcast(FP8X4), scales=w_s[b][:, g, cols], in_=flat
+                out=w_q[b][:, g, cols].bitcast(FP8X4),
+                scales=w_s[b][:, g, cols],
+                in_=grp[:].rearrange("p c t -> p (c t)"),
             )
-            if g == 0:
-                return
+
+        def second_matmul(b, hh):
             acc = ps_o.tile([P, 4, D], F32, name="acc")
             for mm in range(4):
                 mc = slice(512 * hh + P * mm, 512 * hh + P * mm + P)
@@ -150,11 +159,38 @@ def tile_blockselfattention_kernel(tc, features, out):
                 in_=osb[:].rearrange("p t d -> p (t d)"),
             )
 
-        units = [(b, hh, g) for b in range(NB) for hh in range(2) for g in range(2)]
+        def back(b, hh, g):
+            grp = g_of.pop((b, hh, g))
+            flat = grp[:].rearrange("p c t -> p (c t)")
+            nc.vector.tensor_scalar_min(out=flat, in0=flat, scalar1=1.0)
+            quantise(b, hh, g, grp)
+            if (hh, g) == (1, 0):
+                mir = gp.tile([P, 512, 4], BF16, name="mir", tag="grp", align_bytes=64)
+                for half in range(2):
+                    tp = ps_t.tile([P, 2, 4, P], BF16, name="tp")
+                    for a in range(2):
+                        for t in range(4):
+                            nc.tensor.transpose(
+                                tp[:, a, t, :], grp[:, P * t : P * t + P, 2 * half + a], ident_b[:]
+                            )
+                    nc.scalar.copy(
+                        out=mir[:, 256 * half : 256 * half + 256, :].rearrange(
+                            "p (a c) t -> p a c t", a=2
+                        ),
+                        in_=tp[:].rearrange("p a t c -> p a c t"),
+                    )
+                g_of[(b, 0, 1)] = mir
+            elif (hh, g) == (0, 0):
+                quantise(b, 0, 1, g_of.pop((b, 0, 1)))
+                second_matmul(b, 0)
+            else:
+                second_matmul(b, 1)
+
+        units = [(b, hh, g) for b in range(NB) for hh, g in ((1, 0), (0, 0), (1, 1))]
         prologue(0)
         for k, unit in enumerate(units):
             front(*unit)
-            if unit[1] == 0 and unit[2] == 0 and unit[0] + 1 < NB:
+            if (unit[1], unit[2]) == (1, 0) and unit[0] + 1 < NB:
                 prologue(unit[0] + 1)
             if k >= 1:
                 back(*units[k - 1])

@@ -15,19 +15,23 @@ AX = mybir.AxisListType
 P = 128
 NB = 16
 D = 128
+NU = 3 * NB
+QUADS = ((1, 0), (0, 0), (1, 1))
 FLOPS = 2 * 2 * 16 * 1024 * 1024 * 128
 
 
 def tile_blockselfattention_kernel(tc, features, out):
     nc = tc.nc
     with ExitStack() as ctx:
+        ctx.enter_context(tc.manual_schedule())
         const = ctx.enter_context(tc.tile_pool(name="const", bufs=1))
         work = ctx.enter_context(tc.tile_pool(name="work", bufs=2))
+        xgp = ctx.enter_context(tc.tile_pool(name="xgp", bufs=3))
         xtp = ctx.enter_context(tc.tile_pool(name="xtp", bufs=3))
-        hbp = ctx.enter_context(tc.tile_pool(name="hbp", bufs=3))
+        hbp = ctx.enter_context(tc.tile_pool(name="hbp", bufs=4))
         up = ctx.enter_context(tc.tile_pool(name="up", bufs=3))
-        gp = ctx.enter_context(tc.tile_pool(name="gp", bufs=4))
-        wp = ctx.enter_context(tc.tile_pool(name="wp", bufs=2))
+        gp = ctx.enter_context(tc.tile_pool(name="gp", bufs=7))
+        wp = ctx.enter_context(tc.tile_pool(name="wp", bufs=3))
         op = ctx.enter_context(tc.tile_pool(name="op", bufs=3))
         ps_s = ctx.enter_context(tc.psum_pool(name="ps_s", bufs=4))
         ps_m = ctx.enter_context(tc.psum_pool(name="ps_m", bufs=1))
@@ -36,10 +40,17 @@ def tile_blockselfattention_kernel(tc, features, out):
 
         x_sb = const.tile([P, 2 * NB, 4, D], BF16, name="x_sb")
         xv = features.rearrange("(q p t) d -> p q (t d)", p=P, t=4)
-        for q0, q1 in ((0, 2), (2, 4), (4, 8), (8, 16), (16, 32)):
-            nc.sync.dma_start(
+
+        def load(queue, q0, q1):
+            queue.dma_start(
                 out=x_sb[:, q0:q1].rearrange("p q t d -> p q (t d)"), in_=xv[:, q0:q1, :]
             )
+
+        load(nc.sync, 0, 2)
+        load(nc.sync, 2, 4)
+        load(nc.scalar, 4, 8)
+        load(nc.scalar, 8, 16)
+        load(nc.scalar, 16, 32)
 
         ident_b = const.tile([P, P], BF16, name="ident_b")
         make_identity(nc, ident_b[:])
@@ -54,32 +65,64 @@ def tile_blockselfattention_kernel(tc, features, out):
         h_b = {}
         w_q = {}
         w_s = {}
-        g_of = {}
+        grp_of = {}
+        mir_of = {}
+        sq_of = {}
+        xg_of = {}
+        misc = {}
+        s_of = {}
+        u_of = {}
+        tp_of = {}
+        acc_of = {}
 
-        def prologue(b):
-            xb = x_sb[:, 2 * b : 2 * b + 2]
-            xa = xb.rearrange("p g t d -> p (g t) d")
+        def xblock(b):
+            return x_sb[:, 2 * b : 2 * b + 2]
+
+        def squares_scalar(b):
+            sqf = work.tile([P, 8, D], F32, name="sqf")
+            nc.scalar.activation(
+                out=sqf[:].rearrange("p a d -> p (a d)"),
+                in_=xblock(b).rearrange("p g t d -> p (g t d)"),
+                func=ACT.Square,
+            )
+            sq_of[b] = (sqf, D)
+
+        def squares_gpsimd(b):
+            xa = xblock(b).rearrange("p g t d -> p (g t) d")
             sqf = work.tile([P, 8, D], F32, name="sqf")
             nc.gpsimd.tensor_tensor(out=sqf[:], in0=xa, in1=xa, op=ALU.mult)
             for w in (64, 32, 16):
                 nc.gpsimd.tensor_tensor(
                     out=sqf[:, :, 0:w], in0=sqf[:, :, 0:w], in1=sqf[:, :, w : 2 * w], op=ALU.add
                 )
+            sq_of[b] = (sqf, 16)
+
+        def regroup_x(b):
+            xg = xgp.tile([P, 2, D, 4], BF16, name="xg", align_bytes=64)
+            nc.gpsimd.tensor_scalar(
+                out=xg[:],
+                in0=xblock(b).rearrange("p g t d -> p g d t"),
+                scalar1=1.0,
+                scalar2=0.0,
+                op0=ALU.mult,
+                op1=ALU.add,
+            )
+            xg_of[b] = xg
+
+        def half_norms(b):
+            sqf, width = sq_of.pop(b)
             sq8 = work.tile([P, 8], F32, name="sq8")
-            nc.vector.tensor_reduce(out=sq8[:], in_=sqf[:, :, 0:16], axis=AX.X, op=ALU.add)
+            nc.vector.tensor_reduce(out=sq8[:], in_=sqf[:, :, 0:width], axis=AX.X, op=ALU.add)
             nc.vector.tensor_scalar_mul(out=h_col[:, 8 * b : 8 * b + 8], in0=sq8[:], scalar1=0.5)
 
-            xt_ps = ps_m.tile([P, 8, P], BF16, name="xt_ps", tag="misc")
-            for a in range(8):
-                nc.tensor.transpose(xt_ps[:, a, :], x_sb[:, 2 * b + a // 4, a % 4, :], ident_b[:])
-            xt = xtp.tile([P, 8 * P], BF16, name="xt")
-            nc.scalar.copy(out=xt[:], in_=xt_ps[:].rearrange("p a c -> p (a c)"))
-            x_t[b] = xt
-
+        def norms_transpose(b):
             ht_ps = ps_m.tile([P, P], F32, name="ht_ps", tag="misc")
             nc.tensor.transpose(ht_ps[:], h_col[:], ident_f[:])
+            misc[b] = ht_ps
+
+        def norms_broadcast(b):
             ht = work.tile([P, P], F32, name="ht")
-            nc.vector.tensor_copy(out=ht[:], in_=ht_ps[:])
+            nc.vector.tensor_copy(out=ht[:], in_=misc.pop(b)[:])
             scratch = out[1024 * b : 1024 * b + 8, :]
             nc.sync.dma_start(out=scratch, in_=ht[8 * b : 8 * b + 8, :])
             hb = hbp.tile([P, 1024], F32, name="hb")
@@ -88,54 +131,105 @@ def tile_blockselfattention_kernel(tc, features, out):
             )
             h_b[b] = hb
 
-            xg = work.tile([P, 2, D, 4], BF16, name="xg", align_bytes=64)
-            nc.gpsimd.tensor_scalar(
-                out=xg[:],
-                in0=xb.rearrange("p g t d -> p g d t"),
-                scalar1=1.0,
-                scalar2=0.0,
-                op0=ALU.mult,
-                op1=ALU.add,
-            )
+        def x_transpose(b):
+            xt_ps = ps_m.tile([P, 8, P], BF16, name="xt_ps", tag="misc")
+            for a in range(8):
+                nc.tensor.transpose(xt_ps[:, a, :], x_sb[:, 2 * b + a // 4, a % 4, :], ident_b[:])
+            misc[b] = xt_ps
+
+        def x_transpose_out(b):
+            xt = xtp.tile([P, 8 * P], BF16, name="xt")
+            nc.scalar.copy(out=xt[:], in_=misc.pop(b)[:].rearrange("p a c -> p (a c)"))
+            x_t[b] = xt
+
+        def quantise_x(b):
             nc.vector.quantize_mx(
                 out=xq[:, b, :].bitcast(FP8X4),
                 scales=xs[:, b, :],
-                in_=xg[:].rearrange("p g d t -> p (g d t)"),
+                in_=xg_of.pop(b)[:].rearrange("p g d t -> p (g d t)"),
             )
-            w_q[b] = wp.tile([P, 2, 1024], U32, name="wq", align_bytes=64)
-            w_s[b] = wp.tile([P, 2, 1024], U8, name="ws", align_bytes=64)
 
-        def front(b, hh, g):
+        def where(k):
+            return (k // 3,) + QUADS[k % 3]
+
+        def products(k):
+            b, hh, g = where(k)
             xt = x_t[b]
-            cols = slice(512 * hh, 512 * hh + 512)
-            u = up.tile([P, 4, 512], F32, name="u")
+            banks = []
             for t in range(4):
                 a = 4 * g + t
                 s_ps = ps_s.tile([P, 512], F32, name="s_ps")
                 nc.tensor.matmul(
-                    s_ps[:], lhsT=xt[:, P * a : P * a + P], rhs=xt[:, cols], start=True, stop=True
+                    s_ps[:],
+                    lhsT=xt[:, P * a : P * a + P],
+                    rhs=xt[:, 512 * hh : 512 * hh + 512],
+                    start=True,
+                    stop=True,
                 )
-                nc.vector.scalar_tensor_tensor(
-                    out=u[:, t, :],
-                    in0=s_ps[:],
-                    scalar=h_col[:, 8 * b + a : 8 * b + a + 1],
-                    in1=h_b[b][:, cols],
-                    op0=ALU.subtract,
-                    op1=ALU.subtract,
-                )
+                banks.append(s_ps)
+            s_of[k] = banks
+
+        def distances(k, t):
+            b, hh, g = where(k)
+            if t == 0:
+                u_of[k] = up.tile([P, 4, 512], F32, name="u")
+            a = 4 * g + t
+            nc.vector.scalar_tensor_tensor(
+                out=u_of[k][:, t, :],
+                in0=s_of[k][t][:],
+                scalar=h_col[:, 8 * b + a : 8 * b + a + 1],
+                in1=h_b[b][:, 512 * hh : 512 * hh + 512],
+                op0=ALU.subtract,
+                op1=ALU.subtract,
+            )
+
+        def exponentials(k):
             grp = gp.tile([P, 512, 4], BF16, name="grp", align_bytes=64)
             nc.scalar.activation(
-                out=grp[:], in_=u[:].rearrange("p t c -> p c t"), func=ACT.Exp, scale=0.078125
+                out=grp[:],
+                in_=u_of.pop(k)[:].rearrange("p t c -> p c t"),
+                func=ACT.Exp,
+                scale=0.078125,
             )
-            g_of[(b, hh, g)] = grp
+            s_of.pop(k)
+            grp_of[k] = grp
+
+        def clamp(k):
+            flat = grp_of[k][:].rearrange("p c t -> p (c t)")
+            nc.vector.tensor_scalar_min(out=flat, in0=flat, scalar1=1.0)
 
         def quantise(b, hh, g, grp):
+            if b not in w_q:
+                w_q[b] = wp.tile([P, 2, 1024], U32, name="wq", align_bytes=64)
+                w_s[b] = wp.tile([P, 2, 1024], U8, name="ws", align_bytes=64)
             cols = slice(512 * hh, 512 * hh + 512)
             nc.vector.quantize_mx(
                 out=w_q[b][:, g, cols].bitcast(FP8X4),
                 scales=w_s[b][:, g, cols],
                 in_=grp[:].rearrange("p c t -> p (c t)"),
             )
+
+        def mirror_transposes(b, half):
+            grp = grp_of[3 * b]
+            tp = ps_t.tile([P, 2, 4, P], BF16, name="tp")
+            for a in range(2):
+                for t in range(4):
+                    nc.tensor.transpose(
+                        tp[:, a, t, :], grp[:, P * t : P * t + P, 2 * half + a], ident_b[:]
+                    )
+            tp_of[(b, half)] = tp
+
+        def mirror_out(b, half, engine):
+            if half == 0:
+                mir_of[b] = gp.tile([P, 512, 4], BF16, name="mir", tag="grp", align_bytes=64)
+            dst = mir_of[b][:, 256 * half : 256 * half + 256, :].rearrange(
+                "p (a c) t -> p a c t", a=2
+            )
+            src = tp_of.pop((b, half))[:].rearrange("p a t c -> p a c t")
+            if engine == "scalar":
+                nc.scalar.copy(out=dst, in_=src)
+            else:
+                nc.vector.tensor_copy(out=dst, in_=src)
 
         def second_matmul(b, hh):
             acc = ps_o.tile([P, 4, D], F32, name="acc")
@@ -151,47 +245,107 @@ def tile_blockselfattention_kernel(tc, features, out):
                         start=(gg == 0),
                         stop=(gg == 1),
                     )
+            acc_of[(b, hh)] = acc
+
+        def store(b, hh):
             osb = op.tile([P, 4, D], F32, name="osb")
-            nc.scalar.activation(out=osb[:], in_=acc[:], func=ACT.Copy, scale=1.0 / 1024.0)
+            nc.scalar.activation(
+                out=osb[:], in_=acc_of.pop((b, hh))[:], func=ACT.Copy, scale=1.0 / 1024.0
+            )
             rows = out[1024 * b + 512 * hh : 1024 * b + 512 * hh + 512, :]
             nc.sync.dma_start(
                 out=rows.rearrange("(p t) d -> p (t d)", t=4),
                 in_=osb[:].rearrange("p t d -> p (t d)"),
             )
 
-        def back(b, hh, g):
-            grp = g_of.pop((b, hh, g))
-            flat = grp[:].rearrange("p c t -> p (c t)")
-            nc.vector.tensor_scalar_min(out=flat, in0=flat, scalar1=1.0)
-            quantise(b, hh, g, grp)
-            if (hh, g) == (1, 0):
-                mir = gp.tile([P, 512, 4], BF16, name="mir", tag="grp", align_bytes=64)
-                for half in range(2):
-                    tp = ps_t.tile([P, 2, 4, P], BF16, name="tp")
-                    for a in range(2):
-                        for t in range(4):
-                            nc.tensor.transpose(
-                                tp[:, a, t, :], grp[:, P * t : P * t + P, 2 * half + a], ident_b[:]
-                            )
-                    nc.scalar.copy(
-                        out=mir[:, 256 * half : 256 * half + 256, :].rearrange(
-                            "p (a c) t -> p a c t", a=2
-                        ),
-                        in_=tp[:].rearrange("p a t c -> p a c t"),
-                    )
-                g_of[(b, 0, 1)] = mir
-            elif (hh, g) == (0, 0):
-                quantise(b, 0, 1, g_of.pop((b, 0, 1)))
-                second_matmul(b, 0)
-            else:
-                second_matmul(b, 1)
+        def block_at(k, lag):
+            if (k - lag) % 3 == 0 and 0 <= (k - lag) // 3 < NB:
+                return (k - lag) // 3
+            return None
 
-        units = [(b, hh, g) for b in range(NB) for hh, g in ((1, 0), (0, 0), (1, 1))]
-        prologue(0)
-        for k, unit in enumerate(units):
-            front(*unit)
-            if (unit[1], unit[2]) == (1, 0) and unit[0] + 1 < NB:
-                prologue(unit[0] + 1)
-            if k >= 1:
-                back(*units[k - 1])
-        back(*units[-1])
+        regroup_x(0)
+        regroup_x(1)
+        for b in range(2):
+            squares_scalar(b)
+            x_transpose(b)
+            x_transpose_out(b)
+            half_norms(b)
+            norms_transpose(b)
+            norms_broadcast(b)
+        quantise_x(0)
+        quantise_x(1)
+        squares_gpsimd(2)
+        regroup_x(2)
+        products(0)
+
+        for k in range(NU + 7):
+            live = k < NU
+            b = block_at(k, -6)
+            if b is not None and b >= 2:
+                half_norms(b)
+            b = block_at(k, -5)
+            if b is not None and b >= 2:
+                norms_broadcast(b)
+            b = block_at(k, -4)
+            if b is not None and b >= 2:
+                quantise_x(b)
+            b = block_at(k, 4)
+            if b is not None and b % 2 == 1:
+                mirror_out(b, 1, "vector")
+            if live:
+                distances(k, 0)
+                distances(k, 1)
+            if 0 <= k - 2 < NU:
+                clamp(k - 2)
+            if live:
+                distances(k, 2)
+                distances(k, 3)
+            if k + 1 < NU:
+                products(k + 1)
+            b = block_at(k, 2)
+            if b is not None:
+                mirror_transposes(b, 0)
+            b = block_at(k, 3)
+            if b is not None:
+                mirror_transposes(b, 1)
+                grp_of.pop(3 * b)
+            b = block_at(k, -6)
+            if b is not None and b >= 2:
+                norms_transpose(b)
+            b = block_at(k, -5)
+            if b is not None and b >= 2:
+                x_transpose(b)
+            b = block_at(k, 3)
+            if b is not None:
+                mirror_out(b, 0, "scalar")
+            b = block_at(k, 4)
+            if b is not None and b % 2 == 0:
+                mirror_out(b, 1, "scalar")
+            b = block_at(k, 5)
+            if b is not None:
+                store(b, 1)
+            b = block_at(k, 6)
+            if b is not None:
+                store(b, 0)
+            b = block_at(k, -4)
+            if b is not None and b >= 2:
+                x_transpose_out(b)
+            if live:
+                exponentials(k)
+            if 0 <= k - 2 < NU:
+                bb, hh, g = where(k - 2)
+                grp = grp_of[k - 2] if (k - 2) % 3 == 0 else grp_of.pop(k - 2)
+                quantise(bb, hh, g, grp)
+            b = block_at(k, 4)
+            if b is not None:
+                second_matmul(b, 1)
+            b = block_at(k, 5)
+            if b is not None:
+                quantise(b, 0, 1, mir_of.pop(b))
+                second_matmul(b, 0)
+                w_q.pop(b)
+                w_s.pop(b)
+            b = block_at(k, -8)
+            if b is not None and b >= 3:
+                squares_gpsimd(b)
+                regroup_x(b)

@@ -31,6 +31,7 @@ def tile_blockselfattention_kernel(tc, features, out):
         hbp = ctx.enter_context(tc.tile_pool(name="hbp", bufs=4))
         up = ctx.enter_context(tc.tile_pool(name="up", bufs=3))
         gp = ctx.enter_context(tc.tile_pool(name="gp", bufs=7))
+        pp = ctx.enter_context(tc.tile_pool(name="pp", bufs=4))
         wp = ctx.enter_context(tc.tile_pool(name="wp", bufs=3))
         op = ctx.enter_context(tc.tile_pool(name="op", bufs=3))
         ps_s = ctx.enter_context(tc.psum_pool(name="ps_s", bufs=4))
@@ -66,6 +67,7 @@ def tile_blockselfattention_kernel(tc, features, out):
         w_q = {}
         w_s = {}
         grp_of = {}
+        pl_of = {}
         mir_of = {}
         sq_of = {}
         xg_of = {}
@@ -131,6 +133,23 @@ def tile_blockselfattention_kernel(tc, features, out):
             )
             h_b[b] = hb
 
+        def norms_broadcast_on_chip(b):
+            hb = hbp.tile([P, 1024], F32, name="hb")
+            for half in range(2):
+                bank = ps_s.tile([P, 512], F32, name="s_ps")
+                for a in range(4):
+                    col = 8 * b + 4 * half + a
+                    nc.tensor.transpose(
+                        bank[:, P * a : P * a + P],
+                        h_col[:, col : col + 1].to_broadcast([P, P]),
+                        ident_f[:],
+                    )
+                if half == 0:
+                    nc.vector.tensor_copy(out=hb[:, 0:512], in_=bank[:])
+                else:
+                    nc.scalar.copy(out=hb[:, 512:1024], in_=bank[:])
+            h_b[b] = hb
+
         def x_transpose(b):
             xt_ps = ps_m.tile([P, 8, P], BF16, name="xt_ps", tag="misc")
             for a in range(8):
@@ -184,6 +203,12 @@ def tile_blockselfattention_kernel(tc, features, out):
             )
 
         def exponentials(k):
+            s_of.pop(k)
+            if k % 2 == 0:
+                pl = pp.tile([P, 4, 512], BF16, name="pl")
+                nc.scalar.activation(out=pl[:], in_=u_of.pop(k)[:], func=ACT.Exp, scale=0.078125)
+                pl_of[k] = pl
+                return
             grp = gp.tile([P, 512, 4], BF16, name="grp", align_bytes=64)
             nc.scalar.activation(
                 out=grp[:],
@@ -191,10 +216,18 @@ def tile_blockselfattention_kernel(tc, features, out):
                 func=ACT.Exp,
                 scale=0.078125,
             )
-            s_of.pop(k)
             grp_of[k] = grp
 
         def clamp(k):
+            if k % 2 == 0:
+                grp = gp.tile([P, 512, 4], BF16, name="grp", align_bytes=64)
+                nc.vector.tensor_scalar_min(
+                    out=grp[:].rearrange("p (c i) t -> p c t i", i=4),
+                    in0=pl_of.pop(k)[:].rearrange("p t (c i) -> p c t i", i=4),
+                    scalar1=1.0,
+                )
+                grp_of[k] = grp
+                return
             flat = grp_of[k][:].rearrange("p c t -> p (c t)")
             nc.vector.tensor_scalar_min(out=flat, in0=flat, scalar1=1.0)
 
@@ -265,18 +298,22 @@ def tile_blockselfattention_kernel(tc, features, out):
 
         regroup_x(0)
         regroup_x(1)
-        for b in range(2):
-            squares_scalar(b)
-            x_transpose(b)
-            x_transpose_out(b)
-            half_norms(b)
-            norms_transpose(b)
-            norms_broadcast(b)
+        squares_scalar(0)
+        x_transpose(0)
+        half_norms(0)
+        x_transpose_out(0)
+        norms_broadcast_on_chip(0)
+        products(0)
+        squares_scalar(1)
+        x_transpose(1)
+        x_transpose_out(1)
+        half_norms(1)
+        norms_transpose(1)
+        norms_broadcast(1)
         quantise_x(0)
         quantise_x(1)
         squares_gpsimd(2)
         regroup_x(2)
-        products(0)
 
         for k in range(NU + 7):
             live = k < NU
@@ -289,9 +326,6 @@ def tile_blockselfattention_kernel(tc, features, out):
             b = block_at(k, -4)
             if b is not None and b >= 2:
                 quantise_x(b)
-            b = block_at(k, 4)
-            if b is not None and b % 2 == 1:
-                mirror_out(b, 1, "vector")
             if live:
                 distances(k, 0)
                 distances(k, 1)
@@ -319,7 +353,7 @@ def tile_blockselfattention_kernel(tc, features, out):
             if b is not None:
                 mirror_out(b, 0, "scalar")
             b = block_at(k, 4)
-            if b is not None and b % 2 == 0:
+            if b is not None:
                 mirror_out(b, 1, "scalar")
             b = block_at(k, 5)
             if b is not None:

@@ -15,8 +15,7 @@ AX = mybir.AxisListType
 P = 128
 NB = 16
 D = 128
-NU = 3 * NB
-QUADS = ((1, 0), (0, 0), (1, 1))
+NS = 2 * NB
 FLOPS = 2 * 2 * 16 * 1024 * 1024 * 128
 
 
@@ -29,14 +28,15 @@ def tile_blockselfattention_kernel(tc, features, out):
         xgp = ctx.enter_context(tc.tile_pool(name="xgp", bufs=3))
         xtp = ctx.enter_context(tc.tile_pool(name="xtp", bufs=3))
         hbp = ctx.enter_context(tc.tile_pool(name="hbp", bufs=4))
+        rlp = ctx.enter_context(tc.tile_pool(name="rlp", bufs=3))
         up = ctx.enter_context(tc.tile_pool(name="up", bufs=3))
         gp = ctx.enter_context(tc.tile_pool(name="gp", bufs=7))
         pp = ctx.enter_context(tc.tile_pool(name="pp", bufs=4))
         wp = ctx.enter_context(tc.tile_pool(name="wp", bufs=3))
         op = ctx.enter_context(tc.tile_pool(name="op", bufs=3))
-        ps_s = ctx.enter_context(tc.psum_pool(name="ps_s", bufs=4))
-        ps_m = ctx.enter_context(tc.psum_pool(name="ps_m", bufs=1))
-        ps_t = ctx.enter_context(tc.psum_pool(name="ps_t", bufs=2))
+        ps_v = ctx.enter_context(tc.psum_pool(name="ps_v", bufs=3))
+        ps_a = ctx.enter_context(tc.psum_pool(name="ps_a", bufs=2))
+        ps_m = ctx.enter_context(tc.psum_pool(name="ps_m", bufs=2))
         ps_o = ctx.enter_context(tc.psum_pool(name="ps_o", bufs=1))
 
         x_sb = const.tile([P, 2 * NB, 4, D], BF16, name="x_sb")
@@ -61,9 +61,21 @@ def tile_blockselfattention_kernel(tc, features, out):
         nc.vector.memset(h_col[:], 0.0)
         xq = const.tile([P, NB, 256], U32, name="xq", align_bytes=64)
         xs = const.tile([P, NB, 256], U8, name="xs", align_bytes=64)
+        pc_r = []
+        pc_l = []
+        for i in range(2):
+            pcr = const.tile([P, 8, P], BF16, name="pcr%d" % i)
+            pcl = const.tile([P, 8, P], BF16, name="pcl%d" % i)
+            nc.vector.memset(pcr[:], 0.0)
+            nc.vector.memset(pcl[:], 0.0)
+            nc.vector.memset(pcr[:, :, 32:35], 1.0)
+            nc.vector.memset(pcl[:, :, 0:3], 1.0)
+            pc_r.append(pcr)
+            pc_l.append(pcl)
 
         x_t = {}
         h_b = {}
+        r_l = {}
         w_q = {}
         w_s = {}
         grp_of = {}
@@ -101,30 +113,38 @@ def tile_blockselfattention_kernel(tc, features, out):
 
         def regroup_x(b):
             xg = xgp.tile([P, 2, D, 4], BF16, name="xg", align_bytes=64)
-            nc.gpsimd.tensor_scalar(
-                out=xg[:],
-                in0=xblock(b).rearrange("p g t d -> p g d t"),
-                scalar1=1.0,
-                scalar2=0.0,
-                op0=ALU.mult,
-                op1=ALU.add,
-            )
+            nc.vector.tensor_copy(out=xg[:], in_=xblock(b).rearrange("p g t d -> p g d t"))
             xg_of[b] = xg
 
-        def half_norms(b):
+        def norms(b):
             sqf, width = sq_of.pop(b)
             sq8 = work.tile([P, 8], F32, name="sq8")
             nc.vector.tensor_reduce(out=sq8[:], in_=sqf[:, :, 0:width], axis=AX.X, op=ALU.add)
-            nc.vector.tensor_scalar_mul(out=h_col[:, 8 * b : 8 * b + 8], in0=sq8[:], scalar1=0.5)
+            hn = h_col[:, 8 * b : 8 * b + 8]
+            nc.vector.tensor_scalar_mul(out=hn, in0=sq8[:], scalar1=-0.5)
+
+        def norm_pieces(b):
+            engine = nc.vector
+            hn = h_col[:, 8 * b : 8 * b + 8]
+            pcr = pc_r[b % 2]
+            pcl = pc_l[b % 2]
+            r1 = work.tile([P, 8], F32, name="r1")
+            r2 = work.tile([P, 8], F32, name="r2")
+            engine.tensor_copy(out=pcr[:, :, 0], in_=hn)
+            engine.tensor_tensor(out=r1[:], in0=hn, in1=pcr[:, :, 0], op=ALU.subtract)
+            engine.tensor_copy(out=pcr[:, :, 1], in_=r1[:])
+            engine.tensor_tensor(out=r2[:], in0=r1[:], in1=pcr[:, :, 1], op=ALU.subtract)
+            engine.tensor_copy(out=pcr[:, :, 2], in_=r2[:])
+            engine.tensor_copy(out=pcl[:, :, 32:35], in_=pcr[:, :, 0:3])
 
         def norms_transpose(b):
-            ht_ps = ps_m.tile([P, P], F32, name="ht_ps", tag="misc")
+            ht_ps = ps_v.tile([P, P], F32, name="ht_ps", tag="sv")
             nc.tensor.transpose(ht_ps[:], h_col[:], ident_f[:])
-            misc[b] = ht_ps
+            misc[("h", b)] = ht_ps
 
         def norms_broadcast(b):
             ht = work.tile([P, P], F32, name="ht")
-            nc.vector.tensor_copy(out=ht[:], in_=misc.pop(b)[:])
+            nc.vector.tensor_copy(out=ht[:], in_=misc.pop(("h", b))[:])
             scratch = out[1024 * b : 1024 * b + 8, :]
             nc.sync.dma_start(out=scratch, in_=ht[8 * b : 8 * b + 8, :])
             hb = hbp.tile([P, 1024], F32, name="hb")
@@ -136,7 +156,7 @@ def tile_blockselfattention_kernel(tc, features, out):
         def norms_broadcast_on_chip(b):
             hb = hbp.tile([P, 1024], F32, name="hb")
             for half in range(2):
-                bank = ps_s.tile([P, 512], F32, name="s_ps")
+                bank = ps_v.tile([P, 512], F32, name="sv")
                 for a in range(4):
                     col = 8 * b + 4 * half + a
                     nc.tensor.transpose(
@@ -150,15 +170,28 @@ def tile_blockselfattention_kernel(tc, features, out):
                     nc.scalar.copy(out=hb[:, 512:1024], in_=bank[:])
             h_b[b] = hb
 
+        def norm_rows_transpose(b):
+            rl_ps = ps_m.tile([P, 2, 512], BF16, name="rl_ps", tag="misc")
+            for a in range(4):
+                cols = slice(P * a, P * a + P)
+                nc.tensor.transpose(rl_ps[:, 0, cols], pc_r[b % 2][:, a, :], ident_b[:])
+                nc.tensor.transpose(rl_ps[:, 1, cols], pc_l[b % 2][:, a, :], ident_b[:])
+            misc[("r", b)] = rl_ps
+
+        def norm_rows_out(b):
+            rl = rlp.tile([P, 2, 512], BF16, name="rl")
+            nc.scalar.copy(out=rl[:], in_=misc.pop(("r", b))[:])
+            r_l[b] = rl
+
         def x_transpose(b):
             xt_ps = ps_m.tile([P, 8, P], BF16, name="xt_ps", tag="misc")
             for a in range(8):
                 nc.tensor.transpose(xt_ps[:, a, :], x_sb[:, 2 * b + a // 4, a % 4, :], ident_b[:])
-            misc[b] = xt_ps
+            misc[("x", b)] = xt_ps
 
         def x_transpose_out(b):
             xt = xtp.tile([P, 8 * P], BF16, name="xt")
-            nc.scalar.copy(out=xt[:], in_=misc.pop(b)[:].rearrange("p a c -> p (a c)"))
+            nc.scalar.copy(out=xt[:], in_=misc.pop(("x", b))[:].rearrange("p a c -> p (a c)"))
             x_t[b] = xt
 
         def quantise_x(b):
@@ -168,67 +201,102 @@ def tile_blockselfattention_kernel(tc, features, out):
                 in_=xg_of.pop(b)[:].rearrange("p g d t -> p (g d t)"),
             )
 
-        def where(k):
-            return (k // 3,) + QUADS[k % 3]
+        def norms_after(st):
+            if st == 0:
+                return 1
+            if st % 2 == 1 and (st + 3) // 2 < NB:
+                return (st + 3) // 2
+            return None
 
-        def products(k):
-            b, hh, g = where(k)
+        ring = []
+        for st in range(NS):
+            ring.extend([("s", st, t) for t in range(4)])
+            if norms_after(st) is not None:
+                ring.append(("h", norms_after(st), 0))
+
+        def ring_fill(i):
+            if i >= len(ring):
+                return
+            kind, st, t = ring[i]
+            if kind == "h":
+                norms_transpose(st)
+                return
+            b = st // 2
+            a = 4 * (st % 2) + t
+            sv = ps_v.tile([P, 512], F32, name="sv")
+            nc.tensor.matmul(
+                sv[:], lhsT=x_t[b][:, P * a : P * a + P], rhs=x_t[b][:, 512:1024], start=True, stop=True
+            )
+            s_of[(st, t)] = sv
+
+        def product_bank(j):
+            if j >= 4 * NB:
+                return
+            b = j // 4
+            m = j % 4
             xt = x_t[b]
-            banks = []
+            rl = r_l[b]
+            sa = ps_a.tile([P, 4, P], F32, name="sa")
             for t in range(4):
-                a = 4 * g + t
-                s_ps = ps_s.tile([P, 512], F32, name="s_ps")
                 nc.tensor.matmul(
-                    s_ps[:],
-                    lhsT=xt[:, P * a : P * a + P],
-                    rhs=xt[:, 512 * hh : 512 * hh + 512],
+                    sa[:, t, :],
+                    lhsT=xt[:, P * t : P * t + P],
+                    rhs=xt[:, P * m : P * m + P],
                     start=True,
+                    stop=False,
+                )
+                nc.tensor.matmul(
+                    sa[:, t, :],
+                    lhsT=rl[:, 1, P * t : P * t + P],
+                    rhs=rl[:, 0, P * m : P * m + P],
+                    start=False,
                     stop=True,
                 )
-                banks.append(s_ps)
-            s_of[k] = banks
+            s_of[("a", j)] = sa
 
-        def distances(k, t):
-            b, hh, g = where(k)
+        def distances(st, t):
+            b = st // 2
             if t == 0:
-                u_of[k] = up.tile([P, 4, 512], F32, name="u")
-            a = 4 * g + t
+                u_of[st] = up.tile([P, 4, 512], F32, name="u")
+            a = 4 * (st % 2) + t
             nc.vector.scalar_tensor_tensor(
-                out=u_of[k][:, t, :],
-                in0=s_of[k][t][:],
+                out=u_of[st][:, t, :],
+                in0=s_of.pop((st, t))[:],
                 scalar=h_col[:, 8 * b + a : 8 * b + a + 1],
-                in1=h_b[b][:, 512 * hh : 512 * hh + 512],
-                op0=ALU.subtract,
-                op1=ALU.subtract,
+                in1=h_b[b][:, 512:1024],
+                op0=ALU.add,
+                op1=ALU.add,
             )
+            ring_fill(ring.index(("s", st, t)) + 3)
 
-        def exponentials(k):
-            s_of.pop(k)
-            if k % 2 == 0:
-                pl = pp.tile([P, 4, 512], BF16, name="pl")
-                nc.scalar.activation(out=pl[:], in_=u_of.pop(k)[:], func=ACT.Exp, scale=0.078125)
-                pl_of[k] = pl
-                return
-            grp = gp.tile([P, 512, 4], BF16, name="grp", align_bytes=64)
+        def exponentials(st):
+            pl = pp.tile([P, 4, 512], BF16, name="pl")
+            nc.scalar.activation(out=pl[:], in_=u_of.pop(st)[:], func=ACT.Exp, scale=0.078125)
+            pl_of[st] = pl
+
+        def exponentials_bank(j):
+            b = j // 4
+            m = j % 4
+            if m == 0:
+                grp_of[("a", b)] = gp.tile([P, 512, 4], BF16, name="grp", align_bytes=64)
             nc.scalar.activation(
-                out=grp[:],
-                in_=u_of.pop(k)[:].rearrange("p t c -> p c t"),
+                out=grp_of[("a", b)][:, P * m : P * m + P, :],
+                in_=s_of.pop(("a", j))[:].rearrange("p t c -> p c t"),
                 func=ACT.Exp,
                 scale=0.078125,
             )
-            grp_of[k] = grp
 
-        def clamp(k):
-            if k % 2 == 0:
-                grp = gp.tile([P, 512, 4], BF16, name="grp", align_bytes=64)
-                nc.vector.tensor_scalar_min(
-                    out=grp[:].rearrange("p (c i) t -> p c t i", i=4),
-                    in0=pl_of.pop(k)[:].rearrange("p t (c i) -> p c t i", i=4),
-                    scalar1=1.0,
-                )
-                grp_of[k] = grp
-                return
-            flat = grp_of[k][:].rearrange("p c t -> p (c t)")
+        def regroup_clamp(st):
+            grp = gp.tile([P, 512, 4], BF16, name="grp", align_bytes=64)
+            nc.vector.tensor_scalar_min(
+                out=grp[:].rearrange("p (c i) t -> p c t i", i=4),
+                in0=pl_of.pop(st)[:].rearrange("p t (c i) -> p c t i", i=4),
+                scalar1=1.0,
+            )
+            grp_of[st] = grp
+
+        def clamp_bank_unit(b):
+            flat = grp_of[("a", b)][:].rearrange("p c t -> p (c t)")
             nc.vector.tensor_scalar_min(out=flat, in0=flat, scalar1=1.0)
 
         def quantise(b, hh, g, grp):
@@ -243,8 +311,8 @@ def tile_blockselfattention_kernel(tc, features, out):
             )
 
         def mirror_transposes(b, half):
-            grp = grp_of[3 * b]
-            tp = ps_t.tile([P, 2, 4, P], BF16, name="tp")
+            grp = grp_of[2 * b]
+            tp = ps_m.tile([P, 2, 4, P], BF16, name="tp", tag="misc")
             for a in range(2):
                 for t in range(4):
                     nc.tensor.transpose(
@@ -252,17 +320,15 @@ def tile_blockselfattention_kernel(tc, features, out):
                     )
             tp_of[(b, half)] = tp
 
-        def mirror_out(b, half, engine):
+        def mirror_out(b, half):
             if half == 0:
                 mir_of[b] = gp.tile([P, 512, 4], BF16, name="mir", tag="grp", align_bytes=64)
-            dst = mir_of[b][:, 256 * half : 256 * half + 256, :].rearrange(
-                "p (a c) t -> p a c t", a=2
+            nc.scalar.copy(
+                out=mir_of[b][:, 256 * half : 256 * half + 256, :].rearrange(
+                    "p (a c) t -> p a c t", a=2
+                ),
+                in_=tp_of.pop((b, half))[:].rearrange("p a t c -> p a c t"),
             )
-            src = tp_of.pop((b, half))[:].rearrange("p a t c -> p a c t")
-            if engine == "scalar":
-                nc.scalar.copy(out=dst, in_=src)
-            else:
-                nc.vector.tensor_copy(out=dst, in_=src)
 
         def second_matmul(b, hh):
             acc = ps_o.tile([P, 4, D], F32, name="acc")
@@ -291,95 +357,103 @@ def tile_blockselfattention_kernel(tc, features, out):
                 in_=osb[:].rearrange("p t d -> p (t d)"),
             )
 
-        def block_at(k, lag):
-            if (k - lag) % 3 == 0 and 0 <= (k - lag) // 3 < NB:
-                return (k - lag) // 3
+        def block_at(st, lag, first=0):
+            if (st - lag) % 2 == 0 and first <= (st - lag) // 2 < NB:
+                return (st - lag) // 2
             return None
 
-        regroup_x(0)
-        regroup_x(1)
         squares_scalar(0)
+        squares_scalar(1)
         x_transpose(0)
-        half_norms(0)
+        norms(0)
+        norm_pieces(0)
         x_transpose_out(0)
         norms_broadcast_on_chip(0)
-        products(0)
-        squares_scalar(1)
-        x_transpose(1)
-        x_transpose_out(1)
-        half_norms(1)
-        norms_transpose(1)
-        norms_broadcast(1)
-        quantise_x(0)
-        quantise_x(1)
-        squares_gpsimd(2)
-        regroup_x(2)
+        for i in range(3):
+            ring_fill(i)
+        norm_rows_transpose(0)
+        norm_rows_out(0)
+        product_bank(0)
+        product_bank(1)
+        squares_scalar(2)
 
-        for k in range(NU + 7):
-            live = k < NU
-            b = block_at(k, -6)
-            if b is not None and b >= 2:
-                half_norms(b)
-            b = block_at(k, -5)
-            if b is not None and b >= 2:
-                norms_broadcast(b)
-            b = block_at(k, -4)
-            if b is not None and b >= 2:
+        for st in range(NS + 5):
+            live = st < NS
+            if live:
+                exponentials_bank(2 * st)
+                exponentials_bank(2 * st + 1)
+            if live:
+                distances(st, 0)
+            b = block_at(st, 2)
+            if b is not None:
+                clamp_bank_unit(b)
+            if st == 0:
+                norms(1)
+                norm_pieces(1)
+            b = block_at(st, -4, 2)
+            if b is not None:
+                norms(b)
+                norm_pieces(b)
+            if st == 1:
+                quantise_x(0)
+            b = block_at(st, -1, 1)
+            if b is not None:
                 quantise_x(b)
-            if live:
-                distances(k, 0)
-                distances(k, 1)
-            if 0 <= k - 2 < NU:
-                clamp(k - 2)
-            if live:
-                distances(k, 2)
-                distances(k, 3)
-            if k + 1 < NU:
-                products(k + 1)
-            b = block_at(k, 2)
+            b = block_at(st, 2)
             if b is not None:
-                mirror_transposes(b, 0)
-            b = block_at(k, 3)
-            if b is not None:
-                mirror_transposes(b, 1)
-                grp_of.pop(3 * b)
-            b = block_at(k, -6)
-            if b is not None and b >= 2:
-                norms_transpose(b)
-            b = block_at(k, -5)
-            if b is not None and b >= 2:
-                x_transpose(b)
-            b = block_at(k, 3)
-            if b is not None:
-                mirror_out(b, 0, "scalar")
-            b = block_at(k, 4)
-            if b is not None:
-                mirror_out(b, 1, "scalar")
-            b = block_at(k, 5)
+                mirror_out(b, 0)
+                mirror_out(b, 1)
+            b = block_at(st, 3)
             if b is not None:
                 store(b, 1)
-            b = block_at(k, 6)
+            b = block_at(st, 4)
             if b is not None:
                 store(b, 0)
-            b = block_at(k, -4)
-            if b is not None and b >= 2:
+            b = block_at(st, -1, 1)
+            if b is not None:
                 x_transpose_out(b)
+                norm_rows_out(b)
             if live:
-                exponentials(k)
-            if 0 <= k - 2 < NU:
-                bb, hh, g = where(k - 2)
-                grp = grp_of[k - 2] if (k - 2) % 3 == 0 else grp_of.pop(k - 2)
-                quantise(bb, hh, g, grp)
-            b = block_at(k, 4)
+                distances(st, 1)
+            if 0 <= st - 1 < NS:
+                regroup_clamp(st - 1)
+            if live:
+                distances(st, 2)
+                distances(st, 3)
+            b = norms_after(st)
             if b is not None:
-                second_matmul(b, 1)
-            b = block_at(k, 5)
+                norms_broadcast(b)
+                ring_fill(ring.index(("h", b, 0)) + 3)
+            if live:
+                product_bank(2 * st + 2)
+                product_bank(2 * st + 3)
+            b = block_at(st, 1)
             if b is not None:
+                mirror_transposes(b, 0)
+                mirror_transposes(b, 1)
+            b = block_at(st, -2, 1)
+            if b is not None:
+                x_transpose(b)
+                norm_rows_transpose(b)
+            if live:
+                exponentials(st)
+            if 0 <= st - 1 < NS:
+                quantise((st - 1) // 2, 1, (st - 1) % 2, grp_of.pop(st - 1))
+            b = block_at(st, 2)
+            if b is not None:
+                quantise(b, 0, 0, grp_of.pop(("a", b)))
                 quantise(b, 0, 1, mir_of.pop(b))
+                second_matmul(b, 1)
+            b = block_at(st, 3)
+            if b is not None:
                 second_matmul(b, 0)
                 w_q.pop(b)
                 w_s.pop(b)
-            b = block_at(k, -8)
-            if b is not None and b >= 3:
-                squares_gpsimd(b)
+            b = block_at(st, -6, 3)
+            if b is not None:
+                squares_scalar(b)
+            if st == 0:
+                regroup_x(0)
+            b = block_at(st, -2, 1)
+            if b is not None:
                 regroup_x(b)

@@ -15,8 +15,23 @@ AX = mybir.AxisListType
 P = 128
 NB = 16
 D = 128
-NS = 2 * NB
+S8 = 8
+SCALE = 2.0 / 25.6
 FLOPS = 2 * 2 * 16 * 1024 * 1024 * 128
+
+N_BANKS = [
+    [(0, 0, 4)],
+    [(1, 0, 4)],
+    [(2, 4, 4)],
+    [(3, 4, 4)],
+    [(2, 2, 2), (3, 2, 2)],
+    [(4, 4, 4)],
+    [(5, 4, 4)],
+    [(7, 6, 2)],
+]
+V_BANKS = [(0, 4, 4), (1, 4, 4), (6, 6, 2)]
+NN = len(N_BANKS)
+BATCHES = [(0, 1), (1, 4), (4, 8), (8, 12), (12, 16)]
 
 
 def tile_blockselfattention_kernel(tc, features, out):
@@ -25,174 +40,344 @@ def tile_blockselfattention_kernel(tc, features, out):
         ctx.enter_context(tc.manual_schedule())
         const = ctx.enter_context(tc.tile_pool(name="const", bufs=1))
         work = ctx.enter_context(tc.tile_pool(name="work", bufs=2))
-        xgp = ctx.enter_context(tc.tile_pool(name="xgp", bufs=3))
+        xgp = ctx.enter_context(tc.tile_pool(name="xgp", bufs=2))
         xtp = ctx.enter_context(tc.tile_pool(name="xtp", bufs=3))
-        hbp = ctx.enter_context(tc.tile_pool(name="hbp", bufs=4))
-        rlp = ctx.enter_context(tc.tile_pool(name="rlp", bufs=3))
-        up = ctx.enter_context(tc.tile_pool(name="up", bufs=3))
-        gp = ctx.enter_context(tc.tile_pool(name="gp", bufs=7))
-        pp = ctx.enter_context(tc.tile_pool(name="pp", bufs=4))
-        wp = ctx.enter_context(tc.tile_pool(name="wp", bufs=3))
-        op = ctx.enter_context(tc.tile_pool(name="op", bufs=3))
-        ps_v = ctx.enter_context(tc.psum_pool(name="ps_v", bufs=3))
-        ps_a = ctx.enter_context(tc.psum_pool(name="ps_a", bufs=2))
-        ps_m = ctx.enter_context(tc.psum_pool(name="ps_m", bufs=2))
+        hbp = ctx.enter_context(tc.tile_pool(name="hbp", bufs=6))
+        up = ctx.enter_context(tc.tile_pool(name="up", bufs=2))
+        plp = ctx.enter_context(tc.tile_pool(name="plp", bufs=2))
+        gp = ctx.enter_context(tc.tile_pool(name="gp", bufs=2))
+        wp = ctx.enter_context(tc.tile_pool(name="wp", bufs=2))
+        op = ctx.enter_context(tc.tile_pool(name="op", bufs=2))
+        ps_n = ctx.enter_context(tc.psum_pool(name="ps_n", bufs=3))
+        ps_v = ctx.enter_context(tc.psum_pool(name="ps_v", bufs=1))
+        ps_t = ctx.enter_context(tc.psum_pool(name="ps_t", bufs=2))
+        ps_m = ctx.enter_context(tc.psum_pool(name="ps_m", bufs=1))
         ps_o = ctx.enter_context(tc.psum_pool(name="ps_o", bufs=1))
 
-        x_sb = const.tile([P, 2 * NB, 4, D], BF16, name="x_sb")
-        xv = features.rearrange("(q p t) d -> p q (t d)", p=P, t=4)
+        x_sb = const.tile([P, NB * S8, D], BF16, name="x_sb")
+        xv = features.rearrange("(q p e) d -> p q (e d)", p=P, e=2)
 
         def load(queue, q0, q1):
             queue.dma_start(
-                out=x_sb[:, q0:q1].rearrange("p q t d -> p q (t d)"), in_=xv[:, q0:q1, :]
+                out=x_sb[:, 2 * q0 : 2 * q1, :].rearrange("p (q e) d -> p q (e d)", e=2),
+                in_=xv[:, q0:q1, :],
             )
 
         load(nc.sync, 0, 2)
         load(nc.sync, 2, 4)
-        load(nc.scalar, 4, 8)
-        load(nc.scalar, 8, 16)
-        load(nc.scalar, 16, 32)
+        load(nc.scalar, 4, 16)
+        load(nc.sync, 16, 40)
+        load(nc.sync, 40, 64)
 
         ident_b = const.tile([P, P], BF16, name="ident_b")
         make_identity(nc, ident_b[:])
         ident_f = const.tile([P, P], F32, name="ident_f")
         make_identity(nc, ident_f[:])
-        h_col = const.tile([P, P], F32, name="h_col")
-        nc.vector.memset(h_col[:], 0.0)
+        sqc = const.tile([P, P], F32, name="sqc")
+        nc.vector.memset(sqc[:], 0.0)
+        hcol = const.tile([P, P], F32, name="hcol")
+        bias = const.tile([P, P], F32, name="bias")
+        pcs = []
+        for k in range(len(BATCHES)):
+            pc = const.tile([P, P], BF16, name="pc%d" % k)
+            nc.vector.memset(pc[:], 0.0)
+            pcs.append(pc)
+        sel = const.tile([P, 32], F32, name="sel")
+        nc.vector.tensor_reduce(
+            out=sel[:],
+            in_=ident_b[:, 0:96].rearrange("p (j k) -> p j k", k=3),
+            axis=AX.X,
+            op=ALU.add,
+        )
+        selc = const.tile([P, 32, P], BF16, name="selc")
+        nc.vector.tensor_scalar_mul(
+            out=selc[:, 0:8, :], in0=sel[:, 0:8].unsqueeze(2).to_broadcast([P, 8, P]), scalar1=-0.5
+        )
+        nc.gpsimd.tensor_scalar(
+            out=selc[:, 8:32, :],
+            in0=sel[:, 8:32].unsqueeze(2).to_broadcast([P, 24, P]),
+            scalar1=-0.5,
+            scalar2=0.0,
+            op0=ALU.mult,
+            op1=ALU.add,
+        )
         xq = const.tile([P, NB, 256], U32, name="xq", align_bytes=64)
         xs = const.tile([P, NB, 256], U8, name="xs", align_bytes=64)
-        pc_r = []
-        pc_l = []
-        for i in range(2):
-            pcr = const.tile([P, 8, P], BF16, name="pcr%d" % i)
-            pcl = const.tile([P, 8, P], BF16, name="pcl%d" % i)
-            nc.vector.memset(pcr[:], 0.0)
-            nc.vector.memset(pcl[:], 0.0)
-            nc.vector.memset(pcr[:, :, 32:35], 1.0)
-            nc.vector.memset(pcl[:, :, 0:3], 1.0)
-            pc_r.append(pcr)
-            pc_l.append(pcl)
 
         x_t = {}
         h_b = {}
-        r_l = {}
-        w_q = {}
-        w_s = {}
-        grp_of = {}
+        h_t = {}
         pl_of = {}
-        mir_of = {}
-        sq_of = {}
-        xg_of = {}
-        misc = {}
-        s_of = {}
         u_of = {}
-        tp_of = {}
+        n_of = {}
+        v_of = {}
+        t_of = {}
+        grp_of = {}
+        w_of = {}
+        xg_of = {}
         acc_of = {}
+        o_of = {}
+        misc = {}
 
-        def xblock(b):
-            return x_sb[:, 2 * b : 2 * b + 2]
+        def batch_of(b):
+            return [k for k in range(len(BATCHES)) if BATCHES[k][0] <= b < BATCHES[k][1]][0]
 
-        def squares_scalar(b):
-            sqf = work.tile([P, 8, D], F32, name="sqf")
+        def square(b, s):
+            junk = work.tile([P, D], BF16, name="junk")
             nc.scalar.activation(
-                out=sqf[:].rearrange("p a d -> p (a d)"),
-                in_=xblock(b).rearrange("p g t d -> p (g t d)"),
+                out=junk[:],
+                in_=x_sb[:, S8 * b + s, :],
                 func=ACT.Square,
+                accum_out=sqc[:, S8 * b + s : S8 * b + s + 1],
             )
-            sq_of[b] = (sqf, D)
-
-        def squares_gpsimd(b):
-            xa = xblock(b).rearrange("p g t d -> p (g t) d")
-            sqf = work.tile([P, 8, D], F32, name="sqf")
-            nc.gpsimd.tensor_tensor(out=sqf[:], in0=xa, in1=xa, op=ALU.mult)
-            for w in (64, 32, 16):
-                nc.gpsimd.tensor_tensor(
-                    out=sqf[:, :, 0:w], in0=sqf[:, :, 0:w], in1=sqf[:, :, w : 2 * w], op=ALU.add
-                )
-            sq_of[b] = (sqf, 16)
-
-        def regroup_x(b):
-            xg = xgp.tile([P, 2, D, 4], BF16, name="xg", align_bytes=64)
-            nc.vector.tensor_copy(out=xg[:], in_=xblock(b).rearrange("p g t d -> p g d t"))
-            xg_of[b] = xg
-
-        def norms(b):
-            sqf, width = sq_of.pop(b)
-            sq8 = work.tile([P, 8], F32, name="sq8")
-            nc.vector.tensor_reduce(out=sq8[:], in_=sqf[:, :, 0:width], axis=AX.X, op=ALU.add)
-            hn = h_col[:, 8 * b : 8 * b + 8]
-            nc.vector.tensor_scalar_mul(out=hn, in0=sq8[:], scalar1=-0.5)
-
-        def norm_pieces(b):
-            engine = nc.vector
-            hn = h_col[:, 8 * b : 8 * b + 8]
-            pcr = pc_r[b % 2]
-            pcl = pc_l[b % 2]
-            r1 = work.tile([P, 8], F32, name="r1")
-            r2 = work.tile([P, 8], F32, name="r2")
-            engine.tensor_copy(out=pcr[:, :, 0], in_=hn)
-            engine.tensor_tensor(out=r1[:], in0=hn, in1=pcr[:, :, 0], op=ALU.subtract)
-            engine.tensor_copy(out=pcr[:, :, 1], in_=r1[:])
-            engine.tensor_tensor(out=r2[:], in0=r1[:], in1=pcr[:, :, 1], op=ALU.subtract)
-            engine.tensor_copy(out=pcr[:, :, 2], in_=r2[:])
-            engine.tensor_copy(out=pcl[:, :, 32:35], in_=pcr[:, :, 0:3])
-
-        def norms_transpose(b):
-            ht_ps = ps_v.tile([P, P], F32, name="ht_ps", tag="sv")
-            nc.tensor.transpose(ht_ps[:], h_col[:], ident_f[:])
-            misc[("h", b)] = ht_ps
-
-        def norms_broadcast(b):
-            ht = work.tile([P, P], F32, name="ht")
-            nc.vector.tensor_copy(out=ht[:], in_=misc.pop(("h", b))[:])
-            scratch = out[1024 * b : 1024 * b + 8, :]
-            nc.sync.dma_start(out=scratch, in_=ht[8 * b : 8 * b + 8, :])
-            hb = hbp.tile([P, 1024], F32, name="hb")
-            nc.sync.dma_start(
-                out=hb[:], in_=scratch.rearrange("a p -> (a p)").partition_broadcast(P)
-            )
-            h_b[b] = hb
-
-        def norms_broadcast_on_chip(b):
-            hb = hbp.tile([P, 1024], F32, name="hb")
-            for half in range(2):
-                bank = ps_v.tile([P, 512], F32, name="sv")
-                for a in range(4):
-                    col = 8 * b + 4 * half + a
-                    nc.tensor.transpose(
-                        bank[:, P * a : P * a + P],
-                        h_col[:, col : col + 1].to_broadcast([P, P]),
-                        ident_f[:],
-                    )
-                if half == 0:
-                    nc.vector.tensor_copy(out=hb[:, 0:512], in_=bank[:])
-                else:
-                    nc.scalar.copy(out=hb[:, 512:1024], in_=bank[:])
-            h_b[b] = hb
-
-        def norm_rows_transpose(b):
-            rl_ps = ps_m.tile([P, 2, 512], BF16, name="rl_ps", tag="misc")
-            for a in range(4):
-                cols = slice(P * a, P * a + P)
-                nc.tensor.transpose(rl_ps[:, 0, cols], pc_r[b % 2][:, a, :], ident_b[:])
-                nc.tensor.transpose(rl_ps[:, 1, cols], pc_l[b % 2][:, a, :], ident_b[:])
-            misc[("r", b)] = rl_ps
-
-        def norm_rows_out(b):
-            rl = rlp.tile([P, 2, 512], BF16, name="rl")
-            nc.scalar.copy(out=rl[:], in_=misc.pop(("r", b))[:])
-            r_l[b] = rl
 
         def x_transpose(b):
-            xt_ps = ps_m.tile([P, 8, P], BF16, name="xt_ps", tag="misc")
-            for a in range(8):
-                nc.tensor.transpose(xt_ps[:, a, :], x_sb[:, 2 * b + a // 4, a % 4, :], ident_b[:])
+            xt_ps = ps_m.tile([P, S8, P], BF16, name="xt_ps", tag="misc")
+            for s in range(S8):
+                nc.tensor.transpose(xt_ps[:, s, :], x_sb[:, S8 * b + s, :], ident_b[:])
             misc[("x", b)] = xt_ps
 
         def x_transpose_out(b):
-            xt = xtp.tile([P, 8 * P], BF16, name="xt")
-            nc.scalar.copy(out=xt[:], in_=misc.pop(("x", b))[:].rearrange("p a c -> p (a c)"))
+            xt = xtp.tile([P, S8, P], BF16, name="xt")
+            nc.scalar.copy(out=xt[:], in_=misc.pop(("x", b))[:])
             x_t[b] = xt
+
+        def norm_cols(k):
+            b0, b1 = BATCHES[k]
+            return slice(S8 * b0, S8 * b1)
+
+        def norm_scaled(k):
+            cs = norm_cols(k)
+            nc.vector.tensor_scalar_mul(out=bias[:, cs], in0=sqc[:, cs], scalar1=-0.5 * SCALE)
+            nc.vector.tensor_scalar_mul(out=hcol[:, cs], in0=sqc[:, cs], scalar1=-0.5)
+
+        def norm_piece(k, piece):
+            b0, b1 = BATCHES[k]
+            cs = norm_cols(k)
+            n = S8 * (b1 - b0)
+            j0 = S8 * (b0 % 4)
+            pcv = pcs[k][:, 0:96].rearrange("p (j k) -> p j k", k=3)[:, j0 : j0 + n]
+            if piece == 0:
+                nc.vector.tensor_copy(out=pcv[:, :, 0], in_=sqc[:, cs])
+            elif piece == 1:
+                r1 = work.tile([P, 32], F32, name="r1")
+                nc.vector.tensor_tensor(
+                    out=r1[:, 0:n], in0=sqc[:, cs], in1=pcv[:, :, 0], op=ALU.subtract
+                )
+                misc[("r1", k)] = r1
+            elif piece == 2:
+                nc.vector.tensor_copy(out=pcv[:, :, 1], in_=misc[("r1", k)][:, 0:n])
+            else:
+                nc.vector.tensor_tensor(
+                    out=pcv[:, :, 2], in0=misc.pop(("r1", k))[:, 0:n], in1=pcv[:, :, 1], op=ALU.subtract
+                )
+
+        def pieces_transpose(k):
+            hp = ps_m.tile([P, P], BF16, name="hp", tag="misc")
+            nc.tensor.transpose(hp[:], pcs[k][:], ident_b[:])
+            misc[("hp", k)] = hp
+
+        def pieces_out(k):
+            ht = const.tile([P, P], BF16, name="ht%d" % k)
+            nc.vector.tensor_copy(out=ht[:], in_=misc.pop(("hp", k))[:])
+            h_t[k] = ht
+
+        def norms_transpose(k):
+            sp = ps_m.tile([P, P], F32, name="sp", tag="misc")
+            nc.tensor.transpose(sp[:], sqc[:], ident_f[:])
+            misc[("sp", k)] = sp
+
+        def norms_broadcast(k):
+            b0, b1 = BATCHES[k]
+            rows = work.tile([P, P], F32, name="rows")
+            nc.vector.tensor_scalar_mul(out=rows[:], in0=misc.pop(("sp", k))[:], scalar1=-0.5)
+            base = 1024 * (b1 - 1)
+            nc.sync.dma_start(
+                out=out[base : base + S8 * (b1 - b0), :], in_=rows[S8 * b0 : S8 * b1, :]
+            )
+            for b in range(b0, b1):
+                first = base + S8 * (b - b0) + 4
+                hb = hbp.tile([P, 512], F32, name="hb")
+                nc.sync.dma_start(
+                    out=hb[:],
+                    in_=out[first : first + 4, :].rearrange("a p -> (a p)").partition_broadcast(P),
+                )
+                h_b[b] = hb
+
+        def norms_broadcast_on_chip(b):
+            bank = ps_v.tile([P, 512], F32, name="sv")
+            for s in range(4):
+                col = S8 * b + 4 + s
+                nc.tensor.transpose(
+                    bank[:, P * s : P * s + P], sqc[:, col : col + 1].to_broadcast([P, P]), ident_f[:]
+                )
+            hb = hbp.tile([P, 512], F32, name="hb")
+            nc.vector.tensor_scalar_mul(out=hb[:], in0=bank[:], scalar1=-0.5)
+            h_b[b] = hb
+
+        def cols_of(b, s0, ns):
+            return x_t[b][:, s0 : s0 + ns, :].rearrange("p s c -> p (s c)")
+
+        def fill_n(i):
+            if i >= NN * NB:
+                return
+            b = i // NN
+            bank = ps_n.tile([P, 512], F32, name="sn")
+            off = 0
+            for a, s0, ns in N_BANKS[i % NN]:
+                nc.tensor.matmul(
+                    bank[:, off : off + P * ns],
+                    lhsT=x_t[b][:, a, :],
+                    rhs=cols_of(b, s0, ns),
+                    start=True,
+                    stop=False,
+                )
+                for k in range(ns):
+                    nc.tensor.matmul(
+                        bank[:, off + P * k : off + P * k + P],
+                        lhsT=selc[:, S8 * (b % 4) + s0 + k, :],
+                        rhs=h_t[batch_of(b)][:],
+                        start=False,
+                        stop=(k == ns - 1),
+                    )
+                off += P * ns
+            n_of[i] = bank
+
+        def planes(b):
+            if b not in pl_of:
+                pl_of[b] = plp.tile([P, S8, 1024], BF16, name="pl", align_bytes=64)
+            return pl_of[b]
+
+        def exp_n(i):
+            b = i // NN
+            bank = n_of.pop(i)
+            off = 0
+            for a, s0, ns in N_BANKS[i % NN]:
+                nc.scalar.activation(
+                    out=planes(b)[:, a, P * s0 : P * (s0 + ns)].rearrange(
+                        "p (q w e) -> p q w e", w=P, e=2
+                    ),
+                    in_=bank[:, off : off + P * ns].rearrange("p (q e w) -> p q w e", w=P, e=2),
+                    func=ACT.Exp,
+                    scale=SCALE,
+                    bias=bias[:, S8 * b + a : S8 * b + a + 1],
+                )
+                off += P * ns
+
+        def fill_v(i):
+            if i >= 3 * NB:
+                return
+            b = i // 3
+            a, s0, ns = V_BANKS[i % 3]
+            bank = ps_v.tile([P, 512], F32, name="sv")
+            nc.tensor.matmul(
+                bank[:, 0 : P * ns], lhsT=x_t[b][:, a, :], rhs=cols_of(b, s0, ns), start=True, stop=True
+            )
+            v_of[i] = bank
+
+        def distances(b, k):
+            a, s0, ns = V_BANKS[k]
+            if k == 0:
+                u_of[b] = up.tile([P, 3, 512], F32, name="u")
+            nc.vector.scalar_tensor_tensor(
+                out=u_of[b][:, k, 0 : P * ns],
+                in0=v_of.pop(3 * b + k)[:, 0 : P * ns],
+                scalar=hcol[:, S8 * b + a : S8 * b + a + 1],
+                in1=h_b[b][:, P * (s0 - 4) : P * (s0 - 4 + ns)],
+                op0=ALU.add,
+                op1=ALU.add,
+            )
+
+        def exp_v(b, k):
+            a, s0, ns = V_BANKS[k]
+            nc.scalar.activation(
+                out=planes(b)[:, a, P * s0 : P * (s0 + ns)].rearrange("p (q w e) -> p q w e", w=P, e=2),
+                in_=u_of[b][:, k, 0 : P * ns].rearrange("p (q e w) -> p q w e", w=P, e=2),
+                func=ACT.Exp,
+                scale=SCALE,
+            )
+
+        def groups(b):
+            if b not in grp_of:
+                g0 = gp.tile([P, 2, 4, P, 4], BF16, name="g0", align_bytes=64)
+                g1 = gp.tile([P, 2, 4, P, 4], BF16, name="g1", align_bytes=64)
+                grp_of[b] = (g0, g1)
+            return grp_of[b]
+
+        def flat(b, g, e):
+            return groups(b)[g][:, e].rearrange("p q c t -> p (q c t)")
+
+        def regroup(b, g, e):
+            q0 = 1 if g == 0 else 3
+            nc.vector.tensor_scalar_min(
+                out=flat(b, g, e)[:, 512 * q0 : 2048].rearrange("p (k i t) -> p k t i", i=4, t=4),
+                in0=pl_of[b][:, 4 * g : 4 * g + 4, 256 * q0 : 1024].rearrange(
+                    "p t (k i x) -> p x k t i", i=4, x=2
+                )[:, e],
+                scalar1=1.0,
+            )
+
+        def mirror_transpose(b, name):
+            bank = ps_t.tile([P, 2, 2, P], F32, name="tb")
+            if name == "A":
+                units = [(0, 0), (1, 0)]
+                half = 0
+            elif name == "B0":
+                units = [(0, 0), (2, 0)]
+                half = 1
+            elif name == "B1":
+                units = [(1, 0), (3, 0)]
+                half = 1
+            else:
+                units = [(4, 0), (5, 0)]
+                half = 1
+            for k in range(2):
+                a = units[k][0]
+                for u in range(2):
+                    c0 = 512 * half + 256 * u
+                    nc.tensor.transpose(
+                        bank[:, u, k, :], pl_of[b][:, a, c0 : c0 + 256].bitcast(F32), ident_f[:]
+                    )
+            t_of[(b, name)] = bank
+
+        def mirror_out(b, name):
+            bank = t_of.pop((b, name))[:].bitcast(BF16)
+            if name in ("B0", "B1"):
+                e = 0 if name == "B0" else 1
+                nc.vector.tensor_scalar_min(
+                    out=flat(b, 1, e)[:, 0:1024].rearrange("p (r u x) -> p r u x", u=2, x=2),
+                    in0=bank.rearrange("p u k (r x) -> p (k r) u x", x=2),
+                    scalar1=1.0,
+                )
+                return
+            g, q = (0, 0) if name == "A" else (1, 2)
+            for e in range(2):
+                nc.vector.tensor_scalar_min(
+                    out=flat(b, g, e)[:, 512 * q : 512 * q + 512].rearrange(
+                        "p (r u x) -> p r u x", u=2, x=2
+                    ),
+                    in0=bank[:, :, e].rearrange("p u (r x) -> p r u x", x=2),
+                    scalar1=1.0,
+                )
+
+        def quantise(b, g, e):
+            if b not in w_of:
+                wq = wp.tile([P, 2, 1024], U32, name="wq", align_bytes=64)
+                ws = wp.tile([P, 2, 1024], U8, name="ws", align_bytes=64)
+                w_of[b] = (wq, ws)
+            wq, ws = w_of[b]
+            cols = slice(512 * e, 512 * e + 512)
+            nc.vector.quantize_mx(
+                out=wq[:, g, cols].bitcast(FP8X4), scales=ws[:, g, cols], in_=flat(b, g, e)
+            )
+
+        def regroup_x(b):
+            xg = xgp.tile([P, 2, D, 4], BF16, name="xg", align_bytes=64)
+            nc.vector.tensor_copy(
+                out=xg[:],
+                in_=x_sb[:, S8 * b : S8 * b + S8, :].rearrange("p (g t) d -> p g d t", g=2),
+            )
+            xg_of[b] = xg
 
         def quantise_x(b):
             nc.vector.quantize_mx(
@@ -201,259 +386,158 @@ def tile_blockselfattention_kernel(tc, features, out):
                 in_=xg_of.pop(b)[:].rearrange("p g d t -> p (g d t)"),
             )
 
-        def norms_after(st):
-            if st == 0:
-                return 1
-            if st % 2 == 1 and (st + 3) // 2 < NB:
-                return (st + 3) // 2
-            return None
-
-        ring = []
-        for st in range(NS):
-            ring.extend([("s", st, t) for t in range(4)])
-            if norms_after(st) is not None:
-                ring.append(("h", norms_after(st), 0))
-
-        def ring_fill(i):
-            if i >= len(ring):
-                return
-            kind, st, t = ring[i]
-            if kind == "h":
-                norms_transpose(st)
-                return
-            b = st // 2
-            a = 4 * (st % 2) + t
-            sv = ps_v.tile([P, 512], F32, name="sv")
-            nc.tensor.matmul(
-                sv[:], lhsT=x_t[b][:, P * a : P * a + P], rhs=x_t[b][:, 512:1024], start=True, stop=True
-            )
-            s_of[(st, t)] = sv
-
-        def product_bank(j):
-            if j >= 4 * NB:
-                return
-            b = j // 4
-            m = j % 4
-            xt = x_t[b]
-            rl = r_l[b]
-            sa = ps_a.tile([P, 4, P], F32, name="sa")
-            for t in range(4):
-                nc.tensor.matmul(
-                    sa[:, t, :],
-                    lhsT=xt[:, P * t : P * t + P],
-                    rhs=xt[:, P * m : P * m + P],
-                    start=True,
-                    stop=False,
-                )
-                nc.tensor.matmul(
-                    sa[:, t, :],
-                    lhsT=rl[:, 1, P * t : P * t + P],
-                    rhs=rl[:, 0, P * m : P * m + P],
-                    start=False,
-                    stop=True,
-                )
-            s_of[("a", j)] = sa
-
-        def distances(st, t):
-            b = st // 2
-            if t == 0:
-                u_of[st] = up.tile([P, 4, 512], F32, name="u")
-            a = 4 * (st % 2) + t
-            nc.vector.scalar_tensor_tensor(
-                out=u_of[st][:, t, :],
-                in0=s_of.pop((st, t))[:],
-                scalar=h_col[:, 8 * b + a : 8 * b + a + 1],
-                in1=h_b[b][:, 512:1024],
-                op0=ALU.add,
-                op1=ALU.add,
-            )
-            ring_fill(ring.index(("s", st, t)) + 3)
-
-        def exponentials(st):
-            pl = pp.tile([P, 4, 512], BF16, name="pl")
-            nc.scalar.activation(out=pl[:], in_=u_of.pop(st)[:], func=ACT.Exp, scale=0.078125)
-            pl_of[st] = pl
-
-        def exponentials_bank(j):
-            b = j // 4
-            m = j % 4
-            if m == 0:
-                grp_of[("a", b)] = gp.tile([P, 512, 4], BF16, name="grp", align_bytes=64)
-            nc.scalar.activation(
-                out=grp_of[("a", b)][:, P * m : P * m + P, :],
-                in_=s_of.pop(("a", j))[:].rearrange("p t c -> p c t"),
-                func=ACT.Exp,
-                scale=0.078125,
-            )
-
-        def regroup_clamp(st):
-            grp = gp.tile([P, 512, 4], BF16, name="grp", align_bytes=64)
-            nc.vector.tensor_scalar_min(
-                out=grp[:].rearrange("p (c i) t -> p c t i", i=4),
-                in0=pl_of.pop(st)[:].rearrange("p t (c i) -> p c t i", i=4),
-                scalar1=1.0,
-            )
-            grp_of[st] = grp
-
-        def clamp_bank_unit(b):
-            flat = grp_of[("a", b)][:].rearrange("p c t -> p (c t)")
-            nc.vector.tensor_scalar_min(out=flat, in0=flat, scalar1=1.0)
-
-        def quantise(b, hh, g, grp):
-            if b not in w_q:
-                w_q[b] = wp.tile([P, 2, 1024], U32, name="wq", align_bytes=64)
-                w_s[b] = wp.tile([P, 2, 1024], U8, name="ws", align_bytes=64)
-            cols = slice(512 * hh, 512 * hh + 512)
-            nc.vector.quantize_mx(
-                out=w_q[b][:, g, cols].bitcast(FP8X4),
-                scales=w_s[b][:, g, cols],
-                in_=grp[:].rearrange("p c t -> p (c t)"),
-            )
-
-        def mirror_transposes(b, half):
-            grp = grp_of[2 * b]
-            tp = ps_m.tile([P, 2, 4, P], BF16, name="tp", tag="misc")
-            for a in range(2):
-                for t in range(4):
-                    nc.tensor.transpose(
-                        tp[:, a, t, :], grp[:, P * t : P * t + P, 2 * half + a], ident_b[:]
-                    )
-            tp_of[(b, half)] = tp
-
-        def mirror_out(b, half):
-            if half == 0:
-                mir_of[b] = gp.tile([P, 512, 4], BF16, name="mir", tag="grp", align_bytes=64)
-            nc.scalar.copy(
-                out=mir_of[b][:, 256 * half : 256 * half + 256, :].rearrange(
-                    "p (a c) t -> p a c t", a=2
-                ),
-                in_=tp_of.pop((b, half))[:].rearrange("p a t c -> p a c t"),
-            )
-
-        def second_matmul(b, hh):
+        def second_matmul(b, e):
+            wq, ws = w_of[b]
             acc = ps_o.tile([P, 4, D], F32, name="acc")
-            for mm in range(4):
-                mc = slice(512 * hh + P * mm, 512 * hh + P * mm + P)
-                for gg in range(2):
+            for q in range(4):
+                mc = slice(512 * e + P * q, 512 * e + P * q + P)
+                for g in range(2):
                     nc.tensor.matmul_mx(
-                        out=acc[:, mm, :],
-                        lhsT=w_q[b][:, gg, mc].bitcast(FP8X4),
-                        lhsT_scale=w_s[b][:, gg, mc],
-                        rhs=xq[:, b, P * gg : P * gg + P].bitcast(FP8X4),
-                        rhs_scale=xs[:, b, P * gg : P * gg + P],
-                        start=(gg == 0),
-                        stop=(gg == 1),
+                        out=acc[:, q, :],
+                        lhsT=wq[:, g, mc].bitcast(FP8X4),
+                        lhsT_scale=ws[:, g, mc],
+                        rhs=xq[:, b, P * g : P * g + P].bitcast(FP8X4),
+                        rhs_scale=xs[:, b, P * g : P * g + P],
+                        start=(g == 0),
+                        stop=(g == 1),
                     )
-            acc_of[(b, hh)] = acc
+            acc_of[(b, e)] = acc
 
-        def store(b, hh):
-            osb = op.tile([P, 4, D], F32, name="osb")
+        def scale_out(b, e):
+            if e == 0:
+                o_of[b] = op.tile([P, 4, 2, D], F32, name="osb")
             nc.scalar.activation(
-                out=osb[:], in_=acc_of.pop((b, hh))[:], func=ACT.Copy, scale=1.0 / 1024.0
+                out=o_of[b][:, :, e, :], in_=acc_of.pop((b, e))[:], func=ACT.Copy, scale=1.0 / 1024.0
             )
-            rows = out[1024 * b + 512 * hh : 1024 * b + 512 * hh + 512, :]
+
+        def store(b):
             nc.sync.dma_start(
-                out=rows.rearrange("(p t) d -> p (t d)", t=4),
-                in_=osb[:].rearrange("p t d -> p (t d)"),
+                out=out[1024 * b : 1024 * b + 1024, :].rearrange("(q p e) d -> p q (e d)", p=P, e=2),
+                in_=o_of.pop(b)[:].rearrange("p q e d -> p q (e d)"),
             )
 
-        def block_at(st, lag, first=0):
-            if (st - lag) % 2 == 0 and first <= (st - lag) // 2 < NB:
-                return (st - lag) // 2
-            return None
-
-        squares_scalar(0)
-        squares_scalar(1)
+        for s in range(S8):
+            square(0, s)
         x_transpose(0)
-        norms(0)
-        norm_pieces(0)
+        norm_scaled(0)
+        for piece in range(4):
+            norm_piece(0, piece)
         x_transpose_out(0)
+        pieces_transpose(0)
+        pieces_out(0)
         norms_broadcast_on_chip(0)
+        for b in range(1, 4):
+            for s in range(S8):
+                square(b, s)
         for i in range(3):
-            ring_fill(i)
-        norm_rows_transpose(0)
-        norm_rows_out(0)
-        product_bank(0)
-        product_bank(1)
-        squares_scalar(2)
+            fill_n(i)
+        fill_v(0)
+        regroup_x(0)
+        quantise_x(0)
 
-        for st in range(NS + 5):
-            live = st < NS
-            if live:
-                exponentials_bank(2 * st)
-                exponentials_bank(2 * st + 1)
-            if live:
-                distances(st, 0)
-            b = block_at(st, 2)
-            if b is not None:
-                clamp_bank_unit(b)
-            if st == 0:
-                norms(1)
-                norm_pieces(1)
-            b = block_at(st, -4, 2)
-            if b is not None:
-                norms(b)
-                norm_pieces(b)
-            if st == 1:
-                quantise_x(0)
-            b = block_at(st, -1, 1)
-            if b is not None:
-                quantise_x(b)
-            b = block_at(st, 2)
-            if b is not None:
-                mirror_out(b, 0)
-                mirror_out(b, 1)
-            b = block_at(st, 3)
-            if b is not None:
-                store(b, 1)
-            b = block_at(st, 4)
-            if b is not None:
-                store(b, 0)
-            b = block_at(st, -1, 1)
-            if b is not None:
-                x_transpose_out(b)
-                norm_rows_out(b)
-            if live:
-                distances(st, 1)
-            if 0 <= st - 1 < NS:
-                regroup_clamp(st - 1)
-            if live:
-                distances(st, 2)
-                distances(st, 3)
-            b = norms_after(st)
-            if b is not None:
-                norms_broadcast(b)
-                ring_fill(ring.index(("h", b, 0)) + 3)
-            if live:
-                product_bank(2 * st + 2)
-                product_bank(2 * st + 3)
-            b = block_at(st, 1)
-            if b is not None:
-                mirror_transposes(b, 0)
-                mirror_transposes(b, 1)
-            b = block_at(st, -2, 1)
-            if b is not None:
-                x_transpose(b)
-                norm_rows_transpose(b)
-            if live:
-                exponentials(st)
-            if 0 <= st - 1 < NS:
-                quantise((st - 1) // 2, 1, (st - 1) % 2, grp_of.pop(st - 1))
-            b = block_at(st, 2)
-            if b is not None:
-                quantise(b, 0, 0, grp_of.pop(("a", b)))
-                quantise(b, 0, 1, mir_of.pop(b))
-                second_matmul(b, 1)
-            b = block_at(st, 3)
-            if b is not None:
-                second_matmul(b, 0)
-                w_q.pop(b)
-                w_s.pop(b)
-            b = block_at(st, -6, 3)
-            if b is not None:
-                squares_scalar(b)
-            if st == 0:
-                regroup_x(0)
-            b = block_at(st, -2, 1)
-            if b is not None:
-                regroup_x(b)
+        squares_in = {0: [4], 1: [5, 6]}
+        for st in range(2, NB):
+            squares_in[st] = [st + 5] if st + 5 < NB else []
+        norms_in = {0: 1, 3: 2, 7: 3, 11: 4}
+
+        for st in range(NB + 2):
+            b = st if st < NB else None
+            b1 = st - 1 if 0 <= st - 1 < NB else None
+            b2 = st - 2 if 0 <= st - 2 < NB else None
+            nx = st + 1 if st + 1 < NB else None
+            nk = norms_in.get(st)
+            for i in range(NN):
+                if b is not None:
+                    exp_n(NN * b + i)
+                    for sb in squares_in[st]:
+                        square(sb, i)
+                if i == 1 and nx is not None:
+                    x_transpose_out(nx)
+                if i == 1 and b2 is not None:
+                    scale_out(b2, 0)
+                if i == 3 and b is not None:
+                    exp_v(b, 0)
+                    exp_v(b, 1)
+                if i == 4 and b2 is not None:
+                    scale_out(b2, 1)
+                    store(b2)
+                if i == 6 and b is not None:
+                    exp_v(b, 2)
+                if i == 0:
+                    if nk is not None:
+                        norm_scaled(nk)
+                        norm_piece(nk, 0)
+                    if b is not None:
+                        distances(b, 0)
+                    if nk is not None:
+                        norm_piece(nk, 1)
+                    if b1 is not None:
+                        regroup(b1, 0, 0)
+                if i == 1:
+                    if nk is not None:
+                        norm_piece(nk, 2)
+                    if b is not None:
+                        fill_v(3 * b + 1)
+                        distances(b, 1)
+                    if nk is not None:
+                        norm_piece(nk, 3)
+                    if b1 is not None:
+                        mirror_out(b1, "A")
+                if i == 2:
+                    if b1 is not None:
+                        regroup(b1, 0, 1)
+                    if nk is not None:
+                        pieces_out(nk)
+                    if b1 is not None:
+                        quantise(b1, 0, 0)
+                if i == 3:
+                    if b is not None:
+                        fill_v(3 * b + 2)
+                        distances(b, 2)
+                    if nk is not None:
+                        norms_broadcast(nk)
+                    if b1 is not None:
+                        mirror_out(b1, "B0")
+                if i == 4 and b1 is not None:
+                    quantise(b1, 0, 1)
+                    mirror_out(b1, "B1")
+                if i == 5 and b1 is not None:
+                    regroup(b1, 1, 0)
+                    regroup(b1, 1, 1)
+                    mirror_out(b1, "C")
+                if i == 6:
+                    if nx is not None:
+                        regroup_x(nx)
+                    if b1 is not None:
+                        quantise(b1, 1, 0)
+                if i == 7:
+                    if b1 is not None:
+                        quantise(b1, 1, 1)
+                    if nx is not None:
+                        quantise_x(nx)
+                if b is not None:
+                    fill_n(NN * b + i + 3)
+                if i == 0 and nx is not None:
+                    x_transpose(nx)
+                if i == 0 and b1 is not None:
+                    mirror_transpose(b1, "B0")
+                if i == 1 and b1 is not None:
+                    mirror_transpose(b1, "B1")
+                if i == 1 and nk is not None:
+                    pieces_transpose(nk)
+                if i == 2 and nk is not None:
+                    norms_transpose(nk)
+                if i == 2 and b2 is not None:
+                    second_matmul(b2, 1)
+                    w_of.pop(b2)
+                if i == 3 and b1 is not None:
+                    mirror_transpose(b1, "C")
+                if i == 5 and b is not None:
+                    fill_v(3 * b + 3)
+                if i == 7:
+                    if b1 is not None:
+                        second_matmul(b1, 0)
+                        grp_of.pop(b1)
+                        pl_of.pop(b1)
+                    if b is not None:
+                        mirror_transpose(b, "A")

@@ -19,19 +19,10 @@ S8 = 8
 SCALE = 2.0 / 25.6
 FLOPS = 2 * 2 * 16 * 1024 * 1024 * 128
 
-N_BANKS = [
-    [(0, 0, 4)],
-    [(1, 0, 4)],
-    [(2, 4, 4)],
-    [(3, 4, 4)],
-    [(2, 2, 2), (3, 2, 2)],
-    [(4, 4, 4)],
-    [(5, 4, 4)],
-    [(7, 6, 2)],
-]
-V_BANKS = [(0, 4, 4), (1, 4, 4), (6, 6, 2)]
-NN = len(N_BANKS)
-BATCHES = [(0, 1), (1, 4), (4, 8), (8, 12), (12, 16)]
+N_BANKS = [(0, 0), (1, 0), (0, 4), (1, 4), (2, 4), (3, 4), (4, 4), (5, 4)]
+V_BANKS = [[(2, 2, 2), (3, 2, 2)], [(6, 6, 2), (7, 6, 2)], [(5, 4, 4)]]
+BATCHES = [(0, 1), (1, 2), (2, 4), (4, 8), (8, 12), (12, 16)]
+SLOTS = [(1, 0), (1, 1), (1, 2), (0, 0), (0, 1), (0, 2), (0, 3), (1, 3)]
 
 
 def tile_blockselfattention_kernel(tc, features, out):
@@ -48,11 +39,9 @@ def tile_blockselfattention_kernel(tc, features, out):
         gp = ctx.enter_context(tc.tile_pool(name="gp", bufs=2))
         wp = ctx.enter_context(tc.tile_pool(name="wp", bufs=2))
         op = ctx.enter_context(tc.tile_pool(name="op", bufs=2))
-        ps_n = ctx.enter_context(tc.psum_pool(name="ps_n", bufs=3))
+        ps_n = ctx.enter_context(tc.psum_pool(name="ps_n", bufs=4))
         ps_v = ctx.enter_context(tc.psum_pool(name="ps_v", bufs=1))
-        ps_t = ctx.enter_context(tc.psum_pool(name="ps_t", bufs=2))
-        ps_m = ctx.enter_context(tc.psum_pool(name="ps_m", bufs=1))
-        ps_o = ctx.enter_context(tc.psum_pool(name="ps_o", bufs=1))
+        ps_x = ctx.enter_context(tc.psum_pool(name="ps_x", bufs=3))
 
         x_sb = const.tile([P, NB * S8, D], BF16, name="x_sb")
         xv = features.rearrange("(q p e) d -> p q (e d)", p=P, e=2)
@@ -69,12 +58,15 @@ def tile_blockselfattention_kernel(tc, features, out):
         load(nc.sync, 16, 40)
         load(nc.sync, 40, 64)
 
+        warm = const.tile([P, 1], F32, name="warm")
+        nc.vector.memset(warm[:], 0.0)
+        nc.scalar.activation(out=warm[:], in_=warm[:], func=ACT.Exp)
+        sqc = const.tile([P, P], F32, name="sqc")
+        nc.vector.memset(sqc[:], 0.0)
         ident_b = const.tile([P, P], BF16, name="ident_b")
         make_identity(nc, ident_b[:])
         ident_f = const.tile([P, P], F32, name="ident_f")
         make_identity(nc, ident_f[:])
-        sqc = const.tile([P, P], F32, name="sqc")
-        nc.vector.memset(sqc[:], 0.0)
         hcol = const.tile([P, P], F32, name="hcol")
         bias = const.tile([P, P], F32, name="bias")
         pcs = []
@@ -132,7 +124,7 @@ def tile_blockselfattention_kernel(tc, features, out):
             )
 
         def x_transpose(b):
-            xt_ps = ps_m.tile([P, S8, P], BF16, name="xt_ps", tag="misc")
+            xt_ps = ps_x.tile([P, S8, P], BF16, name="xt_ps", tag="x")
             for s in range(S8):
                 nc.tensor.transpose(xt_ps[:, s, :], x_sb[:, S8 * b + s, :], ident_b[:])
             misc[("x", b)] = xt_ps
@@ -173,7 +165,7 @@ def tile_blockselfattention_kernel(tc, features, out):
                 )
 
         def pieces_transpose(k):
-            hp = ps_m.tile([P, P], BF16, name="hp", tag="misc")
+            hp = ps_x.tile([P, P], BF16, name="hp", tag="x")
             nc.tensor.transpose(hp[:], pcs[k][:], ident_b[:])
             misc[("hp", k)] = hp
 
@@ -183,7 +175,7 @@ def tile_blockselfattention_kernel(tc, features, out):
             h_t[k] = ht
 
         def norms_transpose(k):
-            sp = ps_m.tile([P, P], F32, name="sp", tag="misc")
+            sp = ps_x.tile([P, P], F32, name="sp", tag="x")
             nc.tensor.transpose(sp[:], sqc[:], ident_f[:])
             misc[("sp", k)] = sp
 
@@ -196,51 +188,52 @@ def tile_blockselfattention_kernel(tc, features, out):
                 out=out[base : base + S8 * (b1 - b0), :], in_=rows[S8 * b0 : S8 * b1, :]
             )
             for b in range(b0, b1):
-                first = base + S8 * (b - b0) + 4
-                hb = hbp.tile([P, 512], F32, name="hb")
+                first = base + S8 * (b - b0) + 2
+                hb = hbp.tile([P, 1024], F32, name="hb")
                 nc.sync.dma_start(
-                    out=hb[:],
-                    in_=out[first : first + 4, :].rearrange("a p -> (a p)").partition_broadcast(P),
+                    out=hb[:, 0:768],
+                    in_=out[first : first + 6, :].rearrange("a p -> (a p)").partition_broadcast(P),
                 )
                 h_b[b] = hb
 
         def norms_broadcast_on_chip(b):
             bank = ps_v.tile([P, 512], F32, name="sv")
-            for s in range(4):
-                col = S8 * b + 4 + s
+            for k, s in enumerate([2, 3, 6, 7]):
+                col = S8 * b + s
                 nc.tensor.transpose(
-                    bank[:, P * s : P * s + P], sqc[:, col : col + 1].to_broadcast([P, P]), ident_f[:]
+                    bank[:, P * k : P * k + P], sqc[:, col : col + 1].to_broadcast([P, P]), ident_f[:]
                 )
-            hb = hbp.tile([P, 512], F32, name="hb")
-            nc.vector.tensor_scalar_mul(out=hb[:], in0=bank[:], scalar1=-0.5)
+            hb = hbp.tile([P, 1024], F32, name="hb")
+            nc.vector.tensor_scalar_mul(
+                out=hb[:].rearrange("p (y z) -> p y z", y=2)[:, :, 0:256],
+                in0=bank[:].rearrange("p (y z) -> p y z", y=2),
+                scalar1=-0.5,
+            )
             h_b[b] = hb
+
+        n_flat = [(b, a, s0) for b in range(NB) for a, s0 in N_BANKS[: 8 - b % 2]]
+        n_first = [n_flat.index((b, 0, 0)) for b in range(NB)]
+        v_flat = [(b, k) for b in range(NB) for k in range(2 + b % 2)]
 
         def cols_of(b, s0, ns):
             return x_t[b][:, s0 : s0 + ns, :].rearrange("p s c -> p (s c)")
 
         def fill_n(i):
-            if i >= NN * NB:
+            if i >= len(n_flat):
                 return
-            b = i // NN
+            b, a, s0 = n_flat[i]
             bank = ps_n.tile([P, 512], F32, name="sn")
-            off = 0
-            for a, s0, ns in N_BANKS[i % NN]:
+            nc.tensor.matmul(
+                bank[:], lhsT=x_t[b][:, a, :], rhs=cols_of(b, s0, 4), start=True, stop=False
+            )
+            for k in range(4):
                 nc.tensor.matmul(
-                    bank[:, off : off + P * ns],
-                    lhsT=x_t[b][:, a, :],
-                    rhs=cols_of(b, s0, ns),
-                    start=True,
-                    stop=False,
+                    bank[:, P * k : P * k + P],
+                    lhsT=selc[:, S8 * (b % 4) + s0 + k, :],
+                    rhs=h_t[batch_of(b)][:],
+                    start=False,
+                    stop=(k == 3),
                 )
-                for k in range(ns):
-                    nc.tensor.matmul(
-                        bank[:, off + P * k : off + P * k + P],
-                        lhsT=selc[:, S8 * (b % 4) + s0 + k, :],
-                        rhs=h_t[batch_of(b)][:],
-                        start=False,
-                        stop=(k == ns - 1),
-                    )
-                off += P * ns
             n_of[i] = bank
 
         def planes(b):
@@ -249,127 +242,104 @@ def tile_blockselfattention_kernel(tc, features, out):
             return pl_of[b]
 
         def exp_n(i):
-            b = i // NN
-            bank = n_of.pop(i)
-            off = 0
-            for a, s0, ns in N_BANKS[i % NN]:
-                nc.scalar.activation(
-                    out=planes(b)[:, a, P * s0 : P * (s0 + ns)].rearrange(
-                        "p (q w e) -> p q w e", w=P, e=2
-                    ),
-                    in_=bank[:, off : off + P * ns].rearrange("p (q e w) -> p q w e", w=P, e=2),
-                    func=ACT.Exp,
-                    scale=SCALE,
-                    bias=bias[:, S8 * b + a : S8 * b + a + 1],
-                )
-                off += P * ns
-
-        def fill_v(i):
-            if i >= 3 * NB:
-                return
-            b = i // 3
-            a, s0, ns = V_BANKS[i % 3]
-            bank = ps_v.tile([P, 512], F32, name="sv")
-            nc.tensor.matmul(
-                bank[:, 0 : P * ns], lhsT=x_t[b][:, a, :], rhs=cols_of(b, s0, ns), start=True, stop=True
-            )
-            v_of[i] = bank
-
-        def distances(b, k):
-            a, s0, ns = V_BANKS[k]
-            if k == 0:
-                u_of[b] = up.tile([P, 3, 512], F32, name="u")
-            nc.vector.scalar_tensor_tensor(
-                out=u_of[b][:, k, 0 : P * ns],
-                in0=v_of.pop(3 * b + k)[:, 0 : P * ns],
-                scalar=hcol[:, S8 * b + a : S8 * b + a + 1],
-                in1=h_b[b][:, P * (s0 - 4) : P * (s0 - 4 + ns)],
-                op0=ALU.add,
-                op1=ALU.add,
-            )
-
-        def exp_v(b, k):
-            a, s0, ns = V_BANKS[k]
+            b, a, s0 = n_flat[i]
             nc.scalar.activation(
-                out=planes(b)[:, a, P * s0 : P * (s0 + ns)].rearrange("p (q w e) -> p q w e", w=P, e=2),
-                in_=u_of[b][:, k, 0 : P * ns].rearrange("p (q e w) -> p q w e", w=P, e=2),
+                out=planes(b)[:, a, P * s0 : P * s0 + 512].rearrange("p (q w e) -> p q w e", w=P, e=2),
+                in_=n_of.pop(i)[:].rearrange("p (q e w) -> p q w e", w=P, e=2),
                 func=ACT.Exp,
                 scale=SCALE,
+                bias=bias[:, S8 * b + a : S8 * b + a + 1],
             )
 
-        def groups(b):
-            if b not in grp_of:
-                g0 = gp.tile([P, 2, 4, P, 4], BF16, name="g0", align_bytes=64)
-                g1 = gp.tile([P, 2, 4, P, 4], BF16, name="g1", align_bytes=64)
-                grp_of[b] = (g0, g1)
-            return grp_of[b]
+        def fill_v(b, k):
+            if (b, k) not in v_flat:
+                return
+            bank = ps_v.tile([P, 512], F32, name="sv")
+            off = 0
+            for a, s0, ns in V_BANKS[k]:
+                nc.tensor.matmul(
+                    bank[:, off : off + P * ns],
+                    lhsT=x_t[b][:, a, :],
+                    rhs=cols_of(b, s0, ns),
+                    start=True,
+                    stop=True,
+                )
+                off += P * ns
+            v_of[(b, k)] = bank
 
-        def flat(b, g, e):
-            return groups(b)[g][:, e].rearrange("p q c t -> p (q c t)")
+        def distances(b, k):
+            bank = v_of.pop((b, k))
+            u = up.tile([P, 512], F32, name="u%d" % k)
+            off = 0
+            for a, s0, ns in V_BANKS[k]:
+                cs = slice(off, off + P * ns)
+                nc.vector.scalar_tensor_tensor(
+                    out=u[:, cs],
+                    in0=bank[:, cs],
+                    scalar=hcol[:, S8 * b + a : S8 * b + a + 1],
+                    in1=h_b[b][:, P * (s0 - 2) : P * (s0 - 2 + ns)],
+                    op0=ALU.add,
+                    op1=ALU.add,
+                )
+                off += P * ns
+            u_of[(b, k)] = u
+
+        def exp_v(b, k):
+            a, s0, ns = V_BANKS[k][0]
+            rows = len(V_BANKS[k])
+            o = planes(b)[:, a : a + rows, P * s0 : P * (s0 + ns)]
+            i = u_of.pop((b, k))[:].rearrange("p (r z) -> p r z", r=rows)
+            if rows == 1:
+                o = o[:, 0].rearrange("p (q w e) -> p q w e", w=P, e=2)
+                i = i[:, 0].rearrange("p (q e w) -> p q w e", w=P, e=2)
+            else:
+                o = o.rearrange("p r (w e) -> p r w e", e=2)
+                i = i.rearrange("p r (e w) -> p r w e", e=2)
+            nc.scalar.activation(out=o, in_=i, func=ACT.Exp, scale=SCALE)
+
+        def flat(b, e):
+            if b not in grp_of:
+                grp_of[b] = gp.tile([P, 2, 8 * 512], BF16, name="grp", align_bytes=64)
+            return grp_of[b][:, e]
 
         def regroup(b, g, e):
-            q0 = 1 if g == 0 else 3
+            q0, s0, s1 = (1, 4, 7) if g == 0 else (3, 7, 8)
             nc.vector.tensor_scalar_min(
-                out=flat(b, g, e)[:, 512 * q0 : 2048].rearrange("p (k i t) -> p k t i", i=4, t=4),
+                out=flat(b, e)[:, 512 * s0 : 512 * s1].rearrange("p (k i t) -> p k t i", i=4, t=4),
                 in0=pl_of[b][:, 4 * g : 4 * g + 4, 256 * q0 : 1024].rearrange(
                     "p t (k i x) -> p x k t i", i=4, x=2
                 )[:, e],
                 scalar1=1.0,
             )
 
-        def mirror_transpose(b, name):
-            bank = ps_t.tile([P, 2, 2, P], F32, name="tb")
-            if name == "A":
-                units = [(0, 0), (1, 0)]
-                half = 0
-            elif name == "B0":
-                units = [(0, 0), (2, 0)]
-                half = 1
-            elif name == "B1":
-                units = [(1, 0), (3, 0)]
-                half = 1
-            else:
-                units = [(4, 0), (5, 0)]
-                half = 1
+        def mirror_transpose(b, e, h):
+            bank = ps_x.tile([P, 2, 2, P], F32, name="tb", tag="x")
             for k in range(2):
-                a = units[k][0]
+                g, q = SLOTS[2 * h + k]
                 for u in range(2):
-                    c0 = 512 * half + 256 * u
+                    c0 = 512 * g + 256 * u
                     nc.tensor.transpose(
-                        bank[:, u, k, :], pl_of[b][:, a, c0 : c0 + 256].bitcast(F32), ident_f[:]
+                        bank[:, u, k, :], pl_of[b][:, 2 * q + e, c0 : c0 + 256].bitcast(F32), ident_f[:]
                     )
-            t_of[(b, name)] = bank
+            t_of[(b, e, h)] = bank
 
-        def mirror_out(b, name):
-            bank = t_of.pop((b, name))[:].bitcast(BF16)
-            if name in ("B0", "B1"):
-                e = 0 if name == "B0" else 1
-                nc.vector.tensor_scalar_min(
-                    out=flat(b, 1, e)[:, 0:1024].rearrange("p (r u x) -> p r u x", u=2, x=2),
-                    in0=bank.rearrange("p u k (r x) -> p (k r) u x", x=2),
-                    scalar1=1.0,
-                )
-                return
-            g, q = (0, 0) if name == "A" else (1, 2)
-            for e in range(2):
-                nc.vector.tensor_scalar_min(
-                    out=flat(b, g, e)[:, 512 * q : 512 * q + 512].rearrange(
-                        "p (r u x) -> p r u x", u=2, x=2
-                    ),
-                    in0=bank[:, :, e].rearrange("p u (r x) -> p r u x", x=2),
-                    scalar1=1.0,
-                )
+        def mirror_out(b, e, h):
+            bank = t_of.pop((b, e, h))[:].bitcast(BF16)
+            nc.vector.tensor_scalar_min(
+                out=flat(b, e)[:, 1024 * h : 1024 * h + 1024].rearrange(
+                    "p (r u x) -> p r u x", u=2, x=2
+                ),
+                in0=bank.rearrange("p u k (r x) -> p (k r) u x", x=2),
+                scalar1=1.0,
+            )
 
-        def quantise(b, g, e):
+        def quantise(b, e):
             if b not in w_of:
                 wq = wp.tile([P, 2, 1024], U32, name="wq", align_bytes=64)
                 ws = wp.tile([P, 2, 1024], U8, name="ws", align_bytes=64)
                 w_of[b] = (wq, ws)
             wq, ws = w_of[b]
-            cols = slice(512 * e, 512 * e + 512)
-            nc.vector.quantize_mx(
-                out=wq[:, g, cols].bitcast(FP8X4), scales=ws[:, g, cols], in_=flat(b, g, e)
-            )
+            nc.vector.quantize_mx(out=wq[:, e].bitcast(FP8X4), scales=ws[:, e], in_=flat(b, e))
 
         def regroup_x(b):
             xg = xgp.tile([P, 2, D, 4], BF16, name="xg", align_bytes=64)
@@ -388,14 +358,14 @@ def tile_blockselfattention_kernel(tc, features, out):
 
         def second_matmul(b, e):
             wq, ws = w_of[b]
-            acc = ps_o.tile([P, 4, D], F32, name="acc")
+            acc = ps_x.tile([P, 4, D], F32, name="acc", tag="x")
             for q in range(4):
-                mc = slice(512 * e + P * q, 512 * e + P * q + P)
                 for g in range(2):
+                    s = SLOTS.index((g, q))
                     nc.tensor.matmul_mx(
                         out=acc[:, q, :],
-                        lhsT=wq[:, g, mc].bitcast(FP8X4),
-                        lhsT_scale=ws[:, g, mc],
+                        lhsT=wq[:, e, P * s : P * s + P].bitcast(FP8X4),
+                        lhsT_scale=ws[:, e, P * s : P * s + P],
                         rhs=xq[:, b, P * g : P * g + P].bitcast(FP8X4),
                         rhs_scale=xs[:, b, P * g : P * g + P],
                         start=(g == 0),
@@ -419,26 +389,25 @@ def tile_blockselfattention_kernel(tc, features, out):
         for s in range(S8):
             square(0, s)
         x_transpose(0)
-        norm_scaled(0)
         for piece in range(4):
             norm_piece(0, piece)
         x_transpose_out(0)
         pieces_transpose(0)
+        norm_scaled(0)
         pieces_out(0)
         norms_broadcast_on_chip(0)
-        for b in range(1, 4):
-            for s in range(S8):
-                square(b, s)
-        for i in range(3):
+        for s in range(S8):
+            square(1, s)
+        for i in range(4):
             fill_n(i)
-        fill_v(0)
+        fill_v(0, 0)
         regroup_x(0)
         quantise_x(0)
 
-        squares_in = {0: [4], 1: [5, 6]}
-        for st in range(2, NB):
+        squares_in = {0: [2, 3], 1: [4, 5], 2: [6, 7]}
+        for st in range(3, NB):
             squares_in[st] = [st + 5] if st + 5 < NB else []
-        norms_in = {0: 1, 3: 2, 7: 3, 11: 4}
+        norms_in = {0: 1, 1: 2, 3: 3, 7: 4, 11: 5}
 
         for st in range(NB + 2):
             b = st if st < NB else None
@@ -446,98 +415,104 @@ def tile_blockselfattention_kernel(tc, features, out):
             b2 = st - 2 if 0 <= st - 2 < NB else None
             nx = st + 1 if st + 1 < NB else None
             nk = norms_in.get(st)
-            for i in range(NN):
+            for i in range(8):
                 if b is not None:
-                    exp_n(NN * b + i)
+                    if i < 8 - b % 2:
+                        exp_n(n_first[b] + i)
+                    else:
+                        exp_v(b, 2)
                     for sb in squares_in[st]:
                         square(sb, i)
-                if i == 1 and nx is not None:
-                    x_transpose_out(nx)
-                if i == 1 and b2 is not None:
+                    if i == 2:
+                        exp_v(b, 0)
+                    if i == 5:
+                        exp_v(b, 1)
+                if i == 0 and b2 is not None:
                     scale_out(b2, 0)
-                if i == 3 and b is not None:
-                    exp_v(b, 0)
-                    exp_v(b, 1)
+                if i == 3 and nx is not None:
+                    x_transpose_out(nx)
                 if i == 4 and b2 is not None:
                     scale_out(b2, 1)
                     store(b2)
-                if i == 6 and b is not None:
-                    exp_v(b, 2)
                 if i == 0:
-                    if nk is not None:
-                        norm_scaled(nk)
-                        norm_piece(nk, 0)
                     if b is not None:
                         distances(b, 0)
+                    if b1 is not None:
+                        regroup(b1, 0, 0)
+                    if nk is not None:
+                        norm_piece(nk, 0)
+                if i == 1:
+                    if b1 is not None:
+                        mirror_out(b1, 0, 0)
                     if nk is not None:
                         norm_piece(nk, 1)
                     if b1 is not None:
-                        regroup(b1, 0, 0)
-                if i == 1:
+                        regroup(b1, 1, 0)
                     if nk is not None:
                         norm_piece(nk, 2)
-                    if b is not None:
-                        fill_v(3 * b + 1)
-                        distances(b, 1)
-                    if nk is not None:
+                        norm_scaled(nk)
                         norm_piece(nk, 3)
-                    if b1 is not None:
-                        mirror_out(b1, "A")
                 if i == 2:
-                    if b1 is not None:
-                        regroup(b1, 0, 1)
-                    if nk is not None:
-                        pieces_out(nk)
-                    if b1 is not None:
-                        quantise(b1, 0, 0)
-                if i == 3:
-                    if b is not None:
-                        fill_v(3 * b + 2)
-                        distances(b, 2)
                     if nk is not None:
                         norms_broadcast(nk)
                     if b1 is not None:
-                        mirror_out(b1, "B0")
-                if i == 4 and b1 is not None:
-                    quantise(b1, 0, 1)
-                    mirror_out(b1, "B1")
+                        mirror_out(b1, 0, 1)
+                    if b is not None:
+                        distances(b, 1)
+                if i == 3:
+                    if nk is not None:
+                        pieces_out(nk)
+                    if b1 is not None:
+                        quantise(b1, 0)
+                if i == 4:
+                    if b is not None and b % 2 == 1:
+                        distances(b, 2)
+                    if b1 is not None:
+                        regroup(b1, 0, 1)
                 if i == 5 and b1 is not None:
-                    regroup(b1, 1, 0)
+                    mirror_out(b1, 1, 0)
                     regroup(b1, 1, 1)
-                    mirror_out(b1, "C")
                 if i == 6:
+                    if b1 is not None:
+                        mirror_out(b1, 1, 1)
                     if nx is not None:
                         regroup_x(nx)
-                    if b1 is not None:
-                        quantise(b1, 1, 0)
                 if i == 7:
                     if b1 is not None:
-                        quantise(b1, 1, 1)
+                        quantise(b1, 1)
                     if nx is not None:
                         quantise_x(nx)
                 if b is not None:
-                    fill_n(NN * b + i + 3)
-                if i == 0 and nx is not None:
-                    x_transpose(nx)
+                    if i < 8 - b % 2:
+                        fill_n(n_first[b] + i + 4)
+                    if i == 1:
+                        fill_v(b, 1)
+                    if i == 3:
+                        fill_v(b, 2)
+                    if i == 5:
+                        fill_v(b + 1, 0)
                 if i == 0 and b1 is not None:
-                    mirror_transpose(b1, "B0")
-                if i == 1 and b1 is not None:
-                    mirror_transpose(b1, "B1")
-                if i == 1 and nk is not None:
-                    pieces_transpose(nk)
-                if i == 2 and nk is not None:
-                    norms_transpose(nk)
-                if i == 2 and b2 is not None:
-                    second_matmul(b2, 1)
-                    w_of.pop(b2)
+                    mirror_transpose(b1, 0, 1)
+                if i == 1:
+                    if nk is not None:
+                        norms_transpose(nk)
+                    if nx is not None:
+                        x_transpose(nx)
+                if i == 2:
+                    if nk is not None:
+                        pieces_transpose(nk)
+                    if b2 is not None:
+                        second_matmul(b2, 1)
+                        w_of.pop(b2)
                 if i == 3 and b1 is not None:
-                    mirror_transpose(b1, "C")
-                if i == 5 and b is not None:
-                    fill_v(3 * b + 3)
+                    mirror_transpose(b1, 1, 0)
+                if i == 4 and b1 is not None:
+                    mirror_transpose(b1, 1, 1)
+                if i == 6 and b1 is not None:
+                    second_matmul(b1, 0)
                 if i == 7:
                     if b1 is not None:
-                        second_matmul(b1, 0)
                         grp_of.pop(b1)
                         pl_of.pop(b1)
                     if b is not None:
-                        mirror_transpose(b, "A")
+                        mirror_transpose(b, 0, 0)

@@ -19,7 +19,7 @@ S8 = 8
 SCALE = 2.0 / 25.6
 FLOPS = 2 * 2 * 16 * 1024 * 1024 * 128
 
-N_BANKS = [(0, 0), (1, 0), (0, 4), (1, 4), (2, 4), (3, 4), (4, 4), (5, 4)]
+N_BANKS = [(0, 0), (0, 4), (2, 4), (4, 4), (1, 4), (3, 4), (1, 0), (5, 4)]
 V_BANKS = [[(2, 2, 2), (3, 2, 2)], [(6, 6, 2), (7, 6, 2)], [(5, 4, 4)]]
 BATCHES = [(0, 1), (1, 2), (2, 4), (4, 8), (8, 12), (12, 16)]
 SLOTS = [(1, 0), (1, 1), (1, 2), (0, 0), (0, 1), (0, 2), (0, 3), (1, 3)]
@@ -31,7 +31,7 @@ def tile_blockselfattention_kernel(tc, features, out):
         ctx.enter_context(tc.manual_schedule())
         const = ctx.enter_context(tc.tile_pool(name="const", bufs=1))
         work = ctx.enter_context(tc.tile_pool(name="work", bufs=2))
-        xgp = ctx.enter_context(tc.tile_pool(name="xgp", bufs=2))
+        xgp = ctx.enter_context(tc.tile_pool(name="xgp", bufs=1))
         xtp = ctx.enter_context(tc.tile_pool(name="xtp", bufs=3))
         hbp = ctx.enter_context(tc.tile_pool(name="hbp", bufs=6))
         up = ctx.enter_context(tc.tile_pool(name="up", bufs=2))
@@ -39,9 +39,9 @@ def tile_blockselfattention_kernel(tc, features, out):
         gp = ctx.enter_context(tc.tile_pool(name="gp", bufs=2))
         wp = ctx.enter_context(tc.tile_pool(name="wp", bufs=2))
         op = ctx.enter_context(tc.tile_pool(name="op", bufs=2))
-        ps_n = ctx.enter_context(tc.psum_pool(name="ps_n", bufs=4))
+        ps_n = ctx.enter_context(tc.psum_pool(name="ps_n", bufs=3))
         ps_v = ctx.enter_context(tc.psum_pool(name="ps_v", bufs=1))
-        ps_x = ctx.enter_context(tc.psum_pool(name="ps_x", bufs=3))
+        ps_x = ctx.enter_context(tc.psum_pool(name="ps_x", bufs=4))
 
         x_sb = const.tile([P, NB * S8, D], BF16, name="x_sb")
         xv = features.rearrange("(q p e) d -> p q (e d)", p=P, e=2)
@@ -61,7 +61,7 @@ def tile_blockselfattention_kernel(tc, features, out):
         warm = const.tile([P, 1], F32, name="warm")
         nc.vector.memset(warm[:], 0.0)
         nc.scalar.activation(out=warm[:], in_=warm[:], func=ACT.Exp)
-        sqc = const.tile([P, P], F32, name="sqc")
+        sqc = const.tile([P, len(BATCHES), P], F32, name="sqc")
         nc.vector.memset(sqc[:], 0.0)
         ident_b = const.tile([P, P], BF16, name="ident_b")
         make_identity(nc, ident_b[:])
@@ -69,11 +69,8 @@ def tile_blockselfattention_kernel(tc, features, out):
         make_identity(nc, ident_f[:])
         hcol = const.tile([P, P], F32, name="hcol")
         bias = const.tile([P, P], F32, name="bias")
-        pcs = []
-        for k in range(len(BATCHES)):
-            pc = const.tile([P, P], BF16, name="pc%d" % k)
-            nc.vector.memset(pc[:], 0.0)
-            pcs.append(pc)
+        pcs = const.tile([P, len(BATCHES), P], BF16, name="pcs")
+        nc.vector.memset(pcs[:], 0.0)
         sel = const.tile([P, 32], F32, name="sel")
         nc.vector.tensor_reduce(
             out=sel[:],
@@ -114,13 +111,18 @@ def tile_blockselfattention_kernel(tc, features, out):
         def batch_of(b):
             return [k for k in range(len(BATCHES)) if BATCHES[k][0] <= b < BATCHES[k][1]][0]
 
+        def norm_col(b, s):
+            k = batch_of(b)
+            col = S8 * (b - BATCHES[k][0]) + s
+            return sqc[:, k, col : col + 1]
+
         def square(b, s):
             junk = work.tile([P, D], BF16, name="junk")
             nc.scalar.activation(
                 out=junk[:],
                 in_=x_sb[:, S8 * b + s, :],
                 func=ACT.Square,
-                accum_out=sqc[:, S8 * b + s : S8 * b + s + 1],
+                accum_out=norm_col(b, s),
             )
 
         def x_transpose(b):
@@ -138,23 +140,26 @@ def tile_blockselfattention_kernel(tc, features, out):
             b0, b1 = BATCHES[k]
             return slice(S8 * b0, S8 * b1)
 
+        def squares_of(k):
+            b0, b1 = BATCHES[k]
+            return sqc[:, k, 0 : S8 * (b1 - b0)]
+
         def norm_scaled(k):
             cs = norm_cols(k)
-            nc.vector.tensor_scalar_mul(out=bias[:, cs], in0=sqc[:, cs], scalar1=-0.5 * SCALE)
-            nc.vector.tensor_scalar_mul(out=hcol[:, cs], in0=sqc[:, cs], scalar1=-0.5)
+            nc.vector.tensor_scalar_mul(out=bias[:, cs], in0=squares_of(k), scalar1=-0.5 * SCALE)
+            nc.vector.tensor_scalar_mul(out=hcol[:, cs], in0=squares_of(k), scalar1=-0.5)
 
         def norm_piece(k, piece):
             b0, b1 = BATCHES[k]
-            cs = norm_cols(k)
             n = S8 * (b1 - b0)
             j0 = S8 * (b0 % 4)
-            pcv = pcs[k][:, 0:96].rearrange("p (j k) -> p j k", k=3)[:, j0 : j0 + n]
+            pcv = pcs[:, k, 0:96].rearrange("p (j k) -> p j k", k=3)[:, j0 : j0 + n]
             if piece == 0:
-                nc.vector.tensor_copy(out=pcv[:, :, 0], in_=sqc[:, cs])
+                nc.vector.tensor_copy(out=pcv[:, :, 0], in_=squares_of(k))
             elif piece == 1:
                 r1 = work.tile([P, 32], F32, name="r1")
                 nc.vector.tensor_tensor(
-                    out=r1[:, 0:n], in0=sqc[:, cs], in1=pcv[:, :, 0], op=ALU.subtract
+                    out=r1[:, 0:n], in0=squares_of(k), in1=pcv[:, :, 0], op=ALU.subtract
                 )
                 misc[("r1", k)] = r1
             elif piece == 2:
@@ -166,7 +171,7 @@ def tile_blockselfattention_kernel(tc, features, out):
 
         def pieces_transpose(k):
             hp = ps_x.tile([P, P], BF16, name="hp", tag="x")
-            nc.tensor.transpose(hp[:], pcs[k][:], ident_b[:])
+            nc.tensor.transpose(hp[:], pcs[:, k, :], ident_b[:])
             misc[("hp", k)] = hp
 
         def pieces_out(k):
@@ -176,7 +181,7 @@ def tile_blockselfattention_kernel(tc, features, out):
 
         def norms_transpose(k):
             sp = ps_x.tile([P, P], F32, name="sp", tag="x")
-            nc.tensor.transpose(sp[:], sqc[:], ident_f[:])
+            nc.tensor.transpose(sp[:], sqc[:, k, :], ident_f[:])
             misc[("sp", k)] = sp
 
         def norms_broadcast(k):
@@ -185,7 +190,7 @@ def tile_blockselfattention_kernel(tc, features, out):
             nc.vector.tensor_scalar_mul(out=rows[:], in0=misc.pop(("sp", k))[:], scalar1=-0.5)
             base = 1024 * (b1 - 1)
             nc.sync.dma_start(
-                out=out[base : base + S8 * (b1 - b0), :], in_=rows[S8 * b0 : S8 * b1, :]
+                out=out[base : base + S8 * (b1 - b0), :], in_=rows[0 : S8 * (b1 - b0), :]
             )
             for b in range(b0, b1):
                 first = base + S8 * (b - b0) + 2
@@ -196,17 +201,19 @@ def tile_blockselfattention_kernel(tc, features, out):
                 )
                 h_b[b] = hb
 
-        def norms_broadcast_on_chip(b):
+        def norms_spread(b):
             bank = ps_v.tile([P, 512], F32, name="sv")
             for k, s in enumerate([2, 3, 6, 7]):
-                col = S8 * b + s
                 nc.tensor.transpose(
-                    bank[:, P * k : P * k + P], sqc[:, col : col + 1].to_broadcast([P, P]), ident_f[:]
+                    bank[:, P * k : P * k + P], norm_col(b, s).to_broadcast([P, P]), ident_f[:]
                 )
+            misc[("hb", b)] = bank
+
+        def norms_spread_out(b):
             hb = hbp.tile([P, 1024], F32, name="hb")
             nc.vector.tensor_scalar_mul(
                 out=hb[:].rearrange("p (y z) -> p y z", y=2)[:, :, 0:256],
-                in0=bank[:].rearrange("p (y z) -> p y z", y=2),
+                in0=misc.pop(("hb", b))[:].rearrange("p (y z) -> p y z", y=2),
                 scalar1=-0.5,
             )
             h_b[b] = hb
@@ -343,9 +350,13 @@ def tile_blockselfattention_kernel(tc, features, out):
 
         def regroup_x(b):
             xg = xgp.tile([P, 2, D, 4], BF16, name="xg", align_bytes=64)
-            nc.vector.tensor_copy(
+            nc.gpsimd.tensor_scalar(
                 out=xg[:],
-                in_=x_sb[:, S8 * b : S8 * b + S8, :].rearrange("p (g t) d -> p g d t", g=2),
+                in0=x_sb[:, S8 * b : S8 * b + S8, :].rearrange("p (g t) d -> p g d t", g=2),
+                scalar1=1.0,
+                scalar2=0.0,
+                op0=ALU.mult,
+                op1=ALU.add,
             )
             xg_of[b] = xg
 
@@ -389,26 +400,30 @@ def tile_blockselfattention_kernel(tc, features, out):
         for s in range(S8):
             square(0, s)
         x_transpose(0)
+        regroup_x(0)
         for piece in range(4):
             norm_piece(0, piece)
         x_transpose_out(0)
+        norms_spread(0)
         pieces_transpose(0)
-        norm_scaled(0)
         pieces_out(0)
-        norms_broadcast_on_chip(0)
+        norm_scaled(0)
+        norms_spread_out(0)
         for s in range(S8):
             square(1, s)
-        for i in range(4):
+        for i in range(2):
             fill_n(i)
         fill_v(0, 0)
-        regroup_x(0)
+        norms_transpose(1)
+        for i in range(2, 3):
+            fill_n(i)
         quantise_x(0)
+        regroup_x(1)
 
         squares_in = {0: [2, 3], 1: [4, 5], 2: [6, 7]}
         for st in range(3, NB):
             squares_in[st] = [st + 5] if st + 5 < NB else []
         norms_in = {0: 1, 1: 2, 3: 3, 7: 4, 11: 5}
-
         for st in range(NB + 2):
             b = st if st < NB else None
             b1 = st - 1 if 0 <= st - 1 < NB else None
@@ -423,17 +438,17 @@ def tile_blockselfattention_kernel(tc, features, out):
                         exp_v(b, 2)
                     for sb in squares_in[st]:
                         square(sb, i)
-                    if i == 2:
+                    if i == 3:
                         exp_v(b, 0)
                     if i == 5:
                         exp_v(b, 1)
-                if i == 0 and b2 is not None:
-                    scale_out(b2, 0)
-                if i == 3 and nx is not None:
-                    x_transpose_out(nx)
-                if i == 4 and b2 is not None:
+                if i == 1 and b2 is not None:
                     scale_out(b2, 1)
                     store(b2)
+                if i == 3 and nx is not None:
+                    x_transpose_out(nx)
+                if i == 6 and b1 is not None:
+                    scale_out(b1, 0)
                 if i == 0:
                     if b is not None:
                         distances(b, 0)
@@ -443,76 +458,71 @@ def tile_blockselfattention_kernel(tc, features, out):
                         norm_piece(nk, 0)
                 if i == 1:
                     if b1 is not None:
-                        mirror_out(b1, 0, 0)
-                    if nk is not None:
-                        norm_piece(nk, 1)
-                    if b1 is not None:
                         regroup(b1, 1, 0)
                     if nk is not None:
+                        norm_piece(nk, 1)
+                    if nx is not None:
+                        quantise_x(nx)
+                        if nx + 1 < NB:
+                            regroup_x(nx + 1)
+                    if b1 is not None:
+                        mirror_out(b1, 1, 0)
+                    if nk is not None:
+                        norms_broadcast(nk)
                         norm_piece(nk, 2)
                         norm_scaled(nk)
                         norm_piece(nk, 3)
                 if i == 2:
-                    if nk is not None:
-                        norms_broadcast(nk)
-                    if b1 is not None:
-                        mirror_out(b1, 0, 1)
                     if b is not None:
                         distances(b, 1)
+                    if b1 is not None:
+                        mirror_out(b1, 1, 1)
                 if i == 3:
+                    if b1 is not None:
+                        quantise(b1, 0)
                     if nk is not None:
                         pieces_out(nk)
                     if b1 is not None:
-                        quantise(b1, 0)
-                if i == 4:
-                    if b is not None and b % 2 == 1:
-                        distances(b, 2)
-                    if b1 is not None:
                         regroup(b1, 0, 1)
+                if i == 4:
+                    if b1 is not None:
+                        regroup(b1, 1, 1)
+                    if b is not None:
+                        if b % 2 == 1:
+                            distances(b, 2)
+                        mirror_out(b, 0, 0)
                 if i == 5 and b1 is not None:
-                    mirror_out(b1, 1, 0)
-                    regroup(b1, 1, 1)
-                if i == 6:
-                    if b1 is not None:
-                        mirror_out(b1, 1, 1)
-                    if nx is not None:
-                        regroup_x(nx)
-                if i == 7:
-                    if b1 is not None:
-                        quantise(b1, 1)
-                    if nx is not None:
-                        quantise_x(nx)
+                    quantise(b1, 1)
+                if i == 6 and b is not None:
+                    mirror_out(b, 0, 1)
                 if b is not None:
                     if i < 8 - b % 2:
-                        fill_n(n_first[b] + i + 4)
-                    if i == 1:
+                        fill_n(n_first[b] + i + 3)
+                    if i == 0:
                         fill_v(b, 1)
-                    if i == 3:
+                    if i == 2:
                         fill_v(b, 2)
                     if i == 5:
                         fill_v(b + 1, 0)
-                if i == 0 and b1 is not None:
-                    mirror_transpose(b1, 0, 1)
-                if i == 1:
-                    if nk is not None:
+                if i == 0:
+                    if nk is not None and nk > 1:
                         norms_transpose(nk)
-                    if nx is not None:
-                        x_transpose(nx)
-                if i == 2:
-                    if nk is not None:
-                        pieces_transpose(nk)
-                    if b2 is not None:
-                        second_matmul(b2, 1)
-                        w_of.pop(b2)
-                if i == 3 and b1 is not None:
-                    mirror_transpose(b1, 1, 0)
-                if i == 4 and b1 is not None:
+                if i == 0 and nx is not None:
+                    x_transpose(nx)
+                if i == 1 and b1 is not None:
                     mirror_transpose(b1, 1, 1)
-                if i == 6 and b1 is not None:
+                if i == 2 and nk is not None:
+                    pieces_transpose(nk)
+                if i == 3 and b is not None:
+                    mirror_transpose(b, 0, 0)
+                if i == 4 and b1 is not None:
                     second_matmul(b1, 0)
-                if i == 7:
-                    if b1 is not None:
-                        grp_of.pop(b1)
-                        pl_of.pop(b1)
-                    if b is not None:
-                        mirror_transpose(b, 0, 0)
+                if i == 5 and b is not None:
+                    mirror_transpose(b, 0, 1)
+                if i == 6 and b1 is not None:
+                    second_matmul(b1, 1)
+                    w_of.pop(b1)
+                    grp_of.pop(b1)
+                    pl_of.pop(b1)
+                if i == 7 and b is not None:
+                    mirror_transpose(b, 1, 0)

@@ -19,10 +19,13 @@ S8 = 8
 SCALE = 2.0 / 25.6
 FLOPS = 2 * 2 * 16 * 1024 * 1024 * 128
 
-N_BANKS = [(0, 0), (0, 4), (2, 4), (4, 4), (1, 4), (3, 4), (1, 0), (5, 4)]
-V_BANKS = [[(2, 2, 2), (3, 2, 2)], [(6, 6, 2), (7, 6, 2)], [(5, 4, 4)]]
-BATCHES = [(0, 1), (1, 2), (2, 4), (4, 8), (8, 12), (12, 16)]
-SLOTS = [(1, 0), (1, 1), (1, 2), (0, 0), (0, 1), (0, 2), (0, 3), (1, 3)]
+N_BANKS = [(0, 0), (1, 0), (0, 4), (1, 4), (2, 4), (3, 4), (4, 4), (5, 4)]
+V_BANKS = [[(2, 2, 2), (3, 3, 1)], [(6, 6, 2), (7, 7, 1)]]
+BATCHES = [(0, 1), (1, 2)] + [(b, b + 2) for b in range(2, 16, 2)]
+SLOTS = [
+    [(1, 0, 0), (1, 0, 1), (1, 1, 0), (1, 1, 1), (0, 0, 0), (0, 0, 1), (0, 1, 0), (0, 1, 1)],
+    [(1, 2, 0), (1, 2, 1), (1, 3, 0), (1, 3, 1), (0, 2, 0), (0, 3, 0), (0, 2, 1), (0, 3, 1)],
+]
 
 
 def tile_blockselfattention_kernel(tc, features, out):
@@ -125,6 +128,14 @@ def tile_blockselfattention_kernel(tc, features, out):
                 accum_out=norm_col(b, s),
             )
 
+        def square_on_vector(b, s):
+            junk = work.tile([P, D], BF16, name="junk_v")
+            x = x_sb[:, S8 * b + s, :]
+            nc.vector.scalar_tensor_tensor(
+                out=junk[:], in0=x, scalar=1.0, in1=x, op0=ALU.mult, op1=ALU.mult,
+                accum_out=norm_col(b, s),
+            )
+
         def x_transpose(b):
             xt_ps = ps_x.tile([P, S8, P], BF16, name="xt_ps", tag="x")
             for s in range(S8):
@@ -146,8 +157,10 @@ def tile_blockselfattention_kernel(tc, features, out):
 
         def norm_scaled(k):
             cs = norm_cols(k)
-            nc.vector.tensor_scalar_mul(out=bias[:, cs], in0=squares_of(k), scalar1=-0.5 * SCALE)
-            nc.vector.tensor_scalar_mul(out=hcol[:, cs], in0=squares_of(k), scalar1=-0.5)
+            nc.scalar.activation(
+                out=bias[:, cs], in_=squares_of(k), func=ACT.Copy, scale=-0.5 * SCALE
+            )
+            nc.scalar.activation(out=hcol[:, cs], in_=squares_of(k), func=ACT.Copy, scale=-0.5)
 
         def norm_piece(k, piece):
             b0, b1 = BATCHES[k]
@@ -176,7 +189,7 @@ def tile_blockselfattention_kernel(tc, features, out):
 
         def pieces_out(k):
             ht = const.tile([P, P], BF16, name="ht%d" % k)
-            nc.vector.tensor_copy(out=ht[:], in_=misc.pop(("hp", k))[:])
+            nc.scalar.copy(out=ht[:], in_=misc.pop(("hp", k))[:])
             h_t[k] = ht
 
         def norms_transpose(k):
@@ -187,7 +200,9 @@ def tile_blockselfattention_kernel(tc, features, out):
         def norms_broadcast(k):
             b0, b1 = BATCHES[k]
             rows = work.tile([P, P], F32, name="rows")
-            nc.vector.tensor_scalar_mul(out=rows[:], in0=misc.pop(("sp", k))[:], scalar1=-0.5)
+            nc.scalar.activation(
+                out=rows[:], in_=misc.pop(("sp", k))[:], func=ACT.Copy, scale=-0.5
+            )
             base = 1024 * (b1 - 1)
             nc.sync.dma_start(
                 out=out[base : base + S8 * (b1 - b0), :], in_=rows[0 : S8 * (b1 - b0), :]
@@ -218,9 +233,9 @@ def tile_blockselfattention_kernel(tc, features, out):
             )
             h_b[b] = hb
 
-        n_flat = [(b, a, s0) for b in range(NB) for a, s0 in N_BANKS[: 8 - b % 2]]
+        n_flat = [(b, a, s0) for b in range(NB) for a, s0 in N_BANKS]
         n_first = [n_flat.index((b, 0, 0)) for b in range(NB)]
-        v_flat = [(b, k) for b in range(NB) for k in range(2 + b % 2)]
+        v_flat = [(b, k) for b in range(NB) for k in range(2)]
 
         def cols_of(b, s0, ns):
             return x_t[b][:, s0 : s0 + ns, :].rearrange("p s c -> p (s c)")
@@ -276,7 +291,7 @@ def tile_blockselfattention_kernel(tc, features, out):
 
         def distances(b, k):
             bank = v_of.pop((b, k))
-            u = up.tile([P, 512], F32, name="u%d" % k)
+            u = up.tile([P, 384], F32, name="u%d" % k)
             off = 0
             for a, s0, ns in V_BANKS[k]:
                 cs = slice(off, off + P * ns)
@@ -292,115 +307,144 @@ def tile_blockselfattention_kernel(tc, features, out):
             u_of[(b, k)] = u
 
         def exp_v(b, k):
+            u = u_of.pop((b, k))
             a, s0, ns = V_BANKS[k][0]
-            rows = len(V_BANKS[k])
-            o = planes(b)[:, a : a + rows, P * s0 : P * (s0 + ns)]
-            i = u_of.pop((b, k))[:].rearrange("p (r z) -> p r z", r=rows)
-            if rows == 1:
-                o = o[:, 0].rearrange("p (q w e) -> p q w e", w=P, e=2)
-                i = i[:, 0].rearrange("p (q e w) -> p q w e", w=P, e=2)
-            else:
-                o = o.rearrange("p r (w e) -> p r w e", e=2)
-                i = i.rearrange("p r (e w) -> p r w e", e=2)
-            nc.scalar.activation(out=o, in_=i, func=ACT.Exp, scale=SCALE)
+            pl = planes(b)
+            cs = slice(P * s0, P * (s0 + 2))
+            nc.scalar.activation(
+                out=pl[:, a + 1, cs].rearrange("p (w e) -> p w e", e=2)[:, :, 1],
+                in_=u[:, 256:384],
+                func=ACT.Exp,
+                scale=SCALE,
+            )
+            nc.scalar.activation(
+                out=pl[:, a, cs].rearrange("p (w e) -> p w e", e=2),
+                in_=u[:, 0:256].rearrange("p (e w) -> p w e", e=2),
+                func=ACT.Exp,
+                scale=SCALE,
+            )
 
-        def flat(b, e):
+        def turn(b, k):
+            a, s0, ns = V_BANKS[k][0]
+            bank = ps_x.tile([P, P], BF16, name="turned", tag="x")
+            nc.tensor.transpose(
+                bank[:],
+                pl_of[b][:, a, P * s0 : P * (s0 + 2)].rearrange("p (w e) -> p w e", e=2)[:, :, 1],
+                ident_b[:],
+            )
+            misc[("turn", b, k)] = bank
+
+        def turn_out(b, k):
+            a, s0, ns = V_BANKS[k][0]
+            copy = nc.vector.tensor_copy if k == 0 else nc.scalar.copy
+            copy(
+                out=pl_of[b][:, a + 1, P * s0 : P * (s0 + 2)].rearrange("p (w e) -> p w e", e=2)[:, :, 0],
+                in_=misc.pop(("turn", b, k))[:],
+            )
+
+        def flat(b, h):
             if b not in grp_of:
                 grp_of[b] = gp.tile([P, 2, 8 * 512], BF16, name="grp", align_bytes=64)
-            return grp_of[b][:, e]
+            return grp_of[b][:, h]
 
-        def regroup(b, g, e):
-            q0, s0, s1 = (1, 4, 7) if g == 0 else (3, 7, 8)
+        def regroup(b, g, q, ns, e):
+            h = q // 2
+            s0 = SLOTS[h].index((g, q, e))
             nc.vector.tensor_scalar_min(
-                out=flat(b, e)[:, 512 * s0 : 512 * s1].rearrange("p (k i t) -> p k t i", i=4, t=4),
-                in0=pl_of[b][:, 4 * g : 4 * g + 4, 256 * q0 : 1024].rearrange(
+                out=flat(b, h)[:, 512 * s0 : 512 * (s0 + ns)].rearrange(
+                    "p (k i t) -> p k t i", i=4, t=4
+                ),
+                in0=pl_of[b][:, 4 * g : 4 * g + 4, 256 * q : 256 * (q + ns)].rearrange(
                     "p t (k i x) -> p x k t i", i=4, x=2
                 )[:, e],
                 scalar1=1.0,
             )
 
-        def mirror_transpose(b, e, h):
+        def mirror_transpose(b, g, q):
             bank = ps_x.tile([P, 2, 2, P], F32, name="tb", tag="x")
-            for k in range(2):
-                g, q = SLOTS[2 * h + k]
+            for e in range(2):
                 for u in range(2):
                     c0 = 512 * g + 256 * u
                     nc.tensor.transpose(
-                        bank[:, u, k, :], pl_of[b][:, 2 * q + e, c0 : c0 + 256].bitcast(F32), ident_f[:]
+                        bank[:, u, e, :], pl_of[b][:, 2 * q + e, c0 : c0 + 256].bitcast(F32), ident_f[:]
                     )
-            t_of[(b, e, h)] = bank
+            t_of[(b, g, q)] = bank
 
-        def mirror_out(b, e, h):
-            bank = t_of.pop((b, e, h))[:].bitcast(BF16)
+        def mirror_out(b, g, q):
+            bank = t_of.pop((b, g, q))[:].bitcast(BF16)
+            h = q // 2
+            s0 = SLOTS[h].index((g, q, 0))
             nc.vector.tensor_scalar_min(
-                out=flat(b, e)[:, 1024 * h : 1024 * h + 1024].rearrange(
+                out=flat(b, h)[:, 512 * s0 : 512 * s0 + 1024].rearrange(
                     "p (r u x) -> p r u x", u=2, x=2
                 ),
                 in0=bank.rearrange("p u k (r x) -> p (k r) u x", x=2),
                 scalar1=1.0,
             )
 
-        def quantise(b, e):
+        def quantise(b, h):
             if b not in w_of:
                 wq = wp.tile([P, 2, 1024], U32, name="wq", align_bytes=64)
                 ws = wp.tile([P, 2, 1024], U8, name="ws", align_bytes=64)
                 w_of[b] = (wq, ws)
             wq, ws = w_of[b]
-            nc.vector.quantize_mx(out=wq[:, e].bitcast(FP8X4), scales=ws[:, e], in_=flat(b, e))
+            nc.vector.quantize_mx(out=wq[:, h].bitcast(FP8X4), scales=ws[:, h], in_=flat(b, h))
 
-        def regroup_x(b):
-            xg = xgp.tile([P, 2, D, 4], BF16, name="xg", align_bytes=64)
+        def regroup_x(b, g):
+            xg = xgp.tile([P, D, 4], BF16, name="xg%d" % g, align_bytes=64)
             nc.gpsimd.tensor_scalar(
                 out=xg[:],
-                in0=x_sb[:, S8 * b : S8 * b + S8, :].rearrange("p (g t) d -> p g d t", g=2),
+                in0=x_sb[:, S8 * b + 4 * g : S8 * b + 4 * g + 4, :].rearrange("p t d -> p d t"),
                 scalar1=1.0,
                 scalar2=0.0,
                 op0=ALU.mult,
                 op1=ALU.add,
             )
-            xg_of[b] = xg
+            xg_of[(b, g)] = xg
 
-        def quantise_x(b):
+        def quantise_x(b, g):
             nc.vector.quantize_mx(
-                out=xq[:, b, :].bitcast(FP8X4),
-                scales=xs[:, b, :],
-                in_=xg_of.pop(b)[:].rearrange("p g d t -> p (g d t)"),
+                out=xq[:, b, P * g : P * g + P].bitcast(FP8X4),
+                scales=xs[:, b, P * g : P * g + P],
+                in_=xg_of.pop((b, g))[:].rearrange("p d t -> p (d t)"),
             )
 
-        def second_matmul(b, e):
+        def second_matmul(b, h):
             wq, ws = w_of[b]
             acc = ps_x.tile([P, 4, D], F32, name="acc", tag="x")
-            for q in range(4):
+            for j in range(4):
                 for g in range(2):
-                    s = SLOTS.index((g, q))
+                    s = SLOTS[h].index((g, 2 * h + j // 2, j % 2))
                     nc.tensor.matmul_mx(
-                        out=acc[:, q, :],
-                        lhsT=wq[:, e, P * s : P * s + P].bitcast(FP8X4),
-                        lhsT_scale=ws[:, e, P * s : P * s + P],
+                        out=acc[:, j, :],
+                        lhsT=wq[:, h, P * s : P * s + P].bitcast(FP8X4),
+                        lhsT_scale=ws[:, h, P * s : P * s + P],
                         rhs=xq[:, b, P * g : P * g + P].bitcast(FP8X4),
                         rhs_scale=xs[:, b, P * g : P * g + P],
                         start=(g == 0),
                         stop=(g == 1),
                     )
-            acc_of[(b, e)] = acc
+            acc_of[(b, h)] = acc
 
-        def scale_out(b, e):
-            if e == 0:
-                o_of[b] = op.tile([P, 4, 2, D], F32, name="osb")
+        def scale_out(b, h):
+            o = op.tile([P, 4, D], F32, name="osb%d" % h)
             nc.scalar.activation(
-                out=o_of[b][:, :, e, :], in_=acc_of.pop((b, e))[:], func=ACT.Copy, scale=1.0 / 1024.0
+                out=o[:], in_=acc_of.pop((b, h))[:], func=ACT.Copy, scale=1.0 / 1024.0
             )
-
-        def store(b):
+            base = 1024 * b + 512 * h
             nc.sync.dma_start(
-                out=out[1024 * b : 1024 * b + 1024, :].rearrange("(q p e) d -> p q (e d)", p=P, e=2),
-                in_=o_of.pop(b)[:].rearrange("p q e d -> p q (e d)"),
+                out=out[base : base + 512, :].rearrange("(q p e) d -> p q (e d)", p=P, e=2),
+                in_=o[:].rearrange("p (q e) d -> p q (e d)", e=2),
             )
 
         for s in range(S8):
-            square(0, s)
+            if s < 5:
+                square(0, s)
+            else:
+                square_on_vector(0, s)
         x_transpose(0)
-        regroup_x(0)
+        regroup_x(0, 0)
+        regroup_x(0, 1)
         for piece in range(4):
             norm_piece(0, piece)
         x_transpose_out(0)
@@ -410,119 +454,145 @@ def tile_blockselfattention_kernel(tc, features, out):
         norm_scaled(0)
         norms_spread_out(0)
         for s in range(S8):
-            square(1, s)
+            square_on_vector(1, s)
         for i in range(2):
             fill_n(i)
         fill_v(0, 0)
-        norms_transpose(1)
         for i in range(2, 3):
             fill_n(i)
-        quantise_x(0)
-        regroup_x(1)
+        norm_piece(1, 0)
+        distances(0, 0)
+        norm_piece(1, 1)
+        norms_transpose(1)
+        fill_v(0, 1)
+        for g in range(2):
+            quantise_x(0, g)
+            regroup_x(1, g)
+            norm_piece(1, 2 + g)
 
-        squares_in = {0: [2, 3], 1: [4, 5], 2: [6, 7]}
-        for st in range(3, NB):
-            squares_in[st] = [st + 5] if st + 5 < NB else []
-        norms_in = {0: 1, 1: 2, 3: 3, 7: 4, 11: 5}
+        squares_in = {0: [2, 3]}
+        for st in range(1, NB):
+            squares_in[st] = [st + 3] if st + 3 < NB else []
+        norms_in = {0: 1}
+        for k in range(2, len(BATCHES)):
+            norms_in[BATCHES[k][0] - 1] = k
+        n_slots = [0, 1, 2, 3, 5, 6, 8, 9]
         for st in range(NB + 2):
             b = st if st < NB else None
             b1 = st - 1 if 0 <= st - 1 < NB else None
             b2 = st - 2 if 0 <= st - 2 < NB else None
             nx = st + 1 if st + 1 < NB else None
             nk = norms_in.get(st)
-            for i in range(8):
+            nl = norms_in.get(st + 1)
+            for i in range(10):
                 if b is not None:
-                    if i < 8 - b % 2:
-                        exp_n(n_first[b] + i)
-                    else:
-                        exp_v(b, 2)
-                    for sb in squares_in[st]:
-                        square(sb, i)
-                    if i == 3:
+                    if i == 4:
                         exp_v(b, 0)
-                    if i == 5:
+                    elif i == 7:
                         exp_v(b, 1)
-                if i == 1 and b2 is not None:
-                    scale_out(b2, 1)
-                    store(b2)
-                if i == 3 and nx is not None:
-                    x_transpose_out(nx)
+                    else:
+                        exp_n(n_first[b] + n_slots.index(i))
+                    if i < 8:
+                        for sb in squares_in[st]:
+                            if st == 0 or i == 7:
+                                square_on_vector(sb, i)
+                            else:
+                                square(sb, i)
                 if i == 6 and b1 is not None:
                     scale_out(b1, 0)
+                if i == 0 and b2 is not None:
+                    scale_out(b2, 1)
+                if i == 4 and nx is not None:
+                    x_transpose_out(nx)
+                if i == 6 and b is not None:
+                    turn_out(b, 0)
+                if i == 9 and b is not None:
+                    turn_out(b, 1)
                 if i == 0:
-                    if b is not None:
-                        distances(b, 0)
                     if b1 is not None:
-                        regroup(b1, 0, 0)
-                    if nk is not None:
-                        norm_piece(nk, 0)
+                        regroup(b1, 0, 2, 2, 1)
+                    if nk is not None and st > 0:
+                        norm_piece(nk, 1)
                 if i == 1:
                     if b1 is not None:
-                        regroup(b1, 1, 0)
-                    if nk is not None:
-                        norm_piece(nk, 1)
-                    if nx is not None:
-                        quantise_x(nx)
-                        if nx + 1 < NB:
-                            regroup_x(nx + 1)
-                    if b1 is not None:
-                        mirror_out(b1, 1, 0)
-                    if nk is not None:
-                        norms_broadcast(nk)
+                        quantise(b1, 0)
+                    if nk is not None and st > 0:
                         norm_piece(nk, 2)
-                        norm_scaled(nk)
-                        norm_piece(nk, 3)
                 if i == 2:
+                    if nx is not None:
+                        quantise_x(nx, 0)
+                        if nx + 1 < NB:
+                            regroup_x(nx + 1, 0)
+                    if b1 is not None:
+                        mirror_out(b1, 1, 2)
                     if b is not None:
                         distances(b, 1)
-                    if b1 is not None:
-                        mirror_out(b1, 1, 1)
+                    if nk is not None and st > 0:
+                        norm_piece(nk, 3)
+                if st == 0 and i == 1:
+                    norms_broadcast(1)
+                    norm_scaled(1)
+                if i == 9 and nl is not None:
+                    norms_broadcast(nl)
+                    norm_scaled(nl)
                 if i == 3:
                     if b1 is not None:
-                        quantise(b1, 0)
-                    if nk is not None:
-                        pieces_out(nk)
-                    if b1 is not None:
-                        regroup(b1, 0, 1)
-                if i == 4:
-                    if b1 is not None:
-                        regroup(b1, 1, 1)
+                        regroup(b1, 1, 3, 1, 0)
+                        regroup(b1, 1, 3, 1, 1)
                     if b is not None:
-                        if b % 2 == 1:
-                            distances(b, 2)
                         mirror_out(b, 0, 0)
+                if i == 5 and nk is not None:
+                    pieces_out(nk)
                 if i == 5 and b1 is not None:
                     quantise(b1, 1)
                 if i == 6 and b is not None:
-                    mirror_out(b, 0, 1)
+                    mirror_out(b, 1, 0)
+                if i == 7 and b is not None:
+                    regroup(b, 0, 1, 1, 0)
+                    regroup(b, 0, 1, 1, 1)
+                if i == 8:
+                    if nx is not None:
+                        quantise_x(nx, 1)
+                        if nx + 1 < NB:
+                            regroup_x(nx + 1, 1)
+                    if b is not None:
+                        mirror_out(b, 1, 1)
+                    if nx is not None:
+                        distances(nx, 0)
+                if i == 9:
+                    if nl is not None:
+                        norm_piece(nl, 0)
+                    if b is not None:
+                        regroup(b, 0, 2, 2, 0)
                 if b is not None:
-                    if i < 8 - b % 2:
-                        fill_n(n_first[b] + i + 3)
-                    if i == 0:
-                        fill_v(b, 1)
-                    if i == 2:
-                        fill_v(b, 2)
+                    if i == 9:
+                        fill_v(b + 1, 1)
                     if i == 5:
                         fill_v(b + 1, 0)
-                if i == 0:
-                    if nk is not None and nk > 1:
-                        norms_transpose(nk)
-                if i == 0 and nx is not None:
-                    x_transpose(nx)
-                if i == 1 and b1 is not None:
-                    mirror_transpose(b1, 1, 1)
-                if i == 2 and nk is not None:
+                        turn(b, 0)
+                    if i == 8:
+                        turn(b, 1)
+                if i == 8 and nl is not None:
+                    norms_transpose(nl)
+                if i == 0 and b1 is not None:
+                    mirror_transpose(b1, 1, 2)
+                if i == 2:
+                    if nx is not None:
+                        x_transpose(nx)
+                    if b is not None:
+                        mirror_transpose(b, 0, 0)
+                if i == 4 and nk is not None:
                     pieces_transpose(nk)
-                if i == 3 and b is not None:
-                    mirror_transpose(b, 0, 0)
                 if i == 4 and b1 is not None:
                     second_matmul(b1, 0)
                 if i == 5 and b is not None:
-                    mirror_transpose(b, 0, 1)
-                if i == 6 and b1 is not None:
+                    mirror_transpose(b, 1, 0)
+                if i == 7 and b is not None:
+                    mirror_transpose(b, 1, 1)
+                if i == 8 and b1 is not None:
                     second_matmul(b1, 1)
                     w_of.pop(b1)
                     grp_of.pop(b1)
                     pl_of.pop(b1)
-                if i == 7 and b is not None:
-                    mirror_transpose(b, 1, 0)
+                if b is not None and i in n_slots:
+                    fill_n(n_first[b] + n_slots.index(i) + 3)

@@ -64,16 +64,15 @@ def tile_blockselfattention_kernel(tc, features, out):
         warm = const.tile([P, 1], F32, name="warm")
         nc.vector.memset(warm[:], 0.0)
         nc.scalar.activation(out=warm[:], in_=warm[:], func=ACT.Exp)
-        sqc = const.tile([P, len(BATCHES), P], F32, name="sqc")
-        nc.vector.memset(sqc[:], 0.0)
+        sqc = const.tile([P, P], F32, name="sqc")
         ident_b = const.tile([P, P], BF16, name="ident_b")
         make_identity(nc, ident_b[:])
         ident_f = const.tile([P, P], F32, name="ident_f")
         make_identity(nc, ident_f[:])
         hcol = const.tile([P, P], F32, name="hcol")
         bias = const.tile([P, P], F32, name="bias")
-        pcs = const.tile([P, len(BATCHES), P], BF16, name="pcs")
-        nc.vector.memset(pcs[:], 0.0)
+        pcs = const.tile([P, P], BF16, name="pcs")
+        token = const.tile([P, 4], U32, name="token")
         sel = const.tile([P, 32], F32, name="sel")
         nc.vector.tensor_reduce(
             out=sel[:],
@@ -82,16 +81,19 @@ def tile_blockselfattention_kernel(tc, features, out):
             op=ALU.add,
         )
         selc = const.tile([P, 32, P], BF16, name="selc")
-        nc.vector.tensor_scalar_mul(
-            out=selc[:, 0:8, :], in0=sel[:, 0:8].unsqueeze(2).to_broadcast([P, 8, P]), scalar1=-0.5
-        )
-        nc.gpsimd.tensor_scalar(
-            out=selc[:, 8:32, :],
-            in0=sel[:, 8:32].unsqueeze(2).to_broadcast([P, 24, P]),
-            scalar1=-0.5,
-            scalar2=0.0,
-            op0=ALU.mult,
-            op1=ALU.add,
+        nc.vector.memset(sqc[:], 0.0)
+        nc.vector.memset(pcs[:], 0.0)
+        for j in (0, 16, 24):
+            nc.vector.tensor_scalar_mul(
+                out=selc[:, j : j + 8, :],
+                in0=sel[:, j : j + 8].unsqueeze(2).to_broadcast([P, 8, P]),
+                scalar1=-0.5,
+            )
+        nc.scalar.activation(
+            out=selc[:, 8:16, :],
+            in_=sel[:, 8:16].unsqueeze(2).to_broadcast([P, 8, P]),
+            func=ACT.Copy,
+            scale=-0.5,
         )
         xq = const.tile([P, NB, 256], U32, name="xq", align_bytes=64)
         xs = const.tile([P, NB, 256], U8, name="xs", align_bytes=64)
@@ -115,9 +117,7 @@ def tile_blockselfattention_kernel(tc, features, out):
             return [k for k in range(len(BATCHES)) if BATCHES[k][0] <= b < BATCHES[k][1]][0]
 
         def norm_col(b, s):
-            k = batch_of(b)
-            col = S8 * (b - BATCHES[k][0]) + s
-            return sqc[:, k, col : col + 1]
+            return sqc[:, S8 * b + s : S8 * b + s + 1]
 
         def square(b, s):
             junk = work.tile([P, D], BF16, name="junk")
@@ -152,8 +152,7 @@ def tile_blockselfattention_kernel(tc, features, out):
             return slice(S8 * b0, S8 * b1)
 
         def squares_of(k):
-            b0, b1 = BATCHES[k]
-            return sqc[:, k, 0 : S8 * (b1 - b0)]
+            return sqc[:, norm_cols(k)]
 
         def norm_scaled(k):
             cs = norm_cols(k)
@@ -162,21 +161,26 @@ def tile_blockselfattention_kernel(tc, features, out):
             )
             nc.scalar.activation(out=hcol[:, cs], in_=squares_of(k), func=ACT.Copy, scale=-0.5)
 
+        def piece_copy(k):
+            return nc.vector.tensor_copy if k < 2 else nc.scalar.copy
+
         def norm_piece(k, piece):
             b0, b1 = BATCHES[k]
             n = S8 * (b1 - b0)
             j0 = S8 * (b0 % 4)
-            pcv = pcs[:, k, 0:96].rearrange("p (j k) -> p j k", k=3)[:, j0 : j0 + n]
+            pcv = pcs[:, 0:96].rearrange("p (j k) -> p j k", k=3)[:, j0 : j0 + n]
             if piece == 0:
-                nc.vector.tensor_copy(out=pcv[:, :, 0], in_=squares_of(k))
+                piece_copy(k)(out=pcv[:, :, 0], in_=squares_of(k))
             elif piece == 1:
+                nc.vector.tensor_tensor(
+                    out=pcv[:, :, 1], in0=squares_of(k), in1=pcv[:, :, 0], op=ALU.subtract
+                )
+            elif piece == 2:
                 r1 = work.tile([P, 32], F32, name="r1")
                 nc.vector.tensor_tensor(
                     out=r1[:, 0:n], in0=squares_of(k), in1=pcv[:, :, 0], op=ALU.subtract
                 )
                 misc[("r1", k)] = r1
-            elif piece == 2:
-                nc.vector.tensor_copy(out=pcv[:, :, 1], in_=misc[("r1", k)][:, 0:n])
             else:
                 nc.vector.tensor_tensor(
                     out=pcv[:, :, 2], in0=misc.pop(("r1", k))[:, 0:n], in1=pcv[:, :, 1], op=ALU.subtract
@@ -184,7 +188,7 @@ def tile_blockselfattention_kernel(tc, features, out):
 
         def pieces_transpose(k):
             hp = ps_x.tile([P, P], BF16, name="hp", tag="x")
-            nc.tensor.transpose(hp[:], pcs[:, k, :], ident_b[:])
+            nc.tensor.transpose(hp[:], pcs[:], ident_b[:])
             misc[("hp", k)] = hp
 
         def pieces_out(k):
@@ -194,7 +198,7 @@ def tile_blockselfattention_kernel(tc, features, out):
 
         def norms_transpose(k):
             sp = ps_x.tile([P, P], F32, name="sp", tag="x")
-            nc.tensor.transpose(sp[:], sqc[:, k, :], ident_f[:])
+            nc.tensor.transpose(sp[:], sqc[:], ident_f[:])
             misc[("sp", k)] = sp
 
         def norms_broadcast(k):
@@ -205,7 +209,7 @@ def tile_blockselfattention_kernel(tc, features, out):
             )
             base = 1024 * (b1 - 1)
             nc.sync.dma_start(
-                out=out[base : base + S8 * (b1 - b0), :], in_=rows[0 : S8 * (b1 - b0), :]
+                out=out[base : base + S8 * (b1 - b0), :], in_=rows[S8 * b0 : S8 * b1, :]
             )
             for b in range(b0, b1):
                 first = base + S8 * (b - b0) + 2
@@ -336,7 +340,7 @@ def tile_blockselfattention_kernel(tc, features, out):
 
         def turn_out(b, k):
             a, s0, ns = V_BANKS[k][0]
-            copy = nc.vector.tensor_copy if k == 0 else nc.scalar.copy
+            copy = nc.vector.tensor_copy if k == 0 and b < 13 else nc.scalar.copy
             copy(
                 out=pl_of[b][:, a + 1, P * s0 : P * (s0 + 2)].rearrange("p (w e) -> p w e", e=2)[:, :, 0],
                 in_=misc.pop(("turn", b, k))[:],
@@ -382,17 +386,55 @@ def tile_blockselfattention_kernel(tc, features, out):
                 scalar1=1.0,
             )
 
-        def quantise(b, h):
+        def plain_regroup(b, g, q, e):
+            h = q // 2
+            s0 = SLOTS[h].index((g, q, e))
+            o = flat(b, h)[:, 512 * s0 : 512 * s0 + 512].rearrange("p (k t) -> p k t", t=4)
+            i = pl_of[b][:, 4 * g : 4 * g + 4, 256 * q : 256 * q + 256].rearrange(
+                "p t (k x) -> p x k t", x=2
+            )[:, e]
+            if b == NB - 1:
+                nc.scalar.copy(out=o, in_=i)
+            else:
+                nc.gpsimd.tensor_scalar(
+                    out=o, in0=i, scalar1=1.0, scalar2=0.0, op0=ALU.mult, op1=ALU.add
+                )
+
+        def hold_gpsimd(b):
+            nc.gpsimd.tensor_copy(out=token[:], in_=w_of[b][0][:, 0, 1020:1024])
+
+        def mirror_words_out(b, g, q):
+            bank = t_of.pop((b, g, q))
+            h = q // 2
+            s0 = SLOTS[h].index((g, q, 0))
+            nc.scalar.copy(
+                out=flat(b, h)[:, 512 * s0 : 512 * s0 + 1024]
+                .bitcast(F32)
+                .rearrange("p (k r u) -> p k r u", k=2, u=2),
+                in_=bank[:].rearrange("p u k r -> p k r u"),
+            )
+
+        def clamp(b, h, s0, ns):
+            cs = slice(512 * s0, 512 * (s0 + ns))
+            nc.vector.tensor_scalar_min(out=flat(b, h)[:, cs], in0=flat(b, h)[:, cs], scalar1=1.0)
+
+        def quantise(b, h, s0=0, ns=8):
             if b not in w_of:
                 wq = wp.tile([P, 2, 1024], U32, name="wq", align_bytes=64)
                 ws = wp.tile([P, 2, 1024], U8, name="ws", align_bytes=64)
                 w_of[b] = (wq, ws)
             wq, ws = w_of[b]
-            nc.vector.quantize_mx(out=wq[:, h].bitcast(FP8X4), scales=ws[:, h], in_=flat(b, h))
+            cs = slice(P * s0, P * (s0 + ns))
+            nc.vector.quantize_mx(
+                out=wq[:, h, cs].bitcast(FP8X4),
+                scales=ws[:, h, cs],
+                in_=flat(b, h)[:, 512 * s0 : 512 * (s0 + ns)],
+            )
 
         def regroup_x(b, g):
             xg = xgp.tile([P, D, 4], BF16, name="xg%d" % g, align_bytes=64)
-            nc.gpsimd.tensor_scalar(
+            engine = nc.vector if b == 0 else nc.gpsimd
+            engine.tensor_scalar(
                 out=xg[:],
                 in0=x_sb[:, S8 * b + 4 * g : S8 * b + 4 * g + 4, :].rearrange("p t d -> p d t"),
                 scalar1=1.0,
@@ -443,8 +485,6 @@ def tile_blockselfattention_kernel(tc, features, out):
             else:
                 square_on_vector(0, s)
         x_transpose(0)
-        regroup_x(0, 0)
-        regroup_x(0, 1)
         for piece in range(4):
             norm_piece(0, piece)
         x_transpose_out(0)
@@ -466,8 +506,7 @@ def tile_blockselfattention_kernel(tc, features, out):
         norms_transpose(1)
         fill_v(0, 1)
         for g in range(2):
-            quantise_x(0, g)
-            regroup_x(1, g)
+            regroup_x(0, g)
             norm_piece(1, 2 + g)
 
         squares_in = {0: [2, 3]}
@@ -504,6 +543,12 @@ def tile_blockselfattention_kernel(tc, features, out):
                     scale_out(b2, 1)
                 if i == 4 and nx is not None:
                     x_transpose_out(nx)
+                if b1 == NB - 1:
+                    if i == 0:
+                        plain_regroup(b1, 1, 3, 0)
+                        plain_regroup(b1, 1, 3, 1)
+                    if i == 2:
+                        mirror_words_out(b1, 1, 2)
                 if i == 6 and b is not None:
                     turn_out(b, 0)
                 if i == 9 and b is not None:
@@ -519,11 +564,13 @@ def tile_blockselfattention_kernel(tc, features, out):
                     if nk is not None and st > 0:
                         norm_piece(nk, 2)
                 if i == 2:
-                    if nx is not None:
-                        quantise_x(nx, 0)
-                        if nx + 1 < NB:
-                            regroup_x(nx + 1, 0)
-                    if b1 is not None:
+                    if b is not None:
+                        quantise_x(b, 0)
+                        if nx is not None:
+                            regroup_x(nx, 0)
+                    if b1 == NB - 1:
+                        clamp(b1, 1, 0, 4)
+                    elif b1 is not None:
                         mirror_out(b1, 1, 2)
                     if b is not None:
                         distances(b, 1)
@@ -536,14 +583,17 @@ def tile_blockselfattention_kernel(tc, features, out):
                     norms_broadcast(nl)
                     norm_scaled(nl)
                 if i == 3:
-                    if b1 is not None:
+                    if b1 is not None and b is not None:
                         regroup(b1, 1, 3, 1, 0)
                         regroup(b1, 1, 3, 1, 1)
                     if b is not None:
                         mirror_out(b, 0, 0)
                 if i == 5 and nk is not None:
                     pieces_out(nk)
-                if i == 5 and b1 is not None:
+                if i == 5 and b1 == NB - 1:
+                    quantise(b1, 1, 4, 4)
+                    quantise(b1, 1, 0, 4)
+                elif i == 5 and b1 is not None:
                     quantise(b1, 1)
                 if i == 6 and b is not None:
                     mirror_out(b, 1, 0)
@@ -551,10 +601,10 @@ def tile_blockselfattention_kernel(tc, features, out):
                     regroup(b, 0, 1, 1, 0)
                     regroup(b, 0, 1, 1, 1)
                 if i == 8:
-                    if nx is not None:
-                        quantise_x(nx, 1)
-                        if nx + 1 < NB:
-                            regroup_x(nx + 1, 1)
+                    if b is not None:
+                        quantise_x(b, 1)
+                        if nx is not None:
+                            regroup_x(nx, 1)
                     if b is not None:
                         mirror_out(b, 1, 1)
                     if nx is not None:

@@ -69,7 +69,6 @@ def tile_blockselfattention_kernel(tc, features, out):
         make_identity(nc, ident_b[:])
         ident_f = const.tile([P, P], F32, name="ident_f")
         make_identity(nc, ident_f[:])
-        hcol = const.tile([P, P], F32, name="hcol")
         bias = const.tile([P, P], F32, name="bias")
         pcs = const.tile([P, P], BF16, name="pcs")
         token = const.tile([P, 4], U32, name="token")
@@ -159,7 +158,6 @@ def tile_blockselfattention_kernel(tc, features, out):
             nc.scalar.activation(
                 out=bias[:, cs], in_=squares_of(k), func=ACT.Copy, scale=-0.5 * SCALE
             )
-            nc.scalar.activation(out=hcol[:, cs], in_=squares_of(k), func=ACT.Copy, scale=-0.5)
 
         def piece_copy(k):
             return nc.vector.tensor_copy if k < 2 else nc.scalar.copy
@@ -299,13 +297,11 @@ def tile_blockselfattention_kernel(tc, features, out):
             off = 0
             for a, s0, ns in V_BANKS[k]:
                 cs = slice(off, off + P * ns)
-                nc.vector.scalar_tensor_tensor(
+                nc.vector.tensor_tensor(
                     out=u[:, cs],
                     in0=bank[:, cs],
-                    scalar=hcol[:, S8 * b + a : S8 * b + a + 1],
                     in1=h_b[b][:, P * (s0 - 2) : P * (s0 - 2 + ns)],
-                    op0=ALU.add,
-                    op1=ALU.add,
+                    op=ALU.add,
                 )
                 off += P * ns
             u_of[(b, k)] = u
@@ -320,12 +316,14 @@ def tile_blockselfattention_kernel(tc, features, out):
                 in_=u[:, 256:384],
                 func=ACT.Exp,
                 scale=SCALE,
+                bias=bias[:, S8 * b + a + 1 : S8 * b + a + 2],
             )
             nc.scalar.activation(
                 out=pl[:, a, cs].rearrange("p (w e) -> p w e", e=2),
                 in_=u[:, 0:256].rearrange("p (e w) -> p w e", e=2),
                 func=ACT.Exp,
                 scale=SCALE,
+                bias=bias[:, S8 * b + a : S8 * b + a + 1],
             )
 
         def turn(b, k):
@@ -340,7 +338,7 @@ def tile_blockselfattention_kernel(tc, features, out):
 
         def turn_out(b, k):
             a, s0, ns = V_BANKS[k][0]
-            copy = nc.vector.tensor_copy if k == 0 and b < 13 else nc.scalar.copy
+            copy = nc.vector.tensor_copy if k == 0 else nc.scalar.copy
             copy(
                 out=pl_of[b][:, a + 1, P * s0 : P * (s0 + 2)].rearrange("p (w e) -> p w e", e=2)[:, :, 0],
                 in_=misc.pop(("turn", b, k))[:],
@@ -386,11 +384,11 @@ def tile_blockselfattention_kernel(tc, features, out):
                 scalar1=1.0,
             )
 
-        def plain_regroup(b, g, q, e):
+        def plain_regroup(b, g, q, e, ns=1):
             h = q // 2
             s0 = SLOTS[h].index((g, q, e))
-            o = flat(b, h)[:, 512 * s0 : 512 * s0 + 512].rearrange("p (k t) -> p k t", t=4)
-            i = pl_of[b][:, 4 * g : 4 * g + 4, 256 * q : 256 * q + 256].rearrange(
+            o = flat(b, h)[:, 512 * s0 : 512 * (s0 + ns)].rearrange("p (k t) -> p k t", t=4)
+            i = pl_of[b][:, 4 * g : 4 * g + 4, 256 * q : 256 * (q + ns)].rearrange(
                 "p t (k x) -> p x k t", x=2
             )[:, e]
             if b == NB - 1:
@@ -451,14 +449,14 @@ def tile_blockselfattention_kernel(tc, features, out):
                 in_=xg_of.pop((b, g))[:].rearrange("p d t -> p (d t)"),
             )
 
-        def second_matmul(b, h):
+        def second_matmul(b, h, j0=0, nj=4):
             wq, ws = w_of[b]
-            acc = ps_x.tile([P, 4, D], F32, name="acc", tag="x")
-            for j in range(4):
+            acc = ps_x.tile([P, nj, D], F32, name="acc%d" % nj, tag="x")
+            for j in range(j0, j0 + nj):
                 for g in range(2):
                     s = SLOTS[h].index((g, 2 * h + j // 2, j % 2))
                     nc.tensor.matmul_mx(
-                        out=acc[:, j, :],
+                        out=acc[:, j - j0, :],
                         lhsT=wq[:, h, P * s : P * s + P].bitcast(FP8X4),
                         lhsT_scale=ws[:, h, P * s : P * s + P],
                         rhs=xq[:, b, P * g : P * g + P].bitcast(FP8X4),
@@ -466,16 +464,16 @@ def tile_blockselfattention_kernel(tc, features, out):
                         start=(g == 0),
                         stop=(g == 1),
                     )
-            acc_of[(b, h)] = acc
+            acc_of[(b, h, j0)] = acc
 
-        def scale_out(b, h):
-            o = op.tile([P, 4, D], F32, name="osb%d" % h)
+        def scale_out(b, h, j0=0, nj=4):
+            o = op.tile([P, nj, D], F32, name="osb%d_%d" % (h, nj))
             nc.scalar.activation(
-                out=o[:], in_=acc_of.pop((b, h))[:], func=ACT.Copy, scale=1.0 / 1024.0
+                out=o[:], in_=acc_of.pop((b, h, j0))[:], func=ACT.Copy, scale=1.0 / 1024.0
             )
-            base = 1024 * b + 512 * h
+            base = 1024 * b + 512 * h + P * j0
             nc.sync.dma_start(
-                out=out[base : base + 512, :].rearrange("(q p e) d -> p q (e d)", p=P, e=2),
+                out=out[base : base + P * nj, :].rearrange("(q p e) d -> p q (e d)", p=P, e=2),
                 in_=o[:].rearrange("p (q e) d -> p q (e d)", e=2),
             )
 
@@ -488,12 +486,14 @@ def tile_blockselfattention_kernel(tc, features, out):
         for piece in range(4):
             norm_piece(0, piece)
         x_transpose_out(0)
+        for s in range(6):
+            square(1, s)
         norms_spread(0)
         pieces_transpose(0)
         pieces_out(0)
         norm_scaled(0)
         norms_spread_out(0)
-        for s in range(S8):
+        for s in range(6, S8):
             square_on_vector(1, s)
         for i in range(2):
             fill_n(i)
@@ -505,9 +505,10 @@ def tile_blockselfattention_kernel(tc, features, out):
         norm_piece(1, 1)
         norms_transpose(1)
         fill_v(0, 1)
-        for g in range(2):
-            regroup_x(0, g)
-            norm_piece(1, 2 + g)
+        norm_piece(1, 2)
+        regroup_x(0, 0)
+        regroup_x(0, 1)
+        norm_piece(1, 3)
 
         squares_in = {0: [2, 3]}
         for st in range(1, NB):
@@ -523,126 +524,231 @@ def tile_blockselfattention_kernel(tc, features, out):
             nx = st + 1 if st + 1 < NB else None
             nk = norms_in.get(st)
             nl = norms_in.get(st + 1)
+            last = b1 == NB - 1
             for i in range(10):
-                if b is not None:
-                    if i == 4:
-                        exp_v(b, 0)
-                    elif i == 7:
-                        exp_v(b, 1)
-                    else:
-                        exp_n(n_first[b] + n_slots.index(i))
-                    if i < 8:
+                if i == 0:
+                    if b is not None:
+                        exp_n(n_first[b] + 0)
+                    if b is not None and st > 0:
                         for sb in squares_in[st]:
-                            if st == 0 or i == 7:
-                                square_on_vector(sb, i)
-                            else:
-                                square(sb, i)
-                if i == 6 and b1 is not None:
-                    scale_out(b1, 0)
-                if i == 0 and b2 is not None:
-                    scale_out(b2, 1)
-                if i == 4 and nx is not None:
-                    x_transpose_out(nx)
-                if b1 == NB - 1:
-                    if i == 0:
+                            square(sb, 0)
+                    if last:
                         plain_regroup(b1, 1, 3, 0)
                         plain_regroup(b1, 1, 3, 1)
-                    if i == 2:
-                        mirror_words_out(b1, 1, 2)
-                if i == 6 and b is not None:
-                    turn_out(b, 0)
-                if i == 9 and b is not None:
-                    turn_out(b, 1)
+                        plain_regroup(b1, 0, 2, 1, 2)
+                if i == 0:
+                    if st == 0:
+                        square_on_vector(2, 0)
+                        square_on_vector(3, 0)
+                    if b1 is not None:
+                        if not last:
+                            regroup(b1, 0, 2, 2, 1)
                 if i == 0:
                     if b1 is not None:
-                        regroup(b1, 0, 2, 2, 1)
-                    if nk is not None and st > 0:
-                        norm_piece(nk, 1)
+                        mirror_transpose(b1, 1, 2)
+                    if b is not None:
+                        fill_n(n_first[b] + 3)
                 if i == 1:
+                    if b is not None:
+                        exp_n(n_first[b] + 1)
+                    if b is not None and st > 0:
+                        for sb in squares_in[st]:
+                            square(sb, 1)
+                    if st == 0:
+                        norms_broadcast(1)
+                        norm_scaled(1)
+                if i == 1:
+                    if st == 0:
+                        square_on_vector(2, 1)
+                        square_on_vector(3, 1)
+                    if nk is not None and st > 0:
+                        norm_piece(nk, 2)
                     if b1 is not None:
                         quantise(b1, 0)
                     if nk is not None and st > 0:
-                        norm_piece(nk, 2)
-                if i == 2:
+                        norm_piece(nk, 3)
                     if b is not None:
                         quantise_x(b, 0)
                         if nx is not None:
                             regroup_x(nx, 0)
-                    if b1 == NB - 1:
+                    if b is not None and b1 is not None and nx is not None:
+                        plain_regroup(b1, 1, 3, 0)
+                        plain_regroup(b1, 1, 3, 1)
+                if i == 1:
+                    if b2 is not None:
+                        if b2 == NB - 1:
+                            second_matmul(b2, 1, 0, 2)
+                            second_matmul(b2, 1, 2, 2)
+                        else:
+                            second_matmul(b2, 1)
+                        w_of.pop(b2)
+                        grp_of.pop(b2)
+                        pl_of.pop(b2)
+                    if b is not None:
+                        fill_n(n_first[b] + 4)
+                if i == 2:
+                    if b is not None:
+                        exp_n(n_first[b] + 2)
+                    if b is not None and st > 0:
+                        for sb in squares_in[st]:
+                            square(sb, 2)
+                    if last:
+                        mirror_words_out(b1, 1, 2)
+                if i == 2:
+                    if st == 0:
+                        square_on_vector(2, 2)
+                        square_on_vector(3, 2)
+                if i == 2:
+                    if b is not None and st > 0:
+                        fill_v(b, 1)
+                    if nx is not None:
+                        x_transpose(nx)
+                    if b is not None:
+                        mirror_transpose(b, 0, 0)
+                    if b is not None:
+                        fill_n(n_first[b] + 5)
+                if i == 3:
+                    if b is not None:
+                        exp_n(n_first[b] + 3)
+                    if b is not None and st > 0:
+                        for sb in squares_in[st]:
+                            square(sb, 3)
+                    if b2 is not None:
+                        if b2 == NB - 1:
+                            scale_out(b2, 1, 0, 2)
+                            scale_out(b2, 1, 2, 2)
+                        else:
+                            scale_out(b2, 1)
+                    if st == 0:
+                        square(2, 3)
+                if i == 3:
+                    if st == 0:
+                        square_on_vector(3, 3)
+                if i == 3:
+                    if nk is not None:
+                        pieces_transpose(nk)
+                    if b is not None:
+                        fill_n(n_first[b] + 6)
+                if i == 4:
+                    if b is not None:
+                        exp_v(b, 0)
+                    if b is not None and st > 0:
+                        for sb in squares_in[st]:
+                            square(sb, 4)
+                    if nx is not None:
+                        x_transpose_out(nx)
+                if i == 4:
+                    if st == 0:
+                        square_on_vector(2, 4)
+                        square_on_vector(3, 4)
+                if i == 4:
+                    if b is not None:
+                        turn(b, 0)
+                        mirror_transpose(b, 1, 0)
+                    if b1 is not None:
+                        second_matmul(b1, 0)
+                if i == 5:
+                    if b is not None:
+                        exp_n(n_first[b] + 4)
+                    if nk is not None:
+                        pieces_out(nk)
+                if i == 5:
+                    if st == 0:
+                        square_on_vector(2, 5)
+                        square_on_vector(3, 5)
+                    if last:
+                        clamp(b1, 1, 6, 2)
                         clamp(b1, 1, 0, 4)
-                    elif b1 is not None:
+                    if b is not None and b1 is not None:
                         mirror_out(b1, 1, 2)
                     if b is not None:
                         distances(b, 1)
-                    if nk is not None and st > 0:
-                        norm_piece(nk, 3)
-                if st == 0 and i == 1:
-                    norms_broadcast(1)
-                    norm_scaled(1)
-                if i == 9 and nl is not None:
-                    norms_broadcast(nl)
-                    norm_scaled(nl)
-                if i == 3:
-                    if b1 is not None and b is not None:
-                        regroup(b1, 1, 3, 1, 0)
-                        regroup(b1, 1, 3, 1, 1)
-                    if b is not None:
                         mirror_out(b, 0, 0)
-                if i == 5 and nk is not None:
-                    pieces_out(nk)
-                if i == 5 and b1 == NB - 1:
-                    quantise(b1, 1, 4, 4)
-                    quantise(b1, 1, 0, 4)
-                elif i == 5 and b1 is not None:
-                    quantise(b1, 1)
-                if i == 6 and b is not None:
-                    mirror_out(b, 1, 0)
-                if i == 7 and b is not None:
-                    regroup(b, 0, 1, 1, 0)
-                    regroup(b, 0, 1, 1, 1)
+                        turn_out(b, 0)
+                        mirror_out(b, 1, 0)
+                if i == 5:
+                    if b is not None:
+                        fill_v(b + 1, 0)
+                    if b is not None:
+                        fill_n(n_first[b] + 7)
+                if i == 6:
+                    if b is not None:
+                        exp_n(n_first[b] + 5)
+                    if b is not None and st > 0:
+                        for sb in squares_in[st]:
+                            square(sb, 6)
+                    if st == 0:
+                        square(2, 6)
+                        square(3, 6)
+                if i == 6:
+                    if b is not None and st > 0:
+                        for sb in squares_in[st]:
+                            square_on_vector(sb, 5)
+                            square_on_vector(sb, 7)
+                if i == 6:
+                    if b is not None:
+                        fill_n(n_first[b] + 8)
+                if i == 7:
+                    if b is not None:
+                        exp_v(b, 1)
+                    if b1 is not None:
+                        scale_out(b1, 0)
+                if i == 7:
+                    if st == 0:
+                        square_on_vector(2, 7)
+                        square_on_vector(3, 7)
+                    if b is not None:
+                        regroup(b, 0, 1, 1, 0)
+                    if b is not None and b1 is not None:
+                        if nx is not None:
+                            clamp(b1, 1, 2, 2)
+                        else:
+                            regroup(b1, 1, 3, 1, 0)
+                            regroup(b1, 1, 3, 1, 1)
+                    if b is not None:
+                        regroup(b, 0, 1, 1, 1)
+                    if last:
+                        quantise(b1, 1, 4, 4)
+                        quantise(b1, 1, 0, 2)
+                        quantise(b1, 1, 2, 2)
+                    if b is not None and b1 is not None:
+                        quantise(b1, 1)
+                if i == 7:
+                    if b is not None:
+                        mirror_transpose(b, 1, 1)
+                if i == 8:
+                    if b is not None:
+                        exp_n(n_first[b] + 6)
                 if i == 8:
                     if b is not None:
                         quantise_x(b, 1)
                         if nx is not None:
                             regroup_x(nx, 1)
-                    if b is not None:
                         mirror_out(b, 1, 1)
                     if nx is not None:
                         distances(nx, 0)
+                if i == 8:
+                    if b is not None:
+                        turn(b, 1)
+                    if nl is not None:
+                        norms_transpose(nl)
+                    if b is not None:
+                        fill_n(n_first[b] + 9)
+                if i == 9:
+                    if b is not None:
+                        exp_n(n_first[b] + 7)
+                    if b is not None:
+                        turn_out(b, 1)
+                    if nl is not None:
+                        norms_broadcast(nl)
+                        norm_scaled(nl)
                 if i == 9:
                     if nl is not None:
                         norm_piece(nl, 0)
                     if b is not None:
                         regroup(b, 0, 2, 2, 0)
-                if b is not None:
-                    if i == 9:
-                        fill_v(b + 1, 1)
-                    if i == 5:
-                        fill_v(b + 1, 0)
-                        turn(b, 0)
-                    if i == 8:
-                        turn(b, 1)
-                if i == 8 and nl is not None:
-                    norms_transpose(nl)
-                if i == 0 and b1 is not None:
-                    mirror_transpose(b1, 1, 2)
-                if i == 2:
-                    if nx is not None:
-                        x_transpose(nx)
+                    if nl is not None:
+                        norm_piece(nl, 1)
+                if i == 9:
                     if b is not None:
-                        mirror_transpose(b, 0, 0)
-                if i == 4 and nk is not None:
-                    pieces_transpose(nk)
-                if i == 4 and b1 is not None:
-                    second_matmul(b1, 0)
-                if i == 5 and b is not None:
-                    mirror_transpose(b, 1, 0)
-                if i == 7 and b is not None:
-                    mirror_transpose(b, 1, 1)
-                if i == 8 and b1 is not None:
-                    second_matmul(b1, 1)
-                    w_of.pop(b1)
-                    grp_of.pop(b1)
-                    pl_of.pop(b1)
-                if b is not None and i in n_slots:
-                    fill_n(n_first[b] + n_slots.index(i) + 3)
+                        fill_n(n_first[b] + 10)

@@ -429,24 +429,24 @@ def tile_blockselfattention_kernel(tc, features, out):
                 in_=flat(b, h)[:, 512 * s0 : 512 * (s0 + ns)],
             )
 
-        def regroup_x(b, g):
-            xg = xgp.tile([P, D, 4], BF16, name="xg%d" % g, align_bytes=64)
+        def regroup_x(b):
+            xg = xgp.tile([P, 2, D, 4], BF16, name="xg", align_bytes=64)
             engine = nc.vector if b == 0 else nc.gpsimd
             engine.tensor_scalar(
                 out=xg[:],
-                in0=x_sb[:, S8 * b + 4 * g : S8 * b + 4 * g + 4, :].rearrange("p t d -> p d t"),
+                in0=x_sb[:, S8 * b : S8 * b + S8, :].rearrange("p (g t) d -> p g d t", g=2),
                 scalar1=1.0,
                 scalar2=0.0,
                 op0=ALU.mult,
                 op1=ALU.add,
             )
-            xg_of[(b, g)] = xg
+            xg_of[b] = xg
 
-        def quantise_x(b, g):
+        def quantise_x(b):
             nc.vector.quantize_mx(
-                out=xq[:, b, P * g : P * g + P].bitcast(FP8X4),
-                scales=xs[:, b, P * g : P * g + P],
-                in_=xg_of.pop((b, g))[:].rearrange("p d t -> p (d t)"),
+                out=xq[:, b, :].bitcast(FP8X4),
+                scales=xs[:, b, :],
+                in_=xg_of.pop(b)[:].rearrange("p g d t -> p (g d t)"),
             )
 
         def second_matmul(b, h, j0=0, nj=4):
@@ -506,8 +506,7 @@ def tile_blockselfattention_kernel(tc, features, out):
         norms_transpose(1)
         fill_v(0, 1)
         norm_piece(1, 2)
-        regroup_x(0, 0)
-        regroup_x(0, 1)
+        regroup_x(0)
         norm_piece(1, 3)
 
         squares_in = {0: [2, 3]}
@@ -568,12 +567,9 @@ def tile_blockselfattention_kernel(tc, features, out):
                     if nk is not None and st > 0:
                         norm_piece(nk, 3)
                     if b is not None:
-                        quantise_x(b, 0)
+                        quantise_x(b)
                         if nx is not None:
-                            regroup_x(nx, 0)
-                    if b is not None and b1 is not None and nx is not None:
-                        plain_regroup(b1, 1, 3, 0)
-                        plain_regroup(b1, 1, 3, 1)
+                            regroup_x(nx)
                 if i == 1:
                     if b2 is not None:
                         if b2 == NB - 1:
@@ -594,9 +590,10 @@ def tile_blockselfattention_kernel(tc, features, out):
                             square(sb, 2)
                     if last:
                         mirror_words_out(b1, 1, 2)
+                    if st == 0:
+                        square(2, 2)
                 if i == 2:
                     if st == 0:
-                        square_on_vector(2, 2)
                         square_on_vector(3, 2)
                 if i == 2:
                     if b is not None and st > 0:
@@ -650,11 +647,15 @@ def tile_blockselfattention_kernel(tc, features, out):
                 if i == 5:
                     if b is not None:
                         exp_n(n_first[b] + 4)
+                    if b is not None and st > 0:
+                        for sb in squares_in[st]:
+                            square(sb, 5)
                     if nk is not None:
                         pieces_out(nk)
+                    if st == 0:
+                        square(2, 5)
                 if i == 5:
                     if st == 0:
-                        square_on_vector(2, 5)
                         square_on_vector(3, 5)
                     if last:
                         clamp(b1, 1, 6, 2)
@@ -677,13 +678,12 @@ def tile_blockselfattention_kernel(tc, features, out):
                     if b is not None and st > 0:
                         for sb in squares_in[st]:
                             square(sb, 6)
-                    if st == 0:
-                        square(2, 6)
-                        square(3, 6)
                 if i == 6:
+                    if st == 0:
+                        square_on_vector(2, 6)
+                        square_on_vector(3, 6)
                     if b is not None and st > 0:
                         for sb in squares_in[st]:
-                            square_on_vector(sb, 5)
                             square_on_vector(sb, 7)
                 if i == 6:
                     if b is not None:
@@ -700,11 +700,8 @@ def tile_blockselfattention_kernel(tc, features, out):
                     if b is not None:
                         regroup(b, 0, 1, 1, 0)
                     if b is not None and b1 is not None:
-                        if nx is not None:
-                            clamp(b1, 1, 2, 2)
-                        else:
-                            regroup(b1, 1, 3, 1, 0)
-                            regroup(b1, 1, 3, 1, 1)
+                        regroup(b1, 1, 3, 1, 0)
+                        regroup(b1, 1, 3, 1, 1)
                     if b is not None:
                         regroup(b, 0, 1, 1, 1)
                     if last:
@@ -721,9 +718,6 @@ def tile_blockselfattention_kernel(tc, features, out):
                         exp_n(n_first[b] + 6)
                 if i == 8:
                     if b is not None:
-                        quantise_x(b, 1)
-                        if nx is not None:
-                            regroup_x(nx, 1)
                         mirror_out(b, 1, 1)
                     if nx is not None:
                         distances(nx, 0)

@@ -209,13 +209,21 @@ def tile_blockselfattention_kernel(tc, features, out):
             nc.sync.dma_start(
                 out=out[base : base + S8 * (b1 - b0), :], in_=rows[S8 * b0 : S8 * b1, :]
             )
+            copy = base + S8 * (b1 - b0)
+            nc.sync.dma_start(
+                out=out[copy : copy + S8 * (b1 - b0), :], in_=rows[S8 * b0 : S8 * b1, :]
+            )
             for b in range(b0, b1):
-                first = base + S8 * (b - b0) + 2
-                hb = hbp.tile([P, 1024], F32, name="hb")
-                nc.sync.dma_start(
-                    out=hb[:, 0:768],
-                    in_=out[first : first + 6, :].rearrange("a p -> (a p)").partition_broadcast(P),
-                )
+                hb = hbp.tile([P, 2, 384], F32, name="hb")
+                for first, a0, a1 in ((base, 2, 4), (copy, 3, 4)):
+                    first += S8 * (b - b0)
+                    nc.sync.dma_start(
+                        out=hb[:, :, 0:256] if a0 == 2 else hb[:, :, 256:384],
+                        in_=out[first : first + S8, :]
+                        .rearrange("(y a) p -> y a p", a=4)[:, a0:a1]
+                        .rearrange("y a p -> y (a p)")
+                        .partition_broadcast(P),
+                    )
                 h_b[b] = hb
 
         def norms_spread(b):
@@ -227,9 +235,9 @@ def tile_blockselfattention_kernel(tc, features, out):
             misc[("hb", b)] = bank
 
         def norms_spread_out(b):
-            hb = hbp.tile([P, 1024], F32, name="hb")
+            hb = hbp.tile([P, 2, 384], F32, name="hb")
             nc.vector.tensor_scalar_mul(
-                out=hb[:].rearrange("p (y z) -> p y z", y=2)[:, :, 0:256],
+                out=hb[:, :, 0:256],
                 in0=misc.pop(("hb", b))[:].rearrange("p (y z) -> p y z", y=2),
                 scalar1=-0.5,
             )
@@ -242,6 +250,16 @@ def tile_blockselfattention_kernel(tc, features, out):
         def cols_of(b, s0, ns):
             return x_t[b][:, s0 : s0 + ns, :].rearrange("p s c -> p (s c)")
 
+        def add_norms(b, s0, ns, bank):
+            for k in range(ns):
+                nc.tensor.matmul(
+                    bank[:, P * k : P * k + P],
+                    lhsT=selc[:, S8 * (b % 4) + s0 + k, :],
+                    rhs=h_t[batch_of(b)][:],
+                    start=False,
+                    stop=(k == ns - 1),
+                )
+
         def fill_n(i):
             if i >= len(n_flat):
                 return
@@ -250,14 +268,7 @@ def tile_blockselfattention_kernel(tc, features, out):
             nc.tensor.matmul(
                 bank[:], lhsT=x_t[b][:, a, :], rhs=cols_of(b, s0, 4), start=True, stop=False
             )
-            for k in range(4):
-                nc.tensor.matmul(
-                    bank[:, P * k : P * k + P],
-                    lhsT=selc[:, S8 * (b % 4) + s0 + k, :],
-                    rhs=h_t[batch_of(b)][:],
-                    start=False,
-                    stop=(k == 3),
-                )
+            add_norms(b, s0, 4, bank)
             n_of[i] = bank
 
         def planes(b):
@@ -286,24 +297,27 @@ def tile_blockselfattention_kernel(tc, features, out):
                     lhsT=x_t[b][:, a, :],
                     rhs=cols_of(b, s0, ns),
                     start=True,
-                    stop=True,
+                    stop=b < NB - 1,
                 )
+                if b == NB - 1:
+                    add_norms(b, s0, ns, bank[:, off : off + P * ns])
                 off += P * ns
-            v_of[(b, k)] = bank
+            if b == NB - 1:
+                u_of[(b, k)] = bank
+            else:
+                v_of[(b, k)] = bank
 
         def distances(b, k):
+            if b == NB - 1:
+                return
             bank = v_of.pop((b, k))
             u = up.tile([P, 384], F32, name="u%d" % k)
-            off = 0
-            for a, s0, ns in V_BANKS[k]:
-                cs = slice(off, off + P * ns)
+            hb = h_b[b][:, k, :]
+            parts = [(0, 384, 0)] if b > 0 else [(0, 256, 0), (256, 384, 128)]
+            for c0, c1, h0 in parts:
                 nc.vector.tensor_tensor(
-                    out=u[:, cs],
-                    in0=bank[:, cs],
-                    in1=h_b[b][:, P * (s0 - 2) : P * (s0 - 2 + ns)],
-                    op=ALU.add,
+                    out=u[:, c0:c1], in0=bank[:, c0:c1], in1=hb[:, h0 : h0 + c1 - c0], op=ALU.add
                 )
-                off += P * ns
             u_of[(b, k)] = u
 
         def exp_v(b, k):
@@ -534,14 +548,12 @@ def tile_blockselfattention_kernel(tc, features, out):
                     if last:
                         plain_regroup(b1, 1, 3, 0)
                         plain_regroup(b1, 1, 3, 1)
-                        plain_regroup(b1, 0, 2, 1, 2)
                 if i == 0:
                     if st == 0:
                         square_on_vector(2, 0)
                         square_on_vector(3, 0)
                     if b1 is not None:
-                        if not last:
-                            regroup(b1, 0, 2, 2, 1)
+                        regroup(b1, 0, 2, 2, 1)
                 if i == 0:
                     if b1 is not None:
                         mirror_transpose(b1, 1, 2)
@@ -596,7 +608,7 @@ def tile_blockselfattention_kernel(tc, features, out):
                     if st == 0:
                         square_on_vector(3, 2)
                 if i == 2:
-                    if b is not None and st > 0:
+                    if b is not None and 0 < st < NB - 1:
                         fill_v(b, 1)
                     if nx is not None:
                         x_transpose(nx)
@@ -642,14 +654,13 @@ def tile_blockselfattention_kernel(tc, features, out):
                     if b is not None:
                         turn(b, 0)
                         mirror_transpose(b, 1, 0)
+                    if st == NB - 1:
+                        fill_v(b, 1)
                     if b1 is not None:
                         second_matmul(b1, 0)
                 if i == 5:
                     if b is not None:
                         exp_n(n_first[b] + 4)
-                    if b is not None and st > 0:
-                        for sb in squares_in[st]:
-                            square(sb, 5)
                     if nk is not None:
                         pieces_out(nk)
                     if st == 0:
@@ -658,7 +669,6 @@ def tile_blockselfattention_kernel(tc, features, out):
                     if st == 0:
                         square_on_vector(3, 5)
                     if last:
-                        clamp(b1, 1, 6, 2)
                         clamp(b1, 1, 0, 4)
                     if b is not None and b1 is not None:
                         mirror_out(b1, 1, 2)
@@ -684,6 +694,7 @@ def tile_blockselfattention_kernel(tc, features, out):
                         square_on_vector(3, 6)
                     if b is not None and st > 0:
                         for sb in squares_in[st]:
+                            square_on_vector(sb, 5)
                             square_on_vector(sb, 7)
                 if i == 6:
                     if b is not None:

@@ -22,10 +22,7 @@ FLOPS = 2 * 2 * 16 * 1024 * 1024 * 128
 N_BANKS = [(0, 0), (1, 0), (0, 4), (1, 4), (2, 4), (3, 4), (4, 4), (5, 4)]
 V_BANKS = [[(2, 2, 2), (3, 3, 1)], [(6, 6, 2), (7, 7, 1)]]
 BATCHES = [(0, 1), (1, 2)] + [(b, b + 2) for b in range(2, 16, 2)]
-SLOTS = [
-    [(1, 0, 0), (1, 0, 1), (1, 1, 0), (1, 1, 1), (0, 0, 0), (0, 0, 1), (0, 1, 0), (0, 1, 1)],
-    [(1, 2, 0), (1, 2, 1), (1, 3, 0), (1, 3, 1), (0, 2, 0), (0, 3, 0), (0, 2, 1), (0, 3, 1)],
-]
+PIECES = [[(1, 0), (1, 1), (0, 0), (0, 1)], [(1, 2), (1, 3), (0, 2), (0, 3)]]
 
 
 def tile_blockselfattention_kernel(tc, features, out):
@@ -162,18 +159,18 @@ def tile_blockselfattention_kernel(tc, features, out):
         def piece_copy(k):
             return nc.vector.tensor_copy if k < 2 else nc.scalar.copy
 
-        def norm_piece(k, piece):
+        def norm_piece(k, part):
             b0, b1 = BATCHES[k]
             n = S8 * (b1 - b0)
             j0 = S8 * (b0 % 4)
             pcv = pcs[:, 0:96].rearrange("p (j k) -> p j k", k=3)[:, j0 : j0 + n]
-            if piece == 0:
+            if part == 0:
                 piece_copy(k)(out=pcv[:, :, 0], in_=squares_of(k))
-            elif piece == 1:
+            elif part == 1:
                 nc.vector.tensor_tensor(
                     out=pcv[:, :, 1], in0=squares_of(k), in1=pcv[:, :, 0], op=ALU.subtract
                 )
-            elif piece == 2:
+            elif part == 2:
                 r1 = work.tile([P, 32], F32, name="r1")
                 nc.vector.tensor_tensor(
                     out=r1[:, 0:n], in0=squares_of(k), in1=pcv[:, :, 0], op=ALU.subtract
@@ -363,71 +360,52 @@ def tile_blockselfattention_kernel(tc, features, out):
                 grp_of[b] = gp.tile([P, 2, 8 * 512], BF16, name="grp", align_bytes=64)
             return grp_of[b][:, h]
 
-        def regroup(b, g, q, ns, e):
+        def piece(b, g, q, n=1):
             h = q // 2
-            s0 = SLOTS[h].index((g, q, e))
+            s0 = PIECES[h].index((g, q))
+            return flat(b, h)[:, 1024 * s0 : 1024 * (s0 + n)]
+
+        def plane_piece(b, g, q, n):
+            return pl_of[b][:, 4 * g : 4 * g + 4, 256 * q : 256 * (q + n)]
+
+        def regroup(b, g, q, n=1):
             nc.vector.tensor_scalar_min(
-                out=flat(b, h)[:, 512 * s0 : 512 * (s0 + ns)].rearrange(
-                    "p (k i t) -> p k t i", i=4, t=4
-                ),
-                in0=pl_of[b][:, 4 * g : 4 * g + 4, 256 * q : 256 * (q + ns)].rearrange(
-                    "p t (k i x) -> p x k t i", i=4, x=2
-                )[:, e],
+                out=piece(b, g, q, n).rearrange("p (k i t) -> p k t i", i=4, t=4),
+                in0=plane_piece(b, g, q, n).rearrange("p t (k i) -> p k t i", i=4),
                 scalar1=1.0,
             )
 
         def mirror_transpose(b, g, q):
-            bank = ps_x.tile([P, 2, 2, P], F32, name="tb", tag="x")
+            bank = ps_x.tile([P, 4, P], F32, name="tb", tag="x")
             for e in range(2):
                 for u in range(2):
                     c0 = 512 * g + 256 * u
                     nc.tensor.transpose(
-                        bank[:, u, e, :], pl_of[b][:, 2 * q + e, c0 : c0 + 256].bitcast(F32), ident_f[:]
+                        bank[:, 2 * e + u, :], pl_of[b][:, 2 * q + e, c0 : c0 + 256].bitcast(F32), ident_f[:]
                     )
             t_of[(b, g, q)] = bank
 
         def mirror_out(b, g, q):
-            bank = t_of.pop((b, g, q))[:].bitcast(BF16)
-            h = q // 2
-            s0 = SLOTS[h].index((g, q, 0))
             nc.vector.tensor_scalar_min(
-                out=flat(b, h)[:, 512 * s0 : 512 * s0 + 1024].rearrange(
-                    "p (r u x) -> p r u x", u=2, x=2
-                ),
-                in0=bank.rearrange("p u k (r x) -> p (k r) u x", x=2),
+                out=piece(b, g, q).rearrange("p (r j x) -> p r j x", j=4, x=2),
+                in0=t_of.pop((b, g, q))[:].bitcast(BF16).rearrange("p j (r x) -> p r j x", x=2),
                 scalar1=1.0,
             )
 
-        def plain_regroup(b, g, q, e, ns=1):
-            h = q // 2
-            s0 = SLOTS[h].index((g, q, e))
-            o = flat(b, h)[:, 512 * s0 : 512 * (s0 + ns)].rearrange("p (k t) -> p k t", t=4)
-            i = pl_of[b][:, 4 * g : 4 * g + 4, 256 * q : 256 * (q + ns)].rearrange(
-                "p t (k x) -> p x k t", x=2
-            )[:, e]
-            if b == NB - 1:
-                nc.scalar.copy(out=o, in_=i)
-            else:
-                nc.gpsimd.tensor_scalar(
-                    out=o, in0=i, scalar1=1.0, scalar2=0.0, op0=ALU.mult, op1=ALU.add
-                )
-
-        def hold_gpsimd(b):
-            nc.gpsimd.tensor_copy(out=token[:], in_=w_of[b][0][:, 0, 1020:1024])
-
-        def mirror_words_out(b, g, q):
-            bank = t_of.pop((b, g, q))
-            h = q // 2
-            s0 = SLOTS[h].index((g, q, 0))
+        def plain_regroup(b, g, q, n=1):
             nc.scalar.copy(
-                out=flat(b, h)[:, 512 * s0 : 512 * s0 + 1024]
-                .bitcast(F32)
-                .rearrange("p (k r u) -> p k r u", k=2, u=2),
-                in_=bank[:].rearrange("p u k r -> p k r u"),
+                out=piece(b, g, q, n).rearrange("p (k t) -> p k t", t=4),
+                in_=plane_piece(b, g, q, n).rearrange("p t k -> p k t"),
             )
 
-        def clamp(b, h, s0, ns):
-            cs = slice(512 * s0, 512 * (s0 + ns))
+        def mirror_words_out(b, g, q):
+            nc.scalar.copy(
+                out=piece(b, g, q).bitcast(F32).rearrange("p (r j) -> p r j", j=4),
+                in_=t_of.pop((b, g, q))[:].rearrange("p j r -> p r j"),
+            )
+
+        def clamp(b, h, s0, n):
+            cs = slice(1024 * s0, 1024 * (s0 + n))
             nc.vector.tensor_scalar_min(out=flat(b, h)[:, cs], in0=flat(b, h)[:, cs], scalar1=1.0)
 
         def quantise(b, h, s0=0, ns=8):
@@ -468,7 +446,7 @@ def tile_blockselfattention_kernel(tc, features, out):
             acc = ps_x.tile([P, nj, D], F32, name="acc%d" % nj, tag="x")
             for j in range(j0, j0 + nj):
                 for g in range(2):
-                    s = SLOTS[h].index((g, 2 * h + j // 2, j % 2))
+                    s = 2 * PIECES[h].index((g, 2 * h + j // 2)) + j % 2
                     nc.tensor.matmul_mx(
                         out=acc[:, j - j0, :],
                         lhsT=wq[:, h, P * s : P * s + P].bitcast(FP8X4),
@@ -487,8 +465,7 @@ def tile_blockselfattention_kernel(tc, features, out):
             )
             base = 1024 * b + 512 * h + P * j0
             nc.sync.dma_start(
-                out=out[base : base + P * nj, :].rearrange("(q p e) d -> p q (e d)", p=P, e=2),
-                in_=o[:].rearrange("p (q e) d -> p q (e d)", e=2),
+                out=out[base : base + P * nj, :].rearrange("(j p) d -> p j d", p=P), in_=o[:]
             )
 
         for s in range(S8):
@@ -497,8 +474,8 @@ def tile_blockselfattention_kernel(tc, features, out):
             else:
                 square_on_vector(0, s)
         x_transpose(0)
-        for piece in range(4):
-            norm_piece(0, piece)
+        for part in range(4):
+            norm_piece(0, part)
         x_transpose_out(0)
         for s in range(6):
             square(1, s)
@@ -546,14 +523,13 @@ def tile_blockselfattention_kernel(tc, features, out):
                         for sb in squares_in[st]:
                             square(sb, 0)
                     if last:
-                        plain_regroup(b1, 1, 3, 0)
-                        plain_regroup(b1, 1, 3, 1)
+                        plain_regroup(b1, 1, 3)
                 if i == 0:
                     if st == 0:
                         square_on_vector(2, 0)
                         square_on_vector(3, 0)
                     if b1 is not None:
-                        regroup(b1, 0, 2, 2, 1)
+                        regroup(b1, 0, 2, 2)
                 if i == 0:
                     if b1 is not None:
                         mirror_transpose(b1, 1, 2)
@@ -669,7 +645,7 @@ def tile_blockselfattention_kernel(tc, features, out):
                     if st == 0:
                         square_on_vector(3, 5)
                     if last:
-                        clamp(b1, 1, 0, 4)
+                        clamp(b1, 1, 0, 2)
                     if b is not None and b1 is not None:
                         mirror_out(b1, 1, 2)
                     if b is not None:
@@ -705,16 +681,13 @@ def tile_blockselfattention_kernel(tc, features, out):
                     if b1 is not None:
                         scale_out(b1, 0)
                 if i == 7:
+                    if b is not None and b1 is not None:
+                        regroup(b1, 1, 3)
                     if st == 0:
                         square_on_vector(2, 7)
                         square_on_vector(3, 7)
                     if b is not None:
-                        regroup(b, 0, 1, 1, 0)
-                    if b is not None and b1 is not None:
-                        regroup(b1, 1, 3, 1, 0)
-                        regroup(b1, 1, 3, 1, 1)
-                    if b is not None:
-                        regroup(b, 0, 1, 1, 1)
+                        regroup(b, 0, 1)
                     if last:
                         quantise(b1, 1, 4, 4)
                         quantise(b1, 1, 0, 2)
@@ -750,8 +723,6 @@ def tile_blockselfattention_kernel(tc, features, out):
                 if i == 9:
                     if nl is not None:
                         norm_piece(nl, 0)
-                    if b is not None:
-                        regroup(b, 0, 2, 2, 0)
                     if nl is not None:
                         norm_piece(nl, 1)
                 if i == 9:

@@ -199,9 +199,12 @@ def tile_blockselfattention_kernel(tc, features, out):
         def norms_broadcast(k):
             b0, b1 = BATCHES[k]
             rows = work.tile([P, P], F32, name="rows")
-            nc.scalar.activation(
-                out=rows[:], in_=misc.pop(("sp", k))[:], func=ACT.Copy, scale=-0.5
-            )
+            if k < 2:
+                nc.scalar.activation(
+                    out=rows[:], in_=misc.pop(("sp", k))[:], func=ACT.Copy, scale=-0.5
+                )
+            else:
+                nc.vector.tensor_scalar_mul(out=rows[:], in0=misc.pop(("sp", k))[:], scalar1=-0.5)
             base = 1024 * (b1 - 1)
             nc.sync.dma_start(
                 out=out[base : base + S8 * (b1 - b0), :], in_=rows[S8 * b0 : S8 * b1, :]
@@ -578,10 +581,9 @@ def tile_blockselfattention_kernel(tc, features, out):
                             square(sb, 2)
                     if last:
                         mirror_words_out(b1, 1, 2)
-                    if st == 0:
-                        square(2, 2)
                 if i == 2:
                     if st == 0:
+                        square_on_vector(2, 2)
                         square_on_vector(3, 2)
                 if i == 2:
                     if b is not None and 0 < st < NB - 1:
@@ -604,10 +606,9 @@ def tile_blockselfattention_kernel(tc, features, out):
                             scale_out(b2, 1, 2, 2)
                         else:
                             scale_out(b2, 1)
-                    if st == 0:
-                        square(2, 3)
                 if i == 3:
                     if st == 0:
+                        square_on_vector(2, 3)
                         square_on_vector(3, 3)
                 if i == 3:
                     if nk is not None:
@@ -637,13 +638,15 @@ def tile_blockselfattention_kernel(tc, features, out):
                 if i == 5:
                     if b is not None:
                         exp_n(n_first[b] + 4)
+                    if b is not None and st > 0:
+                        for sb in squares_in[st]:
+                            square(sb, 5)
                     if nk is not None:
                         pieces_out(nk)
                     if st == 0:
                         square(2, 5)
+                        square(3, 5)
                 if i == 5:
-                    if st == 0:
-                        square_on_vector(3, 5)
                     if last:
                         clamp(b1, 1, 0, 2)
                     if b is not None and b1 is not None:
@@ -664,13 +667,12 @@ def tile_blockselfattention_kernel(tc, features, out):
                     if b is not None and st > 0:
                         for sb in squares_in[st]:
                             square(sb, 6)
-                if i == 6:
                     if st == 0:
-                        square_on_vector(2, 6)
-                        square_on_vector(3, 6)
+                        square(2, 6)
+                        square(3, 6)
+                if i == 6:
                     if b is not None and st > 0:
                         for sb in squares_in[st]:
-                            square_on_vector(sb, 5)
                             square_on_vector(sb, 7)
                 if i == 6:
                     if b is not None:
@@ -680,12 +682,12 @@ def tile_blockselfattention_kernel(tc, features, out):
                         exp_v(b, 1)
                     if b1 is not None:
                         scale_out(b1, 0)
+                    if st == 0:
+                        square(2, 7)
+                        square(3, 7)
                 if i == 7:
                     if b is not None and b1 is not None:
                         regroup(b1, 1, 3)
-                    if st == 0:
-                        square_on_vector(2, 7)
-                        square_on_vector(3, 7)
                     if b is not None:
                         regroup(b, 0, 1)
                     if last:
@@ -718,9 +720,10 @@ def tile_blockselfattention_kernel(tc, features, out):
                     if b is not None:
                         turn_out(b, 1)
                     if nl is not None:
-                        norms_broadcast(nl)
                         norm_scaled(nl)
                 if i == 9:
+                    if nl is not None:
+                        norms_broadcast(nl)
                     if nl is not None:
                         norm_piece(nl, 0)
                     if nl is not None:

from contextlib import ExitStack

import concourse.mybir as mybir
from concourse.masks import make_identity

F32 = mybir.dt.float32
BF16 = mybir.dt.bfloat16
U32 = mybir.dt.uint32
U8 = mybir.dt.uint8
FP8X4 = mybir.dt.float8_e4m3fn_x4
ALU = mybir.AluOpType
ACT = mybir.ActivationFunctionType
AX = mybir.AxisListType

P = 128
NB = 16
D = 128
S8 = 8
SCALE = 2.0 / 25.6
FLOPS = 2 * 2 * 16 * 1024 * 1024 * 128

N_BANKS = [(0, 0), (1, 0), (0, 4), (1, 4), (2, 4), (3, 4), (4, 4), (5, 4)]
V_BANKS = [[(2, 2, 2), (3, 3, 1)], [(6, 6, 2), (7, 7, 1)]]
BATCHES = [(0, 1), (1, 2)] + [(b, b + 2) for b in range(2, 16, 2)]
PIECES = [[(1, 0), (1, 1), (0, 0), (0, 1)], [(1, 2), (1, 3), (0, 2), (0, 3)]]


def tile_blockselfattention_kernel(tc, features, out):
    nc = tc.nc
    with ExitStack() as ctx:
        ctx.enter_context(tc.manual_schedule())
        const = ctx.enter_context(tc.tile_pool(name="const", bufs=1))
        work = ctx.enter_context(tc.tile_pool(name="work", bufs=2))
        xgp = ctx.enter_context(tc.tile_pool(name="xgp", bufs=1))
        xtp = ctx.enter_context(tc.tile_pool(name="xtp", bufs=3))
        hbp = ctx.enter_context(tc.tile_pool(name="hbp", bufs=6))
        up = ctx.enter_context(tc.tile_pool(name="up", bufs=2))
        plp = ctx.enter_context(tc.tile_pool(name="plp", bufs=2))
        gp = ctx.enter_context(tc.tile_pool(name="gp", bufs=2))
        wp = ctx.enter_context(tc.tile_pool(name="wp", bufs=2))
        op = ctx.enter_context(tc.tile_pool(name="op", bufs=2))
        ps_n = ctx.enter_context(tc.psum_pool(name="ps_n", bufs=3))
        ps_v = ctx.enter_context(tc.psum_pool(name="ps_v", bufs=1))
        ps_x = ctx.enter_context(tc.psum_pool(name="ps_x", bufs=4))

        x_sb = const.tile([P, NB * S8, D], BF16, name="x_sb")
        xv = features.rearrange("(q p e) d -> p q (e d)", p=P, e=2)

        def load(queue, q0, q1):
            queue.dma_start(
                out=x_sb[:, 2 * q0 : 2 * q1, :].rearrange("p (q e) d -> p q (e d)", e=2),
                in_=xv[:, q0:q1, :],
            )

        load(nc.sync, 0, 2)
        load(nc.sync, 2, 4)
        load(nc.scalar, 4, 16)
        load(nc.sync, 16, 40)
        load(nc.sync, 40, 64)

        warm = const.tile([P, 1], F32, name="warm")
        nc.vector.memset(warm[:], 0.0)
        nc.scalar.activation(out=warm[:], in_=warm[:], func=ACT.Exp)
        sqc = const.tile([P, P], F32, name="sqc")
        ident_b = const.tile([P, P], BF16, name="ident_b")
        make_identity(nc, ident_b[:])
        ident_f = const.tile([P, P], F32, name="ident_f")
        make_identity(nc, ident_f[:])
        bias = const.tile([P, P], F32, name="bias")
        pcs = const.tile([P, P], BF16, name="pcs")
        token = const.tile([P, 4], U32, name="token")
        sel = const.tile([P, 32], F32, name="sel")
        nc.vector.tensor_reduce(
            out=sel[:],
            in_=ident_b[:, 0:96].rearrange("p (j k) -> p j k", k=3),
            axis=AX.X,
            op=ALU.add,
        )
        selc = const.tile([P, 32, P], BF16, name="selc")
        nc.vector.memset(sqc[:], 0.0)
        nc.vector.memset(pcs[:], 0.0)
        for j in (0, 16, 24):
            nc.vector.tensor_scalar_mul(
                out=selc[:, j : j + 8, :],
                in0=sel[:, j : j + 8].unsqueeze(2).to_broadcast([P, 8, P]),
                scalar1=-0.5,
            )
        nc.scalar.activation(
            out=selc[:, 8:16, :],
            in_=sel[:, 8:16].unsqueeze(2).to_broadcast([P, 8, P]),
            func=ACT.Copy,
            scale=-0.5,
        )
        xq = const.tile([P, NB, 256], U32, name="xq", align_bytes=64)
        xs = const.tile([P, NB, 256], U8, name="xs", align_bytes=64)

        x_t = {}
        h_b = {}
        h_t = {}
        pl_of = {}
        u_of = {}
        n_of = {}
        v_of = {}
        t_of = {}
        grp_of = {}
        w_of = {}
        xg_of = {}
        acc_of = {}
        o_of = {}
        misc = {}

        def batch_of(b):
            return [k for k in range(len(BATCHES)) if BATCHES[k][0] <= b < BATCHES[k][1]][0]

        def norm_col(b, s):
            return sqc[:, S8 * b + s : S8 * b + s + 1]

        def square(b, s):
            junk = work.tile([P, D], BF16, name="junk")
            nc.scalar.activation(
                out=junk[:],
                in_=x_sb[:, S8 * b + s, :],
                func=ACT.Square,
                accum_out=norm_col(b, s),
            )

        def square_on_vector(b, s):
            junk = work.tile([P, D], BF16, name="junk_v")
            x = x_sb[:, S8 * b + s, :]
            nc.vector.scalar_tensor_tensor(
                out=junk[:], in0=x, scalar=1.0, in1=x, op0=ALU.mult, op1=ALU.mult,
                accum_out=norm_col(b, s),
            )

        def x_transpose(b):
            xt_ps = ps_x.tile([P, S8, P], BF16, name="xt_ps", tag="x")
            for s in range(S8):
                nc.tensor.transpose(xt_ps[:, s, :], x_sb[:, S8 * b + s, :], ident_b[:])
            misc[("x", b)] = xt_ps

        def x_transpose_out(b):
            xt = xtp.tile([P, S8, P], BF16, name="xt")
            nc.scalar.copy(out=xt[:], in_=misc.pop(("x", b))[:])
            x_t[b] = xt

        def norm_cols(k):
            b0, b1 = BATCHES[k]
            return slice(S8 * b0, S8 * b1)

        def squares_of(k):
            return sqc[:, norm_cols(k)]

        def norm_scaled(k):
            cs = norm_cols(k)
            nc.scalar.activation(
                out=bias[:, cs], in_=squares_of(k), func=ACT.Copy, scale=-0.5 * SCALE
            )

        def piece_copy(k):
            return nc.vector.tensor_copy if k < 2 else nc.scalar.copy

        def norm_piece(k, part):
            b0, b1 = BATCHES[k]
            n = S8 * (b1 - b0)
            j0 = S8 * (b0 % 4)
            pcv = pcs[:, 0:96].rearrange("p (j k) -> p j k", k=3)[:, j0 : j0 + n]
            if part == 0:
                piece_copy(k)(out=pcv[:, :, 0], in_=squares_of(k))
            elif part == 1:
                nc.vector.tensor_tensor(
                    out=pcv[:, :, 1], in0=squares_of(k), in1=pcv[:, :, 0], op=ALU.subtract
                )
            elif part == 2:
                r1 = work.tile([P, 32], F32, name="r1")
                nc.vector.tensor_tensor(
                    out=r1[:, 0:n], in0=squares_of(k), in1=pcv[:, :, 0], op=ALU.subtract
                )
                misc[("r1", k)] = r1
            else:
                nc.vector.tensor_tensor(
                    out=pcv[:, :, 2], in0=misc.pop(("r1", k))[:, 0:n], in1=pcv[:, :, 1], op=ALU.subtract
                )

        def pieces_transpose(k):
            hp = ps_x.tile([P, P], BF16, name="hp", tag="x")
            nc.tensor.transpose(hp[:], pcs[:], ident_b[:])
            misc[("hp", k)] = hp

        def pieces_out(k):
            ht = const.tile([P, P], BF16, name="ht%d" % k)
            nc.scalar.copy(out=ht[:], in_=misc.pop(("hp", k))[:])
            h_t[k] = ht

        def norms_transpose(k):
            sp = ps_x.tile([P, P], F32, name="sp", tag="x")
            nc.tensor.transpose(sp[:], sqc[:], ident_f[:])
            misc[("sp", k)] = sp

        def norms_broadcast(k):
            b0, b1 = BATCHES[k]
            rows = work.tile([P, P], F32, name="rows")
            if k < 2:
                nc.scalar.activation(
                    out=rows[:], in_=misc.pop(("sp", k))[:], func=ACT.Copy, scale=-0.5
                )
            else:
                nc.vector.tensor_scalar_mul(out=rows[:], in0=misc.pop(("sp", k))[:], scalar1=-0.5)
            base = 1024 * (b1 - 1)
            nc.sync.dma_start(
                out=out[base : base + S8 * (b1 - b0), :], in_=rows[S8 * b0 : S8 * b1, :]
            )
            copy = base + S8 * (b1 - b0)
            nc.sync.dma_start(
                out=out[copy : copy + S8 * (b1 - b0), :], in_=rows[S8 * b0 : S8 * b1, :]
            )
            for b in range(b0, b1):
                hb = hbp.tile([P, 2, 384], F32, name="hb")
                for first, a0, a1 in ((base, 2, 4), (copy, 3, 4)):
                    first += S8 * (b - b0)
                    nc.sync.dma_start(
                        out=hb[:, :, 0:256] if a0 == 2 else hb[:, :, 256:384],
                        in_=out[first : first + S8, :]
                        .rearrange("(y a) p -> y a p", a=4)[:, a0:a1]
                        .rearrange("y a p -> y (a p)")
                        .partition_broadcast(P),
                    )
                h_b[b] = hb

        def norms_spread(b):
            bank = ps_v.tile([P, 512], F32, name="sv")
            for k, s in enumerate([2, 3, 6, 7]):
                nc.tensor.transpose(
                    bank[:, P * k : P * k + P], norm_col(b, s).to_broadcast([P, P]), ident_f[:]
                )
            misc[("hb", b)] = bank

        def norms_spread_out(b):
            hb = hbp.tile([P, 2, 384], F32, name="hb")
            nc.vector.tensor_scalar_mul(
                out=hb[:, :, 0:256],
                in0=misc.pop(("hb", b))[:].rearrange("p (y z) -> p y z", y=2),
                scalar1=-0.5,
            )
            h_b[b] = hb

        n_flat = [(b, a, s0) for b in range(NB) for a, s0 in N_BANKS]
        n_first = [n_flat.index((b, 0, 0)) for b in range(NB)]
        v_flat = [(b, k) for b in range(NB) for k in range(2)]

        def cols_of(b, s0, ns):
            return x_t[b][:, s0 : s0 + ns, :].rearrange("p s c -> p (s c)")

        def add_norms(b, s0, ns, bank):
            for k in range(ns):
                nc.tensor.matmul(
                    bank[:, P * k : P * k + P],
                    lhsT=selc[:, S8 * (b % 4) + s0 + k, :],
                    rhs=h_t[batch_of(b)][:],
                    start=False,
                    stop=(k == ns - 1),
                )

        def fill_n(i):
            if i >= len(n_flat):
                return
            b, a, s0 = n_flat[i]
            bank = ps_n.tile([P, 512], F32, name="sn")
            nc.tensor.matmul(
                bank[:], lhsT=x_t[b][:, a, :], rhs=cols_of(b, s0, 4), start=True, stop=False
            )
            add_norms(b, s0, 4, bank)
            n_of[i] = bank

        def planes(b):
            if b not in pl_of:
                pl_of[b] = plp.tile([P, S8, 1024], BF16, name="pl", align_bytes=64)
            return pl_of[b]

        def exp_n(i):
            b, a, s0 = n_flat[i]
            nc.scalar.activation(
                out=planes(b)[:, a, P * s0 : P * s0 + 512].rearrange("p (q w e) -> p q w e", w=P, e=2),
                in_=n_of.pop(i)[:].rearrange("p (q e w) -> p q w e", w=P, e=2),
                func=ACT.Exp,
                scale=SCALE,
                bias=bias[:, S8 * b + a : S8 * b + a + 1],
            )

        def fill_v(b, k):
            if (b, k) not in v_flat:
                return
            bank = ps_v.tile([P, 512], F32, name="sv")
            off = 0
            for a, s0, ns in V_BANKS[k]:
                nc.tensor.matmul(
                    bank[:, off : off + P * ns],
                    lhsT=x_t[b][:, a, :],
                    rhs=cols_of(b, s0, ns),
                    start=True,
                    stop=b < NB - 1,
                )
                if b == NB - 1:
                    add_norms(b, s0, ns, bank[:, off : off + P * ns])
                off += P * ns
            if b == NB - 1:
                u_of[(b, k)] = bank
            else:
                v_of[(b, k)] = bank

        def distances(b, k):
            if b == NB - 1:
                return
            bank = v_of.pop((b, k))
            u = up.tile([P, 384], F32, name="u%d" % k)
            hb = h_b[b][:, k, :]
            parts = [(0, 384, 0)] if b > 0 else [(0, 256, 0), (256, 384, 128)]
            for c0, c1, h0 in parts:
                nc.vector.tensor_tensor(
                    out=u[:, c0:c1], in0=bank[:, c0:c1], in1=hb[:, h0 : h0 + c1 - c0], op=ALU.add
                )
            u_of[(b, k)] = u

        def exp_v(b, k):
            u = u_of.pop((b, k))
            a, s0, ns = V_BANKS[k][0]
            pl = planes(b)
            cs = slice(P * s0, P * (s0 + 2))
            nc.scalar.activation(
                out=pl[:, a + 1, cs].rearrange("p (w e) -> p w e", e=2)[:, :, 1],
                in_=u[:, 256:384],
                func=ACT.Exp,
                scale=SCALE,
                bias=bias[:, S8 * b + a + 1 : S8 * b + a + 2],
            )
            nc.scalar.activation(
                out=pl[:, a, cs].rearrange("p (w e) -> p w e", e=2),
                in_=u[:, 0:256].rearrange("p (e w) -> p w e", e=2),
                func=ACT.Exp,
                scale=SCALE,
                bias=bias[:, S8 * b + a : S8 * b + a + 1],
            )

        def turn(b, k):
            a, s0, ns = V_BANKS[k][0]
            bank = ps_x.tile([P, P], BF16, name="turned", tag="x")
            nc.tensor.transpose(
                bank[:],
                pl_of[b][:, a, P * s0 : P * (s0 + 2)].rearrange("p (w e) -> p w e", e=2)[:, :, 1],
                ident_b[:],
            )
            misc[("turn", b, k)] = bank

        def turn_out(b, k):
            a, s0, ns = V_BANKS[k][0]
            copy = nc.vector.tensor_copy if k == 0 else nc.scalar.copy
            copy(
                out=pl_of[b][:, a + 1, P * s0 : P * (s0 + 2)].rearrange("p (w e) -> p w e", e=2)[:, :, 0],
                in_=misc.pop(("turn", b, k))[:],
            )

        def flat(b, h):
            if b not in grp_of:
                grp_of[b] = gp.tile([P, 2, 8 * 512], BF16, name="grp", align_bytes=64)
            return grp_of[b][:, h]

        def piece(b, g, q, n=1):
            h = q // 2
            s0 = PIECES[h].index((g, q))
            return flat(b, h)[:, 1024 * s0 : 1024 * (s0 + n)]

        def plane_piece(b, g, q, n):
            return pl_of[b][:, 4 * g : 4 * g + 4, 256 * q : 256 * (q + n)]

        def regroup(b, g, q, n=1):
            nc.vector.tensor_scalar_min(
                out=piece(b, g, q, n).rearrange("p (k i t) -> p k t i", i=4, t=4),
                in0=plane_piece(b, g, q, n).rearrange("p t (k i) -> p k t i", i=4),
                scalar1=1.0,
            )

        def mirror_transpose(b, g, q):
            bank = ps_x.tile([P, 4, P], F32, name="tb", tag="x")
            for e in range(2):
                for u in range(2):
                    c0 = 512 * g + 256 * u
                    nc.tensor.transpose(
                        bank[:, 2 * e + u, :], pl_of[b][:, 2 * q + e, c0 : c0 + 256].bitcast(F32), ident_f[:]
                    )
            t_of[(b, g, q)] = bank

        def mirror_out(b, g, q):
            nc.vector.tensor_scalar_min(
                out=piece(b, g, q).rearrange("p (r j x) -> p r j x", j=4, x=2),
                in0=t_of.pop((b, g, q))[:].bitcast(BF16).rearrange("p j (r x) -> p r j x", x=2),
                scalar1=1.0,
            )

        def plain_regroup(b, g, q, n=1):
            nc.scalar.copy(
                out=piece(b, g, q, n).rearrange("p (k t) -> p k t", t=4),
                in_=plane_piece(b, g, q, n).rearrange("p t k -> p k t"),
            )

        def mirror_words_out(b, g, q):
            nc.scalar.copy(
                out=piece(b, g, q).bitcast(F32).rearrange("p (r j) -> p r j", j=4),
                in_=t_of.pop((b, g, q))[:].rearrange("p j r -> p r j"),
            )

        def clamp(b, h, s0, n):
            cs = slice(1024 * s0, 1024 * (s0 + n))
            nc.vector.tensor_scalar_min(out=flat(b, h)[:, cs], in0=flat(b, h)[:, cs], scalar1=1.0)

        def quantise(b, h, s0=0, ns=8):
            if b not in w_of:
                wq = wp.tile([P, 2, 1024], U32, name="wq", align_bytes=64)
                ws = wp.tile([P, 2, 1024], U8, name="ws", align_bytes=64)
                w_of[b] = (wq, ws)
            wq, ws = w_of[b]
            cs = slice(P * s0, P * (s0 + ns))
            nc.vector.quantize_mx(
                out=wq[:, h, cs].bitcast(FP8X4),
                scales=ws[:, h, cs],
                in_=flat(b, h)[:, 512 * s0 : 512 * (s0 + ns)],
            )

        def regroup_x(b):
            xg = xgp.tile([P, 2, D, 4], BF16, name="xg", align_bytes=64)
            engine = nc.vector if b == 0 else nc.gpsimd
            engine.tensor_scalar(
                out=xg[:],
                in0=x_sb[:, S8 * b : S8 * b + S8, :].rearrange("p (g t) d -> p g d t", g=2),
                scalar1=1.0,
                scalar2=0.0,
                op0=ALU.mult,
                op1=ALU.add,
            )
            xg_of[b] = xg

        def quantise_x(b):
            nc.vector.quantize_mx(
                out=xq[:, b, :].bitcast(FP8X4),
                scales=xs[:, b, :],
                in_=xg_of.pop(b)[:].rearrange("p g d t -> p (g d t)"),
            )

        def second_matmul(b, h, j0=0, nj=4):
            wq, ws = w_of[b]
            acc = ps_x.tile([P, nj, D], F32, name="acc%d" % nj, tag="x")
            for j in range(j0, j0 + nj):
                for g in range(2):
                    s = 2 * PIECES[h].index((g, 2 * h + j // 2)) + j % 2
                    nc.tensor.matmul_mx(
                        out=acc[:, j - j0, :],
                        lhsT=wq[:, h, P * s : P * s + P].bitcast(FP8X4),
                        lhsT_scale=ws[:, h, P * s : P * s + P],
                        rhs=xq[:, b, P * g : P * g + P].bitcast(FP8X4),
                        rhs_scale=xs[:, b, P * g : P * g + P],
                        start=(g == 0),
                        stop=(g == 1),
                    )
            acc_of[(b, h, j0)] = acc

        def scale_out(b, h, j0=0, nj=4):
            o = op.tile([P, nj, D], F32, name="osb%d_%d" % (h, nj))
            nc.scalar.activation(
                out=o[:], in_=acc_of.pop((b, h, j0))[:], func=ACT.Copy, scale=1.0 / 1024.0
            )
            base = 1024 * b + 512 * h + P * j0
            nc.sync.dma_start(
                out=out[base : base + P * nj, :].rearrange("(j p) d -> p j d", p=P), in_=o[:]
            )

        for s in range(S8):
            if s < 5:
                square(0, s)
            else:
                square_on_vector(0, s)
        x_transpose(0)
        for part in range(4):
            norm_piece(0, part)
        x_transpose_out(0)
        for s in range(6):
            square(1, s)
        norms_spread(0)
        pieces_transpose(0)
        pieces_out(0)
        norm_scaled(0)
        norms_spread_out(0)
        for s in range(6, S8):
            square_on_vector(1, s)
        for i in range(2):
            fill_n(i)
        fill_v(0, 0)
        for i in range(2, 3):
            fill_n(i)
        norm_piece(1, 0)
        distances(0, 0)
        norm_piece(1, 1)
        norms_transpose(1)
        fill_v(0, 1)
        norm_piece(1, 2)
        regroup_x(0)
        norm_piece(1, 3)

        squares_in = {0: [2, 3]}
        for st in range(1, NB):
            squares_in[st] = [st + 3] if st + 3 < NB else []
        norms_in = {0: 1}
        for k in range(2, len(BATCHES)):
            norms_in[BATCHES[k][0] - 1] = k
        n_slots = [0, 1, 2, 3, 5, 6, 8, 9]
        for st in range(NB + 2):
            b = st if st < NB else None
            b1 = st - 1 if 0 <= st - 1 < NB else None
            b2 = st - 2 if 0 <= st - 2 < NB else None
            nx = st + 1 if st + 1 < NB else None
            nk = norms_in.get(st)
            nl = norms_in.get(st + 1)
            last = b1 == NB - 1
            for i in range(10):
                if i == 0:
                    if b is not None:
                        exp_n(n_first[b] + 0)
                    if b is not None and st > 0:
                        for sb in squares_in[st]:
                            square(sb, 0)
                    if last:
                        plain_regroup(b1, 1, 3)
                if i == 0:
                    if st == 0:
                        square_on_vector(2, 0)
                        square_on_vector(3, 0)
                    if b1 is not None:
                        regroup(b1, 0, 2, 2)
                if i == 0:
                    if b1 is not None:
                        mirror_transpose(b1, 1, 2)
                    if b is not None:
                        fill_n(n_first[b] + 3)
                if i == 1:
                    if b is not None:
                        exp_n(n_first[b] + 1)
                    if b is not None and st > 0:
                        for sb in squares_in[st]:
                            square(sb, 1)
                    if st == 0:
                        norms_broadcast(1)
                        norm_scaled(1)
                if i == 1:
                    if st == 0:
                        square_on_vector(2, 1)
                        square_on_vector(3, 1)
                    if nk is not None and st > 0:
                        norm_piece(nk, 2)
                    if b1 is not None:
                        quantise(b1, 0)
                    if nk is not None and st > 0:
                        norm_piece(nk, 3)
                    if b is not None:
                        quantise_x(b)
                        if nx is not None:
                            regroup_x(nx)
                if i == 1:
                    if b2 is not None:
                        if b2 == NB - 1:
                            second_matmul(b2, 1, 0, 2)
                            second_matmul(b2, 1, 2, 2)
                        else:
                            second_matmul(b2, 1)
                        w_of.pop(b2)
                        grp_of.pop(b2)
                        pl_of.pop(b2)
                    if b is not None:
                        fill_n(n_first[b] + 4)
                if i == 2:
                    if b is not None:
                        exp_n(n_first[b] + 2)
                    if b is not None and st > 0:
                        for sb in squares_in[st]:
                            square(sb, 2)
                    if last:
                        mirror_words_out(b1, 1, 2)
                if i == 2:
                    if st == 0:
                        square_on_vector(2, 2)
                        square_on_vector(3, 2)
                if i == 2:
                    if b is not None and 0 < st < NB - 1:
                        fill_v(b, 1)
                    if nx is not None:
                        x_transpose(nx)
                    if b is not None:
                        mirror_transpose(b, 0, 0)
                    if b is not None:
                        fill_n(n_first[b] + 5)
                if i == 3:
                    if b is not None:
                        exp_n(n_first[b] + 3)
                    if b is not None and st > 0:
                        for sb in squares_in[st]:
                            square(sb, 3)
                    if b2 is not None:
                        if b2 == NB - 1:
                            scale_out(b2, 1, 0, 2)
                            scale_out(b2, 1, 2, 2)
                        else:
                            scale_out(b2, 1)
                if i == 3:
                    if st == 0:
                        square_on_vector(2, 3)
                        square_on_vector(3, 3)
                if i == 3:
                    if nk is not None:
                        pieces_transpose(nk)
                    if b is not None:
                        fill_n(n_first[b] + 6)
                if i == 4:
                    if b is not None:
                        exp_v(b, 0)
                    if b is not None and st > 0:
                        for sb in squares_in[st]:
                            square(sb, 4)
                    if nx is not None:
                        x_transpose_out(nx)
                if i == 4:
                    if st == 0:
                        square_on_vector(2, 4)
                        square_on_vector(3, 4)
                if i == 4:
                    if b is not None:
                        turn(b, 0)
                        mirror_transpose(b, 1, 0)
                    if st == NB - 1:
                        fill_v(b, 1)
                    if b1 is not None:
                        second_matmul(b1, 0)
                if i == 5:
                    if b is not None:
                        exp_n(n_first[b] + 4)
                    if b is not None and st > 0:
                        for sb in squares_in[st]:
                            square(sb, 5)
                    if nk is not None:
                        pieces_out(nk)
                    if st == 0:
                        square(2, 5)
                        square(3, 5)
                if i == 5:
                    if last:
                        clamp(b1, 1, 0, 2)
                    if b is not None and b1 is not None:
                        mirror_out(b1, 1, 2)
                    if b is not None:
                        distances(b, 1)
                        mirror_out(b, 0, 0)
                        turn_out(b, 0)
                        mirror_out(b, 1, 0)
                if i == 5:
                    if b is not None:
                        fill_v(b + 1, 0)
                    if b is not None:
                        fill_n(n_first[b] + 7)
                if i == 6:
                    if b is not None:
                        exp_n(n_first[b] + 5)
                    if b is not None and st > 0:
                        for sb in squares_in[st]:
                            square(sb, 6)
                    if st == 0:
                        square(2, 6)
                        square(3, 6)
                if i == 6:
                    if b is not None and st > 0:
                        for sb in squares_in[st]:
                            square_on_vector(sb, 7)
                if i == 6:
                    if b is not None:
                        fill_n(n_first[b] + 8)
                if i == 7:
                    if b is not None:
                        exp_v(b, 1)
                    if b1 is not None:
                        scale_out(b1, 0)
                    if st == 0:
                        square(2, 7)
                        square(3, 7)
                if i == 7:
                    if b is not None and b1 is not None:
                        regroup(b1, 1, 3)
                    if b is not None:
                        regroup(b, 0, 1)
                    if last:
                        quantise(b1, 1, 4, 4)
                        quantise(b1, 1, 0, 2)
                        quantise(b1, 1, 2, 2)
                    if b is not None and b1 is not None:
                        quantise(b1, 1)
                if i == 7:
                    if b is not None:
                        mirror_transpose(b, 1, 1)
                if i == 8:
                    if b is not None:
                        exp_n(n_first[b] + 6)
                if i == 8:
                    if b is not None:
                        mirror_out(b, 1, 1)
                    if nx is not None:
                        distances(nx, 0)
                if i == 8:
                    if b is not None:
                        turn(b, 1)
                    if nl is not None:
                        norms_transpose(nl)
                    if b is not None:
                        fill_n(n_first[b] + 9)
                if i == 9:
                    if b is not None:
                        exp_n(n_first[b] + 7)
                    if b is not None:
                        turn_out(b, 1)
                    if nl is not None:
                        norm_scaled(nl)
                if i == 9:
                    if nl is not None:
                        norms_broadcast(nl)
                    if nl is not None:
                        norm_piece(nl, 0)
                    if nl is not None:
                        norm_piece(nl, 1)
                if i == 9:
                    if b is not None:
                        fill_n(n_first[b] + 10)
